import numpy as np
import ml_dtypes


def mxq(x, axis, fmt="e4m3"):
    dtype, down = {"e4m3": (ml_dtypes.float8_e4m3fn, 7), "e5m2": (ml_dtypes.float8_e5m2, 14)}[fmt]
    v = np.moveaxis(np.asarray(x, np.float32).astype(ml_dtypes.bfloat16).astype(np.float64), axis, -1)
    blocks = v.reshape(v.shape[:-1] + (-1, 32))
    amax = np.abs(blocks).max(-1, keepdims=True)
    byte = np.maximum(np.where(amax > 0, np.frexp(amax)[1] - 1 + 127, 0) - down, 1)
    scale = np.exp2(byte - 127.0)
    codes = (blocks / scale).astype(np.float32).astype(dtype).astype(np.float64)
    return np.moveaxis((codes * scale).reshape(v.shape), -1, axis)


WIDE = False


def mx_kscale(k):
    if not WIDE:
        return np.ones(k)
    levels = np.array([10, -10, 5, -5, 0])
    if k % 512:
        return np.exp2(np.random.permutation(np.resize(levels, k // 32))).repeat(32)
    a = np.empty((k // 512, 16))
    for p in range(k // 512):
        a[p, :8] = np.random.permutation(np.resize(levels, 8))
        for g in range(8):
            far = levels[np.abs(levels - a[p, g]) >= 10]
            a[p, g + 8] = far[np.random.randint(len(far))]
    return np.exp2(a.ravel()).repeat(32)


BF16 = ml_dtypes.bfloat16


def bf(x):
    return np.asarray(x, np.float32).astype(BF16)


def f64(x):
    return np.asarray(x).astype(np.float64)


B, IM, HID, L = 1024, 1024, 4096, 128


def relu(v):
    return np.maximum(v, 0.0)


def draw0():
    s, t = mx_kscale(IM), mx_kscale(HID)
    return {"x": bf(np.random.random((B, IM)) * s),
            "eps": bf(np.random.standard_normal((B, L))),
            "W11": bf(np.random.standard_normal((IM, HID)) * np.sqrt(3.0 / IM) / s[:, None] * t),
            "b11": bf(np.random.standard_normal(HID) * 0.2 * t),
            "W31": bf(np.random.standard_normal((HID, L)) * np.sqrt(2.0 / HID) / t[:, None]),
            "b31": bf(np.random.standard_normal(L) * 0.2),
            "W32": bf(np.random.standard_normal((HID, L)) * np.sqrt(2.0 / HID) / t[:, None]),
            "b32": bf(np.random.standard_normal(L) * 0.2)}


def core(x, eps, W11, b11, W31, b31, W32, b32):
    enc = relu((mxq(f64(x), 1, "e4m3") @ mxq(f64(W11), 0, "e4m3")) + f64(b11))
    encq = mxq(enc, 1, "e4m3")
    mu = relu((encq @ mxq(f64(W31), 0, "e4m3")) + f64(b31))
    sigma = relu((encq @ mxq(f64(W32), 0, "e4m3")) + f64(b32))
    z = f64(eps) * sigma + mu
    return mu, sigma, z


def e4m3fn_bytes(y):
    return np.clip(np.asarray(y, np.float64), -448.0, 448.0).astype(np.float32).astype(ml_dtypes.float8_e4m3fn).view(np.uint8)


def e4m3fn_values(b):
    return np.asarray(b, np.uint8).view(ml_dtypes.float8_e4m3fn).astype(np.float64)


def setup_inputs():
    d = draw0()
    x0 = np.asarray(d['x']).astype(np.float64)
    s = (np.max(np.abs(x0), axis=(0,), keepdims=True) / 448.0).astype(np.float32)
    out = {}
    for k, v in d.items():
        if k == 'x':
            out['x_bytes'] = e4m3fn_bytes(x0 / s.astype(np.float64))
            out['x_scale'] = s
        else:
            out[k] = v
    return out


def reference(x_bytes, x_scale, eps, W11, b11, W31, b31, W32, b32):
    return core(e4m3fn_values(x_bytes) * x_scale.astype(np.float64), eps, W11, b11, W31, b31, W32, b32)

@@ -1,0 +1,367 @@
+from contextlib import ExitStack
+
+import concourse.mybir as mybir
+from concourse.masks import make_identity
+
+TOKENS, IMAGE, HIDDEN, LATENT = 1024, 1024, 4096, 128
+
+F32 = mybir.dt.float32
+BF16 = mybir.dt.bfloat16
+U32 = mybir.dt.uint32
+U8 = mybir.dt.uint8
+FP8 = mybir.dt.float8_e4m3fn
+FP8X4 = mybir.dt.float8_e4m3fn_x4
+
+ADD = mybir.AluOpType.add
+MULT = mybir.AluOpType.mult
+MAX = mybir.AluOpType.max
+RELU = mybir.ActivationFunctionType.Relu
+
+P = 128
+FLOPS = 2 * TOKENS * IMAGE * HIDDEN + 2 * TOKENS * HIDDEN * 2 * LATENT
+
+GROUPS = 8
+HALF = 512
+ROWS = TOKENS // P
+
+UNITS = [(0, 0)] + [(h, g - h) for g in range(1, GROUPS) for h in range(2)] + [(1, GROUPS - 1)]
+
+
+def tile_mae_pa_kernel(tc, x_bytes, x_scale, eps, W11, b11, W31, b31, W32, b32, out_0, out_1, out_2):
+    nc = tc.nc
+    with ExitStack() as ctx:
+        keep = ctx.enter_context(tc.tile_pool(name="keep", bufs=1))
+        work = ctx.enter_context(tc.tile_pool(name="work", bufs=2))
+        psum = ctx.enter_context(tc.psum_pool(name="psum", bufs=4))
+        accs = ctx.enter_context(tc.psum_pool(name="accs", bufs=1))
+
+        ident = keep.tile([P, P], F32, name="ident")
+        make_identity(nc, ident[:])
+        ctx.enter_context(tc.manual_schedule())
+        ctx.enter_context(nc.allow_non_contiguous_dma(reason="runs of four biases"))
+
+        warm = keep.tile([P, 1], F32, name="warm")
+        nc.vector.memset(warm[:], 0.0)
+        warm_out = keep.tile([P, 1], F32, name="warm_out")
+
+        scale = keep.tile([P, IMAGE], F32, name="scale")
+        nc.scalar.dma_start(out=scale[:], in_=x_scale.rearrange("o k -> (o k)").partition_broadcast(P))
+        nc.scalar.activation(out=warm_out[:], in_=warm[:], func=RELU)
+
+        xq = [keep.tile([P, 4 * IMAGE], U8, name=f"xq{h}") for h in range(2)]
+        x_view = x_bytes.rearrange("(p r) k -> p (r k)", r=ROWS)
+
+        def load_x(h, a, b):
+            nc.sync.dma_start(
+                out=xq[h][:, a * IMAGE : b * IMAGE],
+                in_=x_view[:, (4 * h + a) * IMAGE : (4 * h + b) * IMAGE],
+            )
+
+        w_raw = [None] * 4
+        w_view = W11.rearrange("(c p j) n -> c p j n", c=2, j=4)
+
+        def load_w(pair, c, a, b):
+            if w_raw[pair] is None:
+                w_raw[pair] = work.tile([P, 2, 4, 1024], BF16, name="w_raw", bufs=3)
+            nc.sync.dma_start(
+                out=w_raw[pair][:, c, :, a:b], in_=w_view[c, :, :, 1024 * pair + a : 1024 * pair + b]
+            )
+
+        w3_raw = keep.tile([P, 2, GROUPS, 512], BF16, name="w3_raw")
+        w3_view = [w.rearrange("(g p j) l -> p g (j l)", p=P, j=4) for w in (W31, W32)]
+
+        def load_w3(a, b):
+            for i in range(2):
+                nc.sync.dma_start(out=w3_raw[:, i, a:b, :], in_=w3_view[i][:, a:b, :])
+
+        load_x(0, 0, 1)
+        load_w(0, 0, 0, 256)
+        load_x(0, 1, 2)
+        load_w(0, 0, 256, 512)
+        load_x(0, 2, 4)
+        load_w(0, 1, 0, 512)
+        bias_raw = keep.tile([P, GROUPS, 4], BF16, name="bias_raw")
+        nc.scalar.dma_start(out=bias_raw[:], in_=b11.rearrange("(g p t) -> p g t", p=P, t=4))
+        load_w(0, 0, 512, 1024)
+        load_w(0, 1, 512, 1024)
+        load_x(1, 0, 4)
+        load_w3(0, 2)
+        load_w(1, 0, 0, 1024)
+        load_w(1, 1, 0, 1024)
+        load_w3(2, 8)
+        bias3 = keep.tile([P, 2 * LATENT], BF16, name="bias3")
+        nc.sync.dma_start(out=bias3[:, :LATENT], in_=b31.partition_broadcast(P))
+        nc.sync.dma_start(out=bias3[:, LATENT:], in_=b32.partition_broadcast(P))
+        eps_sb = keep.tile([P, ROWS, LATENT], BF16, name="eps_sb")
+        nc.sync.dma_start(out=eps_sb[:], in_=eps.rearrange("(p r) l -> p r l", r=ROWS))
+        load_w(2, 0, 0, 1024)
+        load_w(2, 1, 0, 1024)
+
+        xg = [None, None]
+        x_codes = [keep.tile([P, 2, HALF], U32, name=f"x_codes{h}", align_bytes=64) for h in range(2)]
+        x_planes = [keep.tile([P, 2, HALF], U8, name=f"x_planes{h}", align_bytes=64) for h in range(2)]
+
+        xb = {}
+
+        def x_product(h, r):
+            xb[h, r] = work.tile([P, IMAGE], BF16, name="xb", bufs=3)
+            nc.vector.tensor_tensor(
+                out=xb[h, r][:], in0=xq[h][:, r * IMAGE : (r + 1) * IMAGE].bitcast(FP8), in1=scale[:], op=MULT
+            )
+
+        x_banks = {}
+
+        def x_turn(h, r):
+            bank = psum.tile([P, 4, P], F32, name="bank")
+            words = xb[h, r][:].bitcast(F32)
+            for c in range(2):
+                for u in range(2):
+                    nc.tensor.transpose(
+                        bank[:, 2 * c + u, :], words[:, 256 * c + u : 256 * (c + 1) : 2], ident[:]
+                    )
+            x_banks[h, r] = bank
+
+        def x_out(h, r):
+            if xg[h] is None:
+                xg[h] = work.tile([P, 2, HALF, 4], BF16, name="xg", bufs=1, align_bytes=64)
+            dst = xg[h][:].rearrange("p c n t -> p (c n t)").bitcast(F32)
+            dst = dst.rearrange("p (c n u) -> p c n u", c=2, u=2)
+            nc.scalar.copy(
+                out=dst[:, :, P * r : P * (r + 1), :],
+                in_=x_banks[h, r][:].rearrange("p (c u) n -> p c n u", u=2),
+            )
+
+        def x_quant(h, c):
+            nc.vector.quantize_mx(
+                out=x_codes[h][:, c, :].bitcast(FP8X4),
+                scales=x_planes[h][:, c, :],
+                in_=xg[h][:, c, :, :].rearrange("p n t -> p (n t)"),
+            )
+
+        wg, w_codes, w_planes = {}, {}, {}
+
+        def w_piece(engine_copy, g, c, a, b):
+            if g not in wg:
+                wg[g] = work.tile([P, 2, 2048], BF16, name="wg", bufs=3, align_bytes=64)
+            off = 512 * (g % 2)
+            src = w_raw[g // 2][:, c, :, off + 4 * a : off + 4 * b]
+            dst = wg[g][:, c, :].rearrange("p (t m i j) -> p m t j i", t=4, i=2, j=4)
+            engine_copy(
+                out=dst[:, a // 2 : b // 2, :, :, :],
+                in_=src.rearrange("p j (m i t) -> p m t j i", t=4, i=2),
+            )
+
+        def w_scalar(g, c, a, b):
+            w_piece(nc.scalar.copy, g, c, a, b)
+
+        def w_vector(g, c, a, b):
+            w_piece(nc.vector.tensor_copy, g, c, a, b)
+
+        def w_quant(g, c):
+            if g not in w_codes:
+                w_codes[g] = work.tile([P, 2, 512], U32, name="w_codes", bufs=4, align_bytes=64)
+                w_planes[g] = work.tile([P, 2, 512], U8, name="w_planes", bufs=4, align_bytes=64)
+            nc.vector.quantize_mx(
+                out=w_codes[g][:, c, :].bitcast(FP8X4), scales=w_planes[g][:, c, :], in_=wg[g][:, c, :]
+            )
+
+        w3g = {}
+        w3_codes = keep.tile([P, GROUPS, 2 * LATENT], U32, name="w3_codes", align_bytes=64)
+        w3_planes = keep.tile([P, GROUPS, 2 * LATENT], U8, name="w3_planes", align_bytes=64)
+
+        def w3_lay(g):
+            w3g[g] = work.tile([P, 1024], BF16, name="w3g", bufs=2, align_bytes=64)
+            nc.vector.tensor_copy(
+                out=w3g[g][:].rearrange("p (w c i j) -> p w c j i", w=2, i=4, j=4),
+                in_=w3_raw[:, :, g, :].rearrange("p w (j c i) -> p w c j i", j=4, i=4),
+            )
+
+        def w3_quant(g):
+            nc.vector.quantize_mx(
+                out=w3_codes[:, g, :].bitcast(FP8X4), scales=w3_planes[:, g, :], in_=w3g[g][:]
+            )
+
+        bias = keep.tile([P, GROUPS, 4], F32, name="bias")
+        enc, encg, enc_codes, enc_planes = {}, {}, {}, {}
+
+        def first_stage(h, g, between, a=0, b=HALF):
+            if (h, g) not in enc:
+                enc[h, g] = work.tile([P, 4, HALF], BF16, name="enc", bufs=3)
+            for t in range(4):
+                bank = psum.tile([P, 4, P], F32, name="bank")
+                flat = bank[:].rearrange("p a b -> p (a b)")[:, : b - a]
+                for c in range(2):
+                    nc.tensor.matmul_mx(
+                        out=flat,
+                        lhsT=w_codes[g][:, c, P * t : P * (t + 1)].bitcast(FP8X4),
+                        lhsT_scale=w_planes[g][:, c, P * t : P * (t + 1)],
+                        rhs=x_codes[h][:, c, a:b].bitcast(FP8X4),
+                        rhs_scale=x_planes[h][:, c, a:b],
+                        start=(c == 0),
+                        stop=(c == 1),
+                    )
+                nc.scalar.activation(out=enc[h, g][:, t, a:b], in_=flat, func=RELU, bias=bias[:, g, t : t + 1])
+                for args in between.get(t, []):
+                    w_scalar(*args)
+
+        def enc_lay(h, g, a=0, b=HALF):
+            if (h, g) not in encg:
+                encg[h, g] = work.tile([P, 4 * HALF], BF16, name="encg", bufs=3, align_bytes=64)
+            nc.vector.tensor_copy(
+                out=encg[h, g][:, 4 * a : 4 * b].rearrange("p (c i t) -> p c t i", i=4, t=4),
+                in_=enc[h, g][:, :, a:b].rearrange("p t (c i) -> p c t i", i=4),
+            )
+
+        def enc_quant(h, g, a=0, b=HALF):
+            if (h, g) not in enc_codes:
+                bufs = 3 if h == 0 else 8
+                enc_codes[h, g] = work.tile([P, HALF], U32, name=f"enc_codes{h}", bufs=bufs, align_bytes=64)
+                enc_planes[h, g] = work.tile([P, HALF], U8, name=f"enc_planes{h}", bufs=bufs, align_bytes=64)
+            nc.vector.quantize_mx(
+                out=enc_codes[h, g][:, a:b].bitcast(FP8X4),
+                scales=enc_planes[h, g][:, a:b],
+                in_=encg[h, g][:, 4 * a : 4 * b],
+            )
+
+        acc = {}
+
+        def second_stage(h, g, rows=(0, 1, 2, 3)):
+            for r in rows:
+                if (h, r) not in acc:
+                    acc[h, r] = accs.tile([P, 2 * LATENT], F32, name=f"acc{r}")
+                nc.tensor.matmul_mx(
+                    out=acc[h, r][:],
+                    lhsT=enc_codes[h, g][:, P * r : P * (r + 1)].bitcast(FP8X4),
+                    lhsT_scale=enc_planes[h, g][:, P * r : P * (r + 1)],
+                    rhs=w3_codes[:, g, :].bitcast(FP8X4),
+                    rhs_scale=w3_planes[:, g, :],
+                    start=(g == 0),
+                    stop=(g == GROUPS - 1),
+                )
+
+        y, z, relus = {}, {}, {}
+        views = [o.rearrange("(p r) l -> p r l", r=ROWS) for o in (out_0, out_1, out_2)]
+
+        def add_bias(h, r):
+            if h not in y:
+                y[h] = work.tile([P, 4, 2 * LATENT], F32, name="y", bufs=2)
+                z[h] = work.tile([P, 4, LATENT], F32, name="z", bufs=2)
+                relus[h] = [work.tile([P, 4, LATENT], F32, name=f"relu{i}", bufs=2) for i in range(2)]
+            nc.vector.tensor_tensor(out=y[h][:, r, :], in0=acc[h, r][:], in1=bias3[:], op=ADD)
+
+        def relu_out(h, i, a, b):
+            nc.scalar.activation(
+                out=relus[h][i][:, a:b, :], in_=y[h][:, a:b, LATENT * i : LATENT * (i + 1)], func=RELU
+            )
+            nc.sync.dma_start(out=views[i][:, 4 * h + a : 4 * h + b, :], in_=relus[h][i][:, a:b, :])
+
+        def z_noise(h, a, b):
+            nc.vector.scalar_tensor_tensor(
+                out=z[h][:, a:b, :], in0=y[h][:, a:b, LATENT:], scalar=0.0,
+                in1=eps_sb[:, 4 * h + a : 4 * h + b, :], op0=MAX, op1=MULT,
+            )
+
+        def z_out(h, a, b):
+            nc.vector.scalar_tensor_tensor(
+                out=z[h][:, a:b, :], in0=y[h][:, a:b, :LATENT], scalar=0.0,
+                in1=z[h][:, a:b, :], op0=MAX, op1=ADD,
+            )
+            nc.sync.dma_start(out=views[2][:, 4 * h + a : 4 * h + b, :], in_=z[h][:, a:b, :])
+
+        def x_chain(h, r):
+            x_product(h, r)
+            x_turn(h, r)
+            x_out(h, r)
+
+        x_product(0, 0)
+        x_turn(0, 0)
+        w_scalar(0, 0, 0, 64)
+        x_out(0, 0)
+        x_chain(0, 1)
+        w_scalar(0, 0, 64, 128)
+        x_chain(0, 2)
+        x_chain(0, 3)
+        nc.vector.tensor_copy(out=bias[:], in_=bias_raw[:])
+        w_vector(0, 1, 0, 64)
+        w_vector(0, 1, 64, 128)
+        x_quant(0, 0)
+        x_quant(0, 1)
+        w_quant(0, 0)
+        w_quant(0, 1)
+        for c in range(2):
+            for a in (0, 64):
+                w_scalar(1, c, a, a + 64)
+
+        first_stage(0, 0, {3: [(2, 0, 0, 64)]})
+        x_chain(1, 0)
+        x_chain(1, 1)
+        w_quant(1, 0)
+        x_chain(1, 2)
+        w_quant(1, 1)
+        x_chain(1, 3)
+        enc_lay(0, 0)
+        w3_lay(0)
+        enc_quant(0, 0)
+        w3_quant(0)
+
+        first_stage(0, 1, {1: [(2, 1, 0, 64)]})
+        w_vector(2, 0, 64, 128)
+        x_quant(1, 0)
+        x_quant(1, 1)
+        w_quant(2, 0)
+        w_vector(2, 1, 64, 128)
+        w3_lay(1)
+
+        load_w(3, 0, 0, 1024)
+        load_w(3, 1, 0, 1024)
+
+        for step in range(2, 16):
+            h, g = UNITS[step]
+            lh, lg = UNITS[step - 1]
+            pg, pc = (step + 4) // 2, step % 2
+            prep = pg < GROUPS
+            if step < 15:
+                first_stage(h, g, {1: [(pg, pc, 0, 64)]} if prep else {})
+            else:
+                first_stage(h, g, {}, 0, 256)
+                first_stage(h, g, {}, 256, 512)
+            qg, qc = (step + 3) // 2, (step - 1) % 2
+            if qg < GROUPS:
+                w_quant(qg, qc)
+            if prep:
+                w_vector(pg, pc, 64, 128)
+            enc_lay(lh, lg)
+            w3_group = (step + 1) // 2
+            if w3_group < GROUPS:
+                if step % 2 == 1:
+                    w3_lay(w3_group)
+                else:
+                    w3_quant(step // 2)
+            enc_quant(lh, lg)
+            sh, sg = UNITS[step - 2]
+            if sh == 0:
+                second_stage(sh, sg)
+            if step == 15:
+                for r in range(4):
+                    add_bias(0, r)
+                for gg in range(GROUPS - 1):
+                    second_stage(1, gg)
+
+        h, g = UNITS[15]
+        enc_lay(h, g, 0, 256)
+        z_noise(0, 0, 4)
+        enc_quant(h, g, 0, 256)
+        enc_lay(h, g, 256, 512)
+        z_out(0, 0, 4)
+        enc_quant(h, g, 256, 512)
+        relu_out(0, 0, 0, 4)
+        relu_out(0, 1, 0, 4)
+        for a in (0, 2):
+            second_stage(1, GROUPS - 1, rows=(a, a + 1))
+        for a in (0, 2):
+            add_bias(1, a)
+            add_bias(1, a + 1)
+            relu_out(1, 0, a, a + 2)
+            relu_out(1, 1, a, a + 2)
+            z_noise(1, a, a + 2)
+            z_out(1, a, a + 2)

@@ -16,6 +16,7 @@ ADD = mybir.AluOpType.add
 MULT = mybir.AluOpType.mult
 MAX = mybir.AluOpType.max
 RELU = mybir.ActivationFunctionType.Relu
+COPY = mybir.ActivationFunctionType.Copy
 
 P = 128
 FLOPS = 2 * TOKENS * IMAGE * HIDDEN + 2 * TOKENS * HIDDEN * 2 * LATENT
@@ -23,8 +24,13 @@ FLOPS = 2 * TOKENS * IMAGE * HIDDEN + 2 * TOKENS * HIDDEN * 2 * LATENT
 GROUPS = 8
 HALF = 512
 ROWS = TOKENS // P
+LAG = 2
 
-UNITS = [(0, 0)] + [(h, g - h) for g in range(1, GROUPS) for h in range(2)] + [(1, GROUPS - 1)]
+SPLIT = 2
+
+UNITS = sorted(
+    [(h, g, 0, 4) for h in range(2) for g in range(GROUPS - SPLIT * h)], key=lambda u: (u[1] + LAG * u[0], u[0])
+) + [(1, g, r, 2) for r in (0, 2) for g in range(GROUPS - SPLIT, GROUPS)]
 
 
 def tile_mae_pa_kernel(tc, x_bytes, x_scale, eps, W11, b11, W31, b31, W32, b32, out_0, out_1, out_2):
@@ -38,131 +44,161 @@ def tile_mae_pa_kernel(tc, x_bytes, x_scale, eps, W11, b11, W31, b31, W32, b32, 
         ident = keep.tile([P, P], F32, name="ident")
         make_identity(nc, ident[:])
         ctx.enter_context(tc.manual_schedule())
-        ctx.enter_context(nc.allow_non_contiguous_dma(reason="runs of four biases"))
+        ctx.enter_context(nc.allow_non_contiguous_dma(reason="runs of four scales and of four biases"))
 
-        warm = keep.tile([P, 1], F32, name="warm")
-        nc.vector.memset(warm[:], 0.0)
-        warm_out = keep.tile([P, 1], F32, name="warm_out")
+        scale_cols = keep.tile([P, 2, 4], F32, name="scale_cols")
+        nc.sync.dma_start(out=scale_cols[:], in_=x_scale.rearrange("o (c p t) -> p (o c) t", p=P, t=4))
 
-        scale = keep.tile([P, IMAGE], F32, name="scale")
-        nc.scalar.dma_start(out=scale[:], in_=x_scale.rearrange("o k -> (o k)").partition_broadcast(P))
-        nc.scalar.activation(out=warm_out[:], in_=warm[:], func=RELU)
-
-        xq = [keep.tile([P, 4 * IMAGE], U8, name=f"xq{h}") for h in range(2)]
+        xq = [keep.tile([P, IMAGE], U8, name=f"xq{r}") for r in range(2)]
+        xq_rest = [keep.tile([P, 2 * IMAGE], U8, name="xq23"), keep.tile([P, 4 * IMAGE], U8, name="xq47")]
         x_view = x_bytes.rearrange("(p r) k -> p (r k)", r=ROWS)
 
-        def load_x(h, a, b):
-            nc.sync.dma_start(
-                out=xq[h][:, a * IMAGE : b * IMAGE],
-                in_=x_view[:, (4 * h + a) * IMAGE : (4 * h + b) * IMAGE],
-            )
+        def x_row(r):
+            if r < 2:
+                return xq[r][:]
+            if r < 4:
+                return xq_rest[0][:, (r - 2) * IMAGE : (r - 1) * IMAGE]
+            return xq_rest[1][:, (r - 4) * IMAGE : (r - 3) * IMAGE]
 
-        w_raw = [None] * 4
+        w_raw = {}
         w_view = W11.rearrange("(c p j) n -> c p j n", c=2, j=4)
 
-        def load_w(pair, c, a, b):
-            if w_raw[pair] is None:
-                w_raw[pair] = work.tile([P, 2, 4, 1024], BF16, name="w_raw", bufs=3)
-            nc.sync.dma_start(
-                out=w_raw[pair][:, c, :, a:b], in_=w_view[c, :, :, 1024 * pair + a : 1024 * pair + b]
-            )
+        def load_w(g, c, n):
+            tile = work.tile([P, 4, 512 * n], BF16, name=f"w_raw{n}", bufs=8 // n)
+            nc.sync.dma_start(out=tile[:], in_=w_view[c, :, :, 512 * g : 512 * (g + n)])
+            for i in range(n):
+                w_raw[g + i, c] = tile[:, :, 512 * i : 512 * (i + 1)]
 
-        w3_raw = keep.tile([P, 2, GROUPS, 512], BF16, name="w3_raw")
+        w3_raw = {}
         w3_view = [w.rearrange("(g p j) l -> p g (j l)", p=P, j=4) for w in (W31, W32)]
 
         def load_w3(a, b):
+            tile = keep.tile([P, 2, b - a, 512], BF16, name=f"w3_raw{a}")
             for i in range(2):
-                nc.sync.dma_start(out=w3_raw[:, i, a:b, :], in_=w3_view[i][:, a:b, :])
+                nc.sync.dma_start(out=tile[:, i, :, :], in_=w3_view[i][:, a:b, :])
+            for g in range(a, b):
+                w3_raw[g] = tile[:, :, g - a, :]
 
-        load_x(0, 0, 1)
-        load_w(0, 0, 0, 256)
-        load_x(0, 1, 2)
-        load_w(0, 0, 256, 512)
-        load_x(0, 2, 4)
-        load_w(0, 1, 0, 512)
-        bias_raw = keep.tile([P, GROUPS, 4], BF16, name="bias_raw")
-        nc.scalar.dma_start(out=bias_raw[:], in_=b11.rearrange("(g p t) -> p g t", p=P, t=4))
-        load_w(0, 0, 512, 1024)
-        load_w(0, 1, 512, 1024)
-        load_x(1, 0, 4)
+        load_w(0, 0, 1)
+        nc.sync.dma_start(out=xq[0][:], in_=x_view[:, :IMAGE])
+        nc.sync.dma_start(out=xq[1][:], in_=x_view[:, IMAGE : 2 * IMAGE])
+        nc.sync.dma_start(out=xq_rest[0][:], in_=x_view[:, 2 * IMAGE : 4 * IMAGE])
+        load_w(0, 1, 1)
+        nc.sync.dma_start(out=xq_rest[1][:], in_=x_view[:, 4 * IMAGE :])
+        bias = keep.tile([P, GROUPS, 4], BF16, name="bias")
+        nc.sync.dma_start(out=bias[:], in_=b11.rearrange("(g p t) -> p g t", p=P, t=4))
+        load_w(1, 0, 1)
+        load_w(1, 1, 1)
+        load_w(2, 0, 1)
+        load_w(2, 1, 1)
         load_w3(0, 2)
-        load_w(1, 0, 0, 1024)
-        load_w(1, 1, 0, 1024)
-        load_w3(2, 8)
+        load_w(3, 0, 1)
+        load_w(3, 1, 1)
+        load_w3(2, 4)
+        load_w(4, 0, 2)
+        load_w(4, 1, 2)
+        load_w3(4, 8)
+        load_w(6, 0, 2)
+        load_w(6, 1, 2)
         bias3 = keep.tile([P, 2 * LATENT], BF16, name="bias3")
         nc.sync.dma_start(out=bias3[:, :LATENT], in_=b31.partition_broadcast(P))
         nc.sync.dma_start(out=bias3[:, LATENT:], in_=b32.partition_broadcast(P))
         eps_sb = keep.tile([P, ROWS, LATENT], BF16, name="eps_sb")
         nc.sync.dma_start(out=eps_sb[:], in_=eps.rearrange("(p r) l -> p r l", r=ROWS))
-        load_w(2, 0, 0, 1024)
-        load_w(2, 1, 0, 1024)
 
-        xg = [None, None]
+        ident_bf = keep.tile([P, P], BF16, name="ident_bf")
+        nc.scalar.activation(out=ident_bf[:], in_=ident[:], func=COPY)
+
+        scale = keep.tile([P, IMAGE], F32, name="scale")
+
+        def spread_scale(c):
+            bank = psum.tile([P, 4, P], F32, name="bank")
+            for t in range(4):
+                nc.tensor.transpose(bank[:, t, :], scale_cols[:, c, t : t + 1].to_broadcast([P, P]), ident[:])
+            nc.scalar.copy(
+                out=scale[:, 512 * c : 512 * (c + 1)].rearrange("p (m t) -> p m t", t=4),
+                in_=bank[:].rearrange("p t m -> p m t"),
+            )
+
+        xg, xb = {}, {}
         x_codes = [keep.tile([P, 2, HALF], U32, name=f"x_codes{h}", align_bytes=64) for h in range(2)]
         x_planes = [keep.tile([P, 2, HALF], U8, name=f"x_planes{h}", align_bytes=64) for h in range(2)]
 
-        xb = {}
-
-        def x_product(h, r):
-            xb[h, r] = work.tile([P, IMAGE], BF16, name="xb", bufs=3)
+        def x_product(r, a=0, b=IMAGE):
+            if r not in xb:
+                xb[r] = work.tile([P, IMAGE], BF16, name="xb", bufs=5)
             nc.vector.tensor_tensor(
-                out=xb[h, r][:], in0=xq[h][:, r * IMAGE : (r + 1) * IMAGE].bitcast(FP8), in1=scale[:], op=MULT
+                out=xb[r][:, a:b], in0=x_row(r)[:, a:b].bitcast(FP8), in1=scale[:, a:b], op=MULT
             )
 
-        x_banks = {}
-
-        def x_turn(h, r):
+        def x_turn(r):
+            h = r // 4
             bank = psum.tile([P, 4, P], F32, name="bank")
-            words = xb[h, r][:].bitcast(F32)
+            words = xb[r][:].bitcast(F32)
             for c in range(2):
                 for u in range(2):
                     nc.tensor.transpose(
                         bank[:, 2 * c + u, :], words[:, 256 * c + u : 256 * (c + 1) : 2], ident[:]
                     )
-            x_banks[h, r] = bank
-
-        def x_out(h, r):
-            if xg[h] is None:
-                xg[h] = work.tile([P, 2, HALF, 4], BF16, name="xg", bufs=1, align_bytes=64)
-            dst = xg[h][:].rearrange("p c n t -> p (c n t)").bitcast(F32)
-            dst = dst.rearrange("p (c n u) -> p c n u", c=2, u=2)
+            if h not in xg:
+                xg[h] = work.tile([P, 2, 2 * HALF], F32, name="xg", bufs=2, align_bytes=64)
+            dst = xg[h][:].rearrange("p c (n u) -> p c n u", u=2)
             nc.scalar.copy(
-                out=dst[:, :, P * r : P * (r + 1), :],
-                in_=x_banks[h, r][:].rearrange("p (c u) n -> p c n u", u=2),
+                out=dst[:, :, P * (r % 4) : P * (r % 4 + 1), :],
+                in_=bank[:].rearrange("p (c u) n -> p c n u", u=2),
             )
 
         def x_quant(h, c):
             nc.vector.quantize_mx(
                 out=x_codes[h][:, c, :].bitcast(FP8X4),
                 scales=x_planes[h][:, c, :],
-                in_=xg[h][:, c, :, :].rearrange("p n t -> p (n t)"),
+                in_=xg[h][:, c, :].bitcast(BF16),
             )
 
         wg, w_codes, w_planes = {}, {}, {}
 
-        def w_piece(engine_copy, g, c, a, b):
-            if g not in wg:
-                wg[g] = work.tile([P, 2, 2048], BF16, name="wg", bufs=3, align_bytes=64)
-            off = 512 * (g % 2)
-            src = w_raw[g // 2][:, c, :, off + 4 * a : off + 4 * b]
-            dst = wg[g][:, c, :].rearrange("p (t m i j) -> p m t j i", t=4, i=2, j=4)
+        def w_tile(g, c):
+            if (g, c) not in wg:
+                wg[g, c] = work.tile([P, 1024], F32, name="wg", bufs=5, align_bytes=64)
+            return wg[g, c]
+
+        def w_tensor(g, c, b):
+            bank = psum.tile([P, 4, P], F32, name="bank")
+            flat = bank[:].rearrange("p a b -> p (a b)")
+            for i in range(2):
+                n0 = 256 * b + P * i
+                nc.tensor.matmul(
+                    out=flat[:, 256 * i : 256 * (i + 1)].bitcast(BF16),
+                    lhsT=ident_bf[:],
+                    rhs=w_raw[g, c][:, :, n0 : n0 + P].rearrange("p j n -> p n j"),
+                    start=True,
+                    stop=True,
+                )
+            dst = w_tile(g, c)[:].rearrange("p (t m u) -> p t m u", t=4, u=2)
+            nc.scalar.copy(
+                out=dst[:, :, 64 * b : 64 * (b + 1), :], in_=flat.rearrange("p (m t u) -> p t m u", t=4, u=2)
+            )
+
+        def w_copy(engine_copy, g, c, b):
+            src = w_raw[g, c][:, :, 256 * b : 256 * (b + 1)]
+            dst = w_tile(g, c)[:].bitcast(BF16).rearrange("p (t m i j) -> p m t j i", t=4, i=2, j=4)
             engine_copy(
-                out=dst[:, a // 2 : b // 2, :, :, :],
+                out=dst[:, 32 * b : 32 * (b + 1), :, :, :],
                 in_=src.rearrange("p j (m i t) -> p m t j i", t=4, i=2),
             )
 
-        def w_scalar(g, c, a, b):
-            w_piece(nc.scalar.copy, g, c, a, b)
+        def w_vector(g, c, b):
+            w_copy(nc.vector.tensor_copy, g, c, b)
 
-        def w_vector(g, c, a, b):
-            w_piece(nc.vector.tensor_copy, g, c, a, b)
+        def w_scalar(g, c, b):
+            w_copy(nc.scalar.copy, g, c, b)
 
         def w_quant(g, c):
             if g not in w_codes:
-                w_codes[g] = work.tile([P, 2, 512], U32, name="w_codes", bufs=4, align_bytes=64)
-                w_planes[g] = work.tile([P, 2, 512], U8, name="w_planes", bufs=4, align_bytes=64)
+                w_codes[g] = work.tile([P, 2, 512], U32, name="w_codes", bufs=LAG + 3, align_bytes=64)
+                w_planes[g] = work.tile([P, 2, 512], U8, name="w_planes", bufs=LAG + 3, align_bytes=64)
             nc.vector.quantize_mx(
-                out=w_codes[g][:, c, :].bitcast(FP8X4), scales=w_planes[g][:, c, :], in_=wg[g][:, c, :]
+                out=w_codes[g][:, c, :].bitcast(FP8X4), scales=w_planes[g][:, c, :], in_=wg[g, c][:].bitcast(BF16)
             )
 
         w3g = {}
@@ -173,7 +209,7 @@ def tile_mae_pa_kernel(tc, x_bytes, x_scale, eps, W11, b11, W31, b31, W32, b32, 
             w3g[g] = work.tile([P, 1024], BF16, name="w3g", bufs=2, align_bytes=64)
             nc.vector.tensor_copy(
                 out=w3g[g][:].rearrange("p (w c i j) -> p w c j i", w=2, i=4, j=4),
-                in_=w3_raw[:, :, g, :].rearrange("p w (j c i) -> p w c j i", j=4, i=4),
+                in_=w3_raw[g].rearrange("p w (j c i) -> p w c j i", j=4, i=4),
             )
 
         def w3_quant(g):
@@ -181,12 +217,12 @@ def tile_mae_pa_kernel(tc, x_bytes, x_scale, eps, W11, b11, W31, b31, W32, b32, 
                 out=w3_codes[:, g, :].bitcast(FP8X4), scales=w3_planes[:, g, :], in_=w3g[g][:]
             )
 
-        bias = keep.tile([P, GROUPS, 4], F32, name="bias")
         enc, encg, enc_codes, enc_planes = {}, {}, {}, {}
 
-        def first_stage(h, g, between, a=0, b=HALF):
-            if (h, g) not in enc:
-                enc[h, g] = work.tile([P, 4, HALF], BF16, name="enc", bufs=3)
+        def first_stage(s, between):
+            h, g, r0, rows = UNITS[s]
+            a, b = P * r0, P * (r0 + rows)
+            enc[s] = work.tile([P, 4, b - a], BF16, name="enc", bufs=3)
             for t in range(4):
                 bank = psum.tile([P, 4, P], F32, name="bank")
                 flat = bank[:].rearrange("p a b -> p (a b)")[:, : b - a]
@@ -200,168 +236,158 @@ def tile_mae_pa_kernel(tc, x_bytes, x_scale, eps, W11, b11, W31, b31, W32, b32, 
                         start=(c == 0),
                         stop=(c == 1),
                     )
-                nc.scalar.activation(out=enc[h, g][:, t, a:b], in_=flat, func=RELU, bias=bias[:, g, t : t + 1])
-                for args in between.get(t, []):
-                    w_scalar(*args)
+                nc.scalar.activation(out=enc[s][:, t, :], in_=flat, func=RELU, bias=bias[:, g, t : t + 1])
+                for job in between.get(t, []):
+                    job()
 
-        def enc_lay(h, g, a=0, b=HALF):
-            if (h, g) not in encg:
-                encg[h, g] = work.tile([P, 4 * HALF], BF16, name="encg", bufs=3, align_bytes=64)
+        def enc_lay(s):
+            encg[s] = work.tile([P, 4 * P * UNITS[s][3]], BF16, name="encg", bufs=2, align_bytes=64)
             nc.vector.tensor_copy(
-                out=encg[h, g][:, 4 * a : 4 * b].rearrange("p (c i t) -> p c t i", i=4, t=4),
-                in_=enc[h, g][:, :, a:b].rearrange("p t (c i) -> p c t i", i=4),
+                out=encg[s][:].rearrange("p (c i t) -> p c t i", i=4, t=4),
+                in_=enc[s][:].rearrange("p t (c i) -> p c t i", i=4),
             )
 
-        def enc_quant(h, g, a=0, b=HALF):
-            if (h, g) not in enc_codes:
-                bufs = 3 if h == 0 else 8
-                enc_codes[h, g] = work.tile([P, HALF], U32, name=f"enc_codes{h}", bufs=bufs, align_bytes=64)
-                enc_planes[h, g] = work.tile([P, HALF], U8, name=f"enc_planes{h}", bufs=bufs, align_bytes=64)
-            nc.vector.quantize_mx(
-                out=enc_codes[h, g][:, a:b].bitcast(FP8X4),
-                scales=enc_planes[h, g][:, a:b],
-                in_=encg[h, g][:, 4 * a : 4 * b],
-            )
+        def enc_quant(s):
+            enc_codes[s] = work.tile([P, P * UNITS[s][3]], U32, name="enc_codes", bufs=3, align_bytes=64)
+            enc_planes[s] = work.tile([P, P * UNITS[s][3]], U8, name="enc_planes", bufs=3, align_bytes=64)
+            nc.vector.quantize_mx(out=enc_codes[s][:].bitcast(FP8X4), scales=enc_planes[s][:], in_=encg[s][:])
 
-        acc = {}
+        acc = [accs.tile([P, 2, 2 * LATENT], F32, name=f"acc{i}") for i in range(4)]
 
-        def second_stage(h, g, rows=(0, 1, 2, 3)):
-            for r in rows:
-                if (h, r) not in acc:
-                    acc[h, r] = accs.tile([P, 2 * LATENT], F32, name=f"acc{r}")
+        def second_stage(s):
+            h, g, r0, rows = UNITS[s]
+            for r in range(rows):
                 nc.tensor.matmul_mx(
-                    out=acc[h, r][:],
-                    lhsT=enc_codes[h, g][:, P * r : P * (r + 1)].bitcast(FP8X4),
-                    lhsT_scale=enc_planes[h, g][:, P * r : P * (r + 1)],
+                    out=acc[2 * h + (r0 + r) // 2][:, r % 2, :],
+                    lhsT=enc_codes[s][:, P * r : P * (r + 1)].bitcast(FP8X4),
+                    lhsT_scale=enc_planes[s][:, P * r : P * (r + 1)],
                     rhs=w3_codes[:, g, :].bitcast(FP8X4),
                     rhs_scale=w3_planes[:, g, :],
-                    start=(g == 0),
-                    stop=(g == GROUPS - 1),
+                    start=(g == 0 and r % 2 == 0),
+                    stop=(g == GROUPS - 1 and r % 2 == 1),
                 )
 
         y, z, relus = {}, {}, {}
         views = [o.rearrange("(p r) l -> p r l", r=ROWS) for o in (out_0, out_1, out_2)]
 
-        def add_bias(h, r):
-            if h not in y:
-                y[h] = work.tile([P, 4, 2 * LATENT], F32, name="y", bufs=2)
-                z[h] = work.tile([P, 4, LATENT], F32, name="z", bufs=2)
-                relus[h] = [work.tile([P, 4, LATENT], F32, name=f"relu{i}", bufs=2) for i in range(2)]
-            nc.vector.tensor_tensor(out=y[h][:, r, :], in0=acc[h, r][:], in1=bias3[:], op=ADD)
+        def add_bias(i):
+            y[i] = work.tile([P, 2, 2 * LATENT], F32, name="y", bufs=4)
+            nc.vector.tensor_tensor(
+                out=y[i][:], in0=acc[i][:], in1=bias3[:].unsqueeze(1).to_broadcast([P, 2, 2 * LATENT]), op=ADD
+            )
 
-        def relu_out(h, i, a, b):
+        def relu_out(i):
+            relus[i] = work.tile([P, 2, 2, LATENT], F32, name="relu", bufs=4)
             nc.scalar.activation(
-                out=relus[h][i][:, a:b, :], in_=y[h][:, a:b, LATENT * i : LATENT * (i + 1)], func=RELU
+                out=relus[i][:], in_=y[i][:].rearrange("p r (w l) -> p w r l", w=2), func=RELU
             )
-            nc.sync.dma_start(out=views[i][:, 4 * h + a : 4 * h + b, :], in_=relus[h][i][:, a:b, :])
+            for w in range(2):
+                nc.sync.dma_start(out=views[w][:, 2 * i : 2 * i + 2, :], in_=relus[i][:, w, :, :])
 
-        def z_noise(h, a, b):
+        def z_noise(i):
+            z[i] = work.tile([P, 2, LATENT], F32, name="z", bufs=4)
             nc.vector.scalar_tensor_tensor(
-                out=z[h][:, a:b, :], in0=y[h][:, a:b, LATENT:], scalar=0.0,
-                in1=eps_sb[:, 4 * h + a : 4 * h + b, :], op0=MAX, op1=MULT,
+                out=z[i][:], in0=y[i][:, :, LATENT:], scalar=0.0,
+                in1=eps_sb[:, 2 * i : 2 * i + 2, :], op0=MAX, op1=MULT,
             )
 
-        def z_out(h, a, b):
+        def z_out(i):
             nc.vector.scalar_tensor_tensor(
-                out=z[h][:, a:b, :], in0=y[h][:, a:b, :LATENT], scalar=0.0,
-                in1=z[h][:, a:b, :], op0=MAX, op1=ADD,
+                out=z[i][:], in0=y[i][:, :, :LATENT], scalar=0.0, in1=z[i][:], op0=MAX, op1=ADD,
             )
-            nc.sync.dma_start(out=views[2][:, 4 * h + a : 4 * h + b, :], in_=z[h][:, a:b, :])
+            nc.sync.dma_start(out=views[2][:, 2 * i : 2 * i + 2, :], in_=z[i][:])
 
-        def x_chain(h, r):
-            x_product(h, r)
-            x_turn(h, r)
-            x_out(h, r)
-
-        x_product(0, 0)
-        x_turn(0, 0)
-        w_scalar(0, 0, 0, 64)
-        x_out(0, 0)
-        x_chain(0, 1)
-        w_scalar(0, 0, 64, 128)
-        x_chain(0, 2)
-        x_chain(0, 3)
-        nc.vector.tensor_copy(out=bias[:], in_=bias_raw[:])
-        w_vector(0, 1, 0, 64)
-        w_vector(0, 1, 64, 128)
+        spread_scale(0)
+        spread_scale(1)
+        w_tensor(0, 0, 0)
+        w_tensor(0, 0, 1)
+        x_product(0, 0, 512)
+        x_product(0, 512, IMAGE)
+        x_product(1)
+        x_turn(0)
+        x_product(2)
+        x_turn(1)
+        w_tensor(0, 1, 0)
+        x_product(3)
+        x_turn(2)
+        w_tensor(0, 1, 1)
+        x_turn(3)
+        w_quant(0, 0)
+        x_product(4)
+        w_quant(0, 1)
         x_quant(0, 0)
         x_quant(0, 1)
-        w_quant(0, 0)
-        w_quant(0, 1)
+        x_product(5)
         for c in range(2):
-            for a in (0, 64):
-                w_scalar(1, c, a, a + 64)
+            w_tensor(1, c, 0)
+            w_tensor(1, c, 1)
+        x_turn(4)
 
-        first_stage(0, 0, {3: [(2, 0, 0, 64)]})
-        x_chain(1, 0)
-        x_chain(1, 1)
+        first_stage(0, {
+            0: [lambda: x_turn(5)], 1: [lambda: w_tensor(2, 0, 0), lambda: w_tensor(2, 0, 1)],
+            2: [lambda: w_tensor(2, 1, 0)], 3: [lambda: w_tensor(2, 1, 1)],
+        })
         w_quant(1, 0)
-        x_chain(1, 2)
+        x_product(6)
         w_quant(1, 1)
-        x_chain(1, 3)
-        enc_lay(0, 0)
+        x_product(7)
         w3_lay(0)
-        enc_quant(0, 0)
-        w3_quant(0)
 
-        first_stage(0, 1, {1: [(2, 1, 0, 64)]})
-        w_vector(2, 0, 64, 128)
-        x_quant(1, 0)
-        x_quant(1, 1)
-        w_quant(2, 0)
-        w_vector(2, 1, 64, 128)
-        w3_lay(1)
-
-        load_w(3, 0, 0, 1024)
-        load_w(3, 1, 0, 1024)
-
-        for step in range(2, 16):
-            h, g = UNITS[step]
-            lh, lg = UNITS[step - 1]
-            pg, pc = (step + 4) // 2, step % 2
-            prep = pg < GROUPS
-            if step < 15:
-                first_stage(h, g, {1: [(pg, pc, 0, 64)]} if prep else {})
-            else:
-                first_stage(h, g, {}, 0, 256)
-                first_stage(h, g, {}, 256, 512)
-            qg, qc = (step + 3) // 2, (step - 1) % 2
+        last = len(UNITS) - 1
+        for s in range(1, last + 1):
+            pg, pc = (s + 5) // 2, (s + 1) % 2
+            between = {}
+            if pg < GROUPS:
+                between[0] = [lambda: w_tensor(pg, pc, 0)]
+                if pc == 0:
+                    between[2] = [lambda: w_tensor(pg, pc, 1)]
+            if s == 1:
+                between[1] = [lambda: x_turn(6), lambda: x_turn(7)]
+            if s >= 2:
+                between.setdefault(1, []).append(lambda: second_stage(s - 2))
+            first_stage(s, between)
+            if s == last - 1:
+                relu_out(0)
+                relu_out(1)
+            qg, qc = (s + 4) // 2, s % 2
+            g3 = s if s < 3 else ((s + 3) // 2 if s % 2 else GROUPS)
+            if s == 1:
+                w_quant(2, 0)
+                w3_quant(0)
             if qg < GROUPS:
                 w_quant(qg, qc)
-            if prep:
-                w_vector(pg, pc, 64, 128)
-            enc_lay(lh, lg)
-            w3_group = (step + 1) // 2
-            if w3_group < GROUPS:
-                if step % 2 == 1:
-                    w3_lay(w3_group)
-                else:
-                    w3_quant(step // 2)
-            enc_quant(lh, lg)
-            sh, sg = UNITS[step - 2]
-            if sh == 0:
-                second_stage(sh, sg)
-            if step == 15:
-                for r in range(4):
-                    add_bias(0, r)
-                for gg in range(GROUPS - 1):
-                    second_stage(1, gg)
+            enc_lay(s - 1)
+            if s == 2:
+                x_quant(1, 0)
+                x_quant(1, 1)
+            if pg < GROUPS and pc == 1:
+                w_vector(pg, pc, 1)
+            if g3 < GROUPS:
+                w3_lay(g3)
+            if s == 14:
+                add_bias(0)
+            if s == 15:
+                z_noise(0)
+                z_noise(1)
+            if s == 16:
+                z_out(1)
+            enc_quant(s - 1)
+            if g3 < GROUPS:
+                w3_quant(g3)
+            if s == 14:
+                add_bias(1)
+            if s == 15:
+                z_out(0)
 
-        h, g = UNITS[15]
-        enc_lay(h, g, 0, 256)
-        z_noise(0, 0, 4)
-        enc_quant(h, g, 0, 256)
-        enc_lay(h, g, 256, 512)
-        z_out(0, 0, 4)
-        enc_quant(h, g, 256, 512)
-        relu_out(0, 0, 0, 4)
-        relu_out(0, 1, 0, 4)
-        for a in (0, 2):
-            second_stage(1, GROUPS - 1, rows=(a, a + 1))
-        for a in (0, 2):
-            add_bias(1, a)
-            add_bias(1, a + 1)
-            relu_out(1, 0, a, a + 2)
-            relu_out(1, 1, a, a + 2)
-            z_noise(1, a, a + 2)
-            z_out(1, a, a + 2)
+        add_bias(2)
+        second_stage(last - 1)
+        relu_out(2)
+        enc_lay(last)
+        z_noise(2)
+        enc_quant(last)
+        z_out(2)
+        second_stage(last)
+        add_bias(3)
+        relu_out(3)
+        z_noise(3)
+        z_out(3)

@@ -24,7 +24,10 @@ FLOPS = 2 * TOKENS * IMAGE * HIDDEN + 2 * TOKENS * HIDDEN * 2 * LATENT
 GROUPS = 8
 HALF = 512
 ROWS = TOKENS // P
-LAG = 2
+W_BUFS = {1: 4, 2: 6}
+CUTS = ((256,128),(128,128))
+S2AT = 2
+LAG = 1
 
 SPLIT = 2
 
@@ -64,12 +67,23 @@ def tile_mae_pa_kernel(tc, x_bytes, x_scale, eps, W11, b11, W31, b31, W32, b32, 
         w_view = W11.rearrange("(c p j) n -> c p j n", c=2, j=4)
 
         def load_w(g, c, n):
-            tile = work.tile([P, 4, 512 * n], BF16, name=f"w_raw{n}", bufs=8 // n)
+            tile = work.tile([P, 4, 512 * n], BF16, name=f"w_raw{n}", bufs=W_BUFS[n])
             nc.sync.dma_start(out=tile[:], in_=w_view[c, :, :, 512 * g : 512 * (g + n)])
             for i in range(n):
                 w_raw[g + i, c] = tile[:, :, 512 * i : 512 * (i + 1)]
 
-        w3_raw = {}
+        def load_first(a, b):
+            tile = keep.tile([P, 4, b - a], BF16, name=f"w_first{a}")
+            nc.sync.dma_start(out=tile[:], in_=w_view[0, :, :, a:b])
+            w_first[a] = tile
+
+        def w_src(g, c, a, b):
+            if (g, c) == (0, 0):
+                a0 = max(k for k in w_first if k <= a)
+                return w_first[a0][:, :, a - a0 : b - a0]
+            return w_raw[g, c][:, :, a:b]
+
+        w3_raw, w_first = {}, {}
         w3_view = [w.rearrange("(g p j) l -> p g (j l)", p=P, j=4) for w in (W31, W32)]
 
         def load_w3(a, b):
@@ -79,25 +93,23 @@ def tile_mae_pa_kernel(tc, x_bytes, x_scale, eps, W11, b11, W31, b31, W32, b32, 
             for g in range(a, b):
                 w3_raw[g] = tile[:, :, g - a, :]
 
-        load_w(0, 0, 1)
+        load_first(0, 256)
         nc.sync.dma_start(out=xq[0][:], in_=x_view[:, :IMAGE])
+        load_first(256, 512)
         nc.sync.dma_start(out=xq[1][:], in_=x_view[:, IMAGE : 2 * IMAGE])
         nc.sync.dma_start(out=xq_rest[0][:], in_=x_view[:, 2 * IMAGE : 4 * IMAGE])
         load_w(0, 1, 1)
+        load_w(1, 0, 1)
         nc.sync.dma_start(out=xq_rest[1][:], in_=x_view[:, 4 * IMAGE :])
+        load_w(1, 1, 1)
         bias = keep.tile([P, GROUPS, 4], BF16, name="bias")
         nc.sync.dma_start(out=bias[:], in_=b11.rearrange("(g p t) -> p g t", p=P, t=4))
-        load_w(1, 0, 1)
-        load_w(1, 1, 1)
-        load_w(2, 0, 1)
-        load_w(2, 1, 1)
+        load_w(2, 0, 2)
         load_w3(0, 2)
-        load_w(3, 0, 1)
-        load_w(3, 1, 1)
-        load_w3(2, 4)
+        load_w(2, 1, 2)
         load_w(4, 0, 2)
         load_w(4, 1, 2)
-        load_w3(4, 8)
+        load_w3(2, 8)
         load_w(6, 0, 2)
         load_w(6, 1, 2)
         bias3 = keep.tile([P, 2 * LATENT], BF16, name="bias3")
@@ -162,36 +174,34 @@ def tile_mae_pa_kernel(tc, x_bytes, x_scale, eps, W11, b11, W31, b31, W32, b32, 
                 wg[g, c] = work.tile([P, 1024], F32, name="wg", bufs=5, align_bytes=64)
             return wg[g, c]
 
-        def w_tensor(g, c, b):
+        def w_tensor(g, c, a, b):
             bank = psum.tile([P, 4, P], F32, name="bank")
-            flat = bank[:].rearrange("p a b -> p (a b)")
-            for i in range(2):
-                n0 = 256 * b + P * i
+            flat = bank[:].rearrange("p a b -> p (a b)")[:, : 2 * (b - a)]
+            for n0 in range(a, b, P):
                 nc.tensor.matmul(
-                    out=flat[:, 256 * i : 256 * (i + 1)].bitcast(BF16),
+                    out=flat[:, 2 * (n0 - a) : 2 * (n0 - a + P)].bitcast(BF16),
                     lhsT=ident_bf[:],
-                    rhs=w_raw[g, c][:, :, n0 : n0 + P].rearrange("p j n -> p n j"),
+                    rhs=w_src(g, c, n0, n0 + P).rearrange("p j n -> p n j"),
                     start=True,
                     stop=True,
                 )
             dst = w_tile(g, c)[:].rearrange("p (t m u) -> p t m u", t=4, u=2)
             nc.scalar.copy(
-                out=dst[:, :, 64 * b : 64 * (b + 1), :], in_=flat.rearrange("p (m t u) -> p t m u", t=4, u=2)
+                out=dst[:, :, a // 4 : b // 4, :], in_=flat.rearrange("p (m t u) -> p t m u", t=4, u=2)
             )
 
-        def w_copy(engine_copy, g, c, b):
-            src = w_raw[g, c][:, :, 256 * b : 256 * (b + 1)]
+        def w_copy(engine_copy, g, c, a, b):
             dst = w_tile(g, c)[:].bitcast(BF16).rearrange("p (t m i j) -> p m t j i", t=4, i=2, j=4)
             engine_copy(
-                out=dst[:, 32 * b : 32 * (b + 1), :, :, :],
-                in_=src.rearrange("p j (m i t) -> p m t j i", t=4, i=2),
+                out=dst[:, a // 8 : b // 8, :, :, :],
+                in_=w_src(g, c, a, b).rearrange("p j (m i t) -> p m t j i", t=4, i=2),
             )
 
-        def w_vector(g, c, b):
-            w_copy(nc.vector.tensor_copy, g, c, b)
+        def w_vector(g, c, a, b):
+            w_copy(nc.vector.tensor_copy, g, c, a, b)
 
-        def w_scalar(g, c, b):
-            w_copy(nc.scalar.copy, g, c, b)
+        def w_scalar(g, c, a, b):
+            w_copy(nc.scalar.copy, g, c, a, b)
 
         def w_quant(g, c):
             if g not in w_codes:
@@ -299,84 +309,83 @@ def tile_mae_pa_kernel(tc, x_bytes, x_scale, eps, W11, b11, W31, b31, W32, b32, 
 
         spread_scale(0)
         spread_scale(1)
-        w_tensor(0, 0, 0)
-        w_tensor(0, 0, 1)
+        w_vector(0, 0, 0, 256)
+        w_tensor(0, 0, 256, 512)
         x_product(0, 0, 512)
         x_product(0, 512, IMAGE)
         x_product(1)
         x_turn(0)
         x_product(2)
         x_turn(1)
-        w_tensor(0, 1, 0)
+        w_tensor(0, 1, 0, 256)
         x_product(3)
         x_turn(2)
-        w_tensor(0, 1, 1)
         x_turn(3)
+        w_scalar(0, 1, 256, 512)
         w_quant(0, 0)
         x_product(4)
-        w_quant(0, 1)
         x_quant(0, 0)
         x_quant(0, 1)
+        w_quant(0, 1)
+        w_tensor(1, 0, 0, 256)
+        w_tensor(1, 0, 256, 512)
+        w_tensor(1, 1, 0, 256)
+        w_scalar(1, 1, 256, 512)
         x_product(5)
-        for c in range(2):
-            w_tensor(1, c, 0)
-            w_tensor(1, c, 1)
-        x_turn(4)
+        x_product(6)
+        x_product(7)
 
         first_stage(0, {
-            0: [lambda: x_turn(5)], 1: [lambda: w_tensor(2, 0, 0), lambda: w_tensor(2, 0, 1)],
-            2: [lambda: w_tensor(2, 1, 0)], 3: [lambda: w_tensor(2, 1, 1)],
+            0: [lambda: x_turn(4), lambda: x_turn(5)],
+            1: [lambda: x_turn(6), lambda: x_turn(7)],
+            2: [lambda: w_tensor(2, 0, 0, 256)],
         })
         w_quant(1, 0)
-        x_product(6)
         w_quant(1, 1)
-        x_product(7)
+        w_vector(2, 0, 256, 512)
         w3_lay(0)
+        x_quant(1, 0)
+        x_quant(1, 1)
+        w3_quant(0)
 
         last = len(UNITS) - 1
         for s in range(1, last + 1):
-            pg, pc = (s + 5) // 2, (s + 1) % 2
+            pg, pc = (s + 4) // 2, s % 2
+            n_pe, n_s = CUTS[pc]
             between = {}
             if pg < GROUPS:
-                between[0] = [lambda: w_tensor(pg, pc, 0)]
-                if pc == 0:
-                    between[2] = [lambda: w_tensor(pg, pc, 1)]
-            if s == 1:
-                between[1] = [lambda: x_turn(6), lambda: x_turn(7)]
+                if n_pe:
+                    between[0] = [lambda: w_tensor(pg, pc, 0, n_pe)]
+                between[1] = [lambda: w_scalar(pg, pc, n_pe, n_pe + n_s)]
             if s >= 2:
-                between.setdefault(1, []).append(lambda: second_stage(s - 2))
+                between.setdefault(S2AT if s < 14 else 1, []).insert(0, lambda: second_stage(s - 2))
             first_stage(s, between)
-            if s == last - 1:
+            if s == last:
                 relu_out(0)
                 relu_out(1)
-            qg, qc = (s + 4) // 2, s % 2
-            g3 = s if s < 3 else ((s + 3) // 2 if s % 2 else GROUPS)
-            if s == 1:
-                w_quant(2, 0)
-                w3_quant(0)
+            qg, qc = (s + 3) // 2, (s + 1) % 2
             if qg < GROUPS:
                 w_quant(qg, qc)
             enc_lay(s - 1)
-            if s == 2:
-                x_quant(1, 0)
-                x_quant(1, 1)
-            if pg < GROUPS and pc == 1:
-                w_vector(pg, pc, 1)
-            if g3 < GROUPS:
-                w3_lay(g3)
-            if s == 14:
-                add_bias(0)
+            if pg < GROUPS:
+                w_vector(pg, pc, n_pe + n_s, 512)
+            if s < 14 and s % 2 == 0:
+                w3_lay((s + 2) // 2)
+            if s == 1:
+                w3_lay(1)
             if s == 15:
+                add_bias(0)
+            if s == 16:
                 z_noise(0)
                 z_noise(1)
-            if s == 16:
+            if s == 17:
                 z_out(1)
             enc_quant(s - 1)
-            if g3 < GROUPS:
-                w3_quant(g3)
-            if s == 14:
-                add_bias(1)
+            if s < 15 and s % 2 == 1:
+                w3_quant((s + 1) // 2)
             if s == 15:
+                add_bias(1)
+            if s == 16:
                 z_out(0)
 
         add_bias(2)

@@ -24,9 +24,17 @@ FLOPS = 2 * TOKENS * IMAGE * HIDDEN + 2 * TOKENS * HIDDEN * 2 * LATENT
 GROUPS = 8
 HALF = 512
 ROWS = TOKENS // P
+ENC_BUFS = 3
 W_BUFS = {1: 4, 2: 6}
-CUTS = ((256,128),(128,128))
-S2AT = 2
+CUTS = ((256, 128), (0, 256))
+S2AT = 3
+S2T = 3
+H0 = 0
+SH = (128, 64)
+W37 = 0
+RL = 17
+RT = 1
+LS = 128
 LAG = 1
 
 SPLIT = 2
@@ -52,16 +60,15 @@ def tile_mae_pa_kernel(tc, x_bytes, x_scale, eps, W11, b11, W31, b31, W32, b32, 
         scale_cols = keep.tile([P, 2, 4], F32, name="scale_cols")
         nc.sync.dma_start(out=scale_cols[:], in_=x_scale.rearrange("o (c p t) -> p (o c) t", p=P, t=4))
 
-        xq = [keep.tile([P, IMAGE], U8, name=f"xq{r}") for r in range(2)]
-        xq_rest = [keep.tile([P, 2 * IMAGE], U8, name="xq23"), keep.tile([P, 4 * IMAGE], U8, name="xq47")]
+        xq = [keep.tile([P, IMAGE], U8, name=f"xq{r}") for r in range(4)]
+        xq_rest = keep.tile([P, 4 * IMAGE], U8, name="xq47")
         x_view = x_bytes.rearrange("(p r) k -> p (r k)", r=ROWS)
 
         def x_row(r):
-            if r < 2:
-                return xq[r][:]
-            if r < 4:
-                return xq_rest[0][:, (r - 2) * IMAGE : (r - 1) * IMAGE]
-            return xq_rest[1][:, (r - 4) * IMAGE : (r - 3) * IMAGE]
+            return xq[r][:] if r < 4 else xq_rest[:, (r - 4) * IMAGE : (r - 3) * IMAGE]
+
+        def load_x(r):
+            nc.sync.dma_start(out=xq[r][:], in_=x_view[:, r * IMAGE : (r + 1) * IMAGE])
 
         w_raw = {}
         w_view = W11.rearrange("(c p j) n -> c p j n", c=2, j=4)
@@ -94,22 +101,24 @@ def tile_mae_pa_kernel(tc, x_bytes, x_scale, eps, W11, b11, W31, b31, W32, b32, 
                 w3_raw[g] = tile[:, :, g - a, :]
 
         load_first(0, 256)
-        nc.sync.dma_start(out=xq[0][:], in_=x_view[:, :IMAGE])
+        load_x(0)
         load_first(256, 512)
-        nc.sync.dma_start(out=xq[1][:], in_=x_view[:, IMAGE : 2 * IMAGE])
-        nc.sync.dma_start(out=xq_rest[0][:], in_=x_view[:, 2 * IMAGE : 4 * IMAGE])
+        load_x(1)
         load_w(0, 1, 1)
+        load_x(2)
+        load_x(3)
         load_w(1, 0, 1)
-        nc.sync.dma_start(out=xq_rest[1][:], in_=x_view[:, 4 * IMAGE :])
+        nc.sync.dma_start(out=xq_rest[:], in_=x_view[:, 4 * IMAGE :])
         load_w(1, 1, 1)
         bias = keep.tile([P, GROUPS, 4], BF16, name="bias")
         nc.sync.dma_start(out=bias[:], in_=b11.rearrange("(g p t) -> p g t", p=P, t=4))
         load_w(2, 0, 2)
         load_w3(0, 2)
         load_w(2, 1, 2)
+        load_w3(2, 4)
         load_w(4, 0, 2)
         load_w(4, 1, 2)
-        load_w3(2, 8)
+        load_w3(4, 8)
         load_w(6, 0, 2)
         load_w(6, 1, 2)
         bias3 = keep.tile([P, 2 * LATENT], BF16, name="bias3")
@@ -178,10 +187,11 @@ def tile_mae_pa_kernel(tc, x_bytes, x_scale, eps, W11, b11, W31, b31, W32, b32, 
             bank = psum.tile([P, 4, P], F32, name="bank")
             flat = bank[:].rearrange("p a b -> p (a b)")[:, : 2 * (b - a)]
             for n0 in range(a, b, P):
+                n1 = min(b, n0 + P)
                 nc.tensor.matmul(
-                    out=flat[:, 2 * (n0 - a) : 2 * (n0 - a + P)].bitcast(BF16),
+                    out=flat[:, 2 * (n0 - a) : 2 * (n1 - a)].bitcast(BF16),
                     lhsT=ident_bf[:],
-                    rhs=w_src(g, c, n0, n0 + P).rearrange("p j n -> p n j"),
+                    rhs=w_src(g, c, n0, n1).rearrange("p j n -> p n j"),
                     start=True,
                     stop=True,
                 )
@@ -215,9 +225,9 @@ def tile_mae_pa_kernel(tc, x_bytes, x_scale, eps, W11, b11, W31, b31, W32, b32, 
         w3_codes = keep.tile([P, GROUPS, 2 * LATENT], U32, name="w3_codes", align_bytes=64)
         w3_planes = keep.tile([P, GROUPS, 2 * LATENT], U8, name="w3_planes", align_bytes=64)
 
-        def w3_lay(g):
+        def w3_lay(g, engine_copy=nc.vector.tensor_copy):
             w3g[g] = work.tile([P, 1024], BF16, name="w3g", bufs=2, align_bytes=64)
-            nc.vector.tensor_copy(
+            engine_copy(
                 out=w3g[g][:].rearrange("p (w c i j) -> p w c j i", w=2, i=4, j=4),
                 in_=w3_raw[g].rearrange("p w (j c i) -> p w c j i", j=4, i=4),
             )
@@ -250,23 +260,27 @@ def tile_mae_pa_kernel(tc, x_bytes, x_scale, eps, W11, b11, W31, b31, W32, b32, 
                 for job in between.get(t, []):
                     job()
 
-        def enc_lay(s):
-            encg[s] = work.tile([P, 4 * P * UNITS[s][3]], BF16, name="encg", bufs=2, align_bytes=64)
-            nc.vector.tensor_copy(
-                out=encg[s][:].rearrange("p (c i t) -> p c t i", i=4, t=4),
-                in_=enc[s][:].rearrange("p t (c i) -> p c t i", i=4),
+        def enc_lay(s, a, b, engine_copy=nc.vector.tensor_copy):
+            if s not in encg:
+                encg[s] = work.tile([P, 4 * P * UNITS[s][3]], BF16, name="encg", bufs=3, align_bytes=64)
+            engine_copy(
+                out=encg[s][:, 4 * a : 4 * b].rearrange("p (c i t) -> p c t i", i=4, t=4),
+                in_=enc[s][:, :, a:b].rearrange("p t (c i) -> p c t i", i=4),
             )
 
-        def enc_quant(s):
-            enc_codes[s] = work.tile([P, P * UNITS[s][3]], U32, name="enc_codes", bufs=3, align_bytes=64)
-            enc_planes[s] = work.tile([P, P * UNITS[s][3]], U8, name="enc_planes", bufs=3, align_bytes=64)
-            nc.vector.quantize_mx(out=enc_codes[s][:].bitcast(FP8X4), scales=enc_planes[s][:], in_=encg[s][:])
+        def enc_quant(s, a, b):
+            if s not in enc_codes:
+                enc_codes[s] = work.tile([P, P * UNITS[s][3]], U32, name="enc_codes", bufs=ENC_BUFS, align_bytes=64)
+                enc_planes[s] = work.tile([P, P * UNITS[s][3]], U8, name="enc_planes", bufs=ENC_BUFS, align_bytes=64)
+            nc.vector.quantize_mx(
+                out=enc_codes[s][:, a:b].bitcast(FP8X4), scales=enc_planes[s][:, a:b], in_=encg[s][:, 4 * a : 4 * b]
+            )
 
         acc = [accs.tile([P, 2, 2 * LATENT], F32, name=f"acc{i}") for i in range(4)]
 
-        def second_stage(s):
+        def second_stage(s, only=None):
             h, g, r0, rows = UNITS[s]
-            for r in range(rows):
+            for r in range(rows) if only is None else [only]:
                 nc.tensor.matmul_mx(
                     out=acc[2 * h + (r0 + r) // 2][:, r % 2, :],
                     lhsT=enc_codes[s][:, P * r : P * (r + 1)].bitcast(FP8X4),
@@ -280,32 +294,36 @@ def tile_mae_pa_kernel(tc, x_bytes, x_scale, eps, W11, b11, W31, b31, W32, b32, 
         y, z, relus = {}, {}, {}
         views = [o.rearrange("(p r) l -> p r l", r=ROWS) for o in (out_0, out_1, out_2)]
 
-        def add_bias(i):
-            y[i] = work.tile([P, 2, 2 * LATENT], F32, name="y", bufs=4)
+        def add_bias(i, a=0, b=2):
+            if i not in y:
+                y[i] = work.tile([P, 2, 2 * LATENT], F32, name="y", bufs=3)
             nc.vector.tensor_tensor(
-                out=y[i][:], in0=acc[i][:], in1=bias3[:].unsqueeze(1).to_broadcast([P, 2, 2 * LATENT]), op=ADD
+                out=y[i][:, a:b, :], in0=acc[i][:, a:b, :],
+                in1=bias3[:].unsqueeze(1).to_broadcast([P, b - a, 2 * LATENT]), op=ADD,
             )
 
         def relu_out(i):
-            relus[i] = work.tile([P, 2, 2, LATENT], F32, name="relu", bufs=4)
+            relus[i] = work.tile([P, 2, 2, LATENT], F32, name="relu", bufs=3)
             nc.scalar.activation(
                 out=relus[i][:], in_=y[i][:].rearrange("p r (w l) -> p w r l", w=2), func=RELU
             )
             for w in range(2):
                 nc.sync.dma_start(out=views[w][:, 2 * i : 2 * i + 2, :], in_=relus[i][:, w, :, :])
 
-        def z_noise(i):
-            z[i] = work.tile([P, 2, LATENT], F32, name="z", bufs=4)
+        def z_noise(i, a=0, b=2):
+            if i not in z:
+                z[i] = work.tile([P, 2, LATENT], F32, name="z", bufs=4)
             nc.vector.scalar_tensor_tensor(
-                out=z[i][:], in0=y[i][:, :, LATENT:], scalar=0.0,
-                in1=eps_sb[:, 2 * i : 2 * i + 2, :], op0=MAX, op1=MULT,
+                out=z[i][:, a:b, :], in0=y[i][:, a:b, LATENT:], scalar=0.0,
+                in1=eps_sb[:, 2 * i + a : 2 * i + b, :], op0=MAX, op1=MULT,
             )
 
-        def z_out(i):
+        def z_out(i, a=0, b=2):
             nc.vector.scalar_tensor_tensor(
-                out=z[i][:], in0=y[i][:, :, :LATENT], scalar=0.0, in1=z[i][:], op0=MAX, op1=ADD,
+                out=z[i][:, a:b, :], in0=y[i][:, a:b, :LATENT], scalar=0.0, in1=z[i][:, a:b, :], op0=MAX, op1=ADD,
             )
-            nc.sync.dma_start(out=views[2][:, 2 * i : 2 * i + 2, :], in_=z[i][:])
+            if b == 2:
+                nc.sync.dma_start(out=views[2][:, 2 * i : 2 * i + 2, :], in_=z[i][:])
 
         spread_scale(0)
         spread_scale(1)
@@ -315,22 +333,22 @@ def tile_mae_pa_kernel(tc, x_bytes, x_scale, eps, W11, b11, W31, b31, W32, b32, 
         x_product(0, 512, IMAGE)
         x_product(1)
         x_turn(0)
+        w_scalar(0, 1, 256, 512)
         x_product(2)
-        x_turn(1)
         w_tensor(0, 1, 0, 256)
+        x_turn(1)
         x_product(3)
         x_turn(2)
         x_turn(3)
-        w_scalar(0, 1, 256, 512)
         w_quant(0, 0)
+        w_quant(0, 1)
         x_product(4)
         x_quant(0, 0)
         x_quant(0, 1)
-        w_quant(0, 1)
         w_tensor(1, 0, 0, 256)
-        w_tensor(1, 0, 256, 512)
+        w_scalar(1, 0, 256, 512)
         w_tensor(1, 1, 0, 256)
-        w_scalar(1, 1, 256, 512)
+        w_tensor(1, 1, 256, 512)
         x_product(5)
         x_product(6)
         x_product(7)
@@ -339,10 +357,11 @@ def tile_mae_pa_kernel(tc, x_bytes, x_scale, eps, W11, b11, W31, b31, W32, b32, 
             0: [lambda: x_turn(4), lambda: x_turn(5)],
             1: [lambda: x_turn(6), lambda: x_turn(7)],
             2: [lambda: w_tensor(2, 0, 0, 256)],
+            3: [lambda: w_scalar(2, 0, 256, 256 + H0)] if H0 else [],
         })
         w_quant(1, 0)
         w_quant(1, 1)
-        w_vector(2, 0, 256, 512)
+        w_vector(2, 0, 256 + H0, 512)
         w3_lay(0)
         x_quant(1, 0)
         x_quant(1, 1)
@@ -352,24 +371,30 @@ def tile_mae_pa_kernel(tc, x_bytes, x_scale, eps, W11, b11, W31, b31, W32, b32, 
         for s in range(1, last + 1):
             pg, pc = (s + 4) // 2, s % 2
             n_pe, n_s = CUTS[pc]
-            between = {}
+            width = P * UNITS[s - 1][3]
+            share = SH[0] if s == 14 else (SH[1] if s > 14 else 0)
+            between = {t: [] for t in range(4)}
             if pg < GROUPS:
                 if n_pe:
-                    between[0] = [lambda: w_tensor(pg, pc, 0, n_pe)]
-                between[1] = [lambda: w_scalar(pg, pc, n_pe, n_pe + n_s)]
+                    between[0].append(lambda: w_tensor(pg, pc, 0, n_pe))
+                if n_s:
+                    between[1].append(lambda: w_scalar(pg, pc, n_pe, n_pe + n_s))
             if s >= 2:
-                between.setdefault(S2AT if s < 14 else 1, []).insert(0, lambda: second_stage(s - 2))
+                between[S2AT if s < 14 else S2T].insert(0, lambda: second_stage(s - 2))
+            if share:
+                between[0].append(lambda: enc_lay(s - 1, 0, share, nc.scalar.copy))
+            if s == W37:
+                between[1].append(lambda: w3_lay(GROUPS - 1, nc.scalar.copy))
+            if s >= RL:
+                between[RT].append(lambda: relu_out(s - RL))
             first_stage(s, between)
-            if s == last:
-                relu_out(0)
-                relu_out(1)
             qg, qc = (s + 3) // 2, (s + 1) % 2
             if qg < GROUPS:
                 w_quant(qg, qc)
-            enc_lay(s - 1)
+            enc_lay(s - 1, share, width)
             if pg < GROUPS:
                 w_vector(pg, pc, n_pe + n_s, 512)
-            if s < 14 and s % 2 == 0:
+            if s < (12 if W37 else 14) and s % 2 == 0:
                 w3_lay((s + 2) // 2)
             if s == 1:
                 w3_lay(1)
@@ -380,23 +405,31 @@ def tile_mae_pa_kernel(tc, x_bytes, x_scale, eps, W11, b11, W31, b31, W32, b32, 
                 z_noise(1)
             if s == 17:
                 z_out(1)
-            enc_quant(s - 1)
-            if s < 15 and s % 2 == 1:
+            if s == max(W37, 13):
+                w3_quant(GROUPS - 1)
+            enc_quant(s - 1, 0, width)
+            if s < 13 and s % 2 == 1:
                 w3_quant((s + 1) // 2)
             if s == 15:
                 add_bias(1)
             if s == 16:
                 z_out(0)
 
+        enc_lay(last, 2 * P - LS, 2 * P, nc.scalar.copy)
         add_bias(2)
         second_stage(last - 1)
-        relu_out(2)
-        enc_lay(last)
+        for i in range(last + 1 - RL, 3):
+            relu_out(i)
+        enc_lay(last, 0, 2 * P - LS)
         z_noise(2)
-        enc_quant(last)
-        z_out(2)
+        enc_quant(last, 0, P)
+        enc_quant(last, P, 2 * P)
         second_stage(last)
-        add_bias(3)
+        z_out(2)
+        for r in range(2):
+            add_bias(3, r, r + 1)
         relu_out(3)
-        z_noise(3)
-        z_out(3)
+        for r in range(2):
+            z_noise(3, r, r + 1)
+        for r in range(2):
+            z_out(3, r, r + 1)

@@ -25,8 +25,8 @@ GROUPS = 8
 HALF = 512
 ROWS = TOKENS // P
 ENC_BUFS = 3
-W_BUFS = {1: 4, 2: 6}
-CUTS = ((256, 128), (0, 256))
+W_BUFS = 6
+CUTS = ((256, 64), (0, 256))
 S2AT = 3
 S2T = 3
 H0 = 0
@@ -52,6 +52,8 @@ def tile_mae_pa_kernel(tc, x_bytes, x_scale, eps, W11, b11, W31, b31, W32, b32, 
         psum = ctx.enter_context(tc.psum_pool(name="psum", bufs=4))
         accs = ctx.enter_context(tc.psum_pool(name="accs", bufs=1))
 
+        zeros = keep.tile([P, 256], F32, name="zeros")
+        nc.vector.memset(zeros[:], 0.0)
         ident = keep.tile([P, P], F32, name="ident")
         make_identity(nc, ident[:])
         ctx.enter_context(tc.manual_schedule())
@@ -70,27 +72,21 @@ def tile_mae_pa_kernel(tc, x_bytes, x_scale, eps, W11, b11, W31, b31, W32, b32, 
         def load_x(r):
             nc.sync.dma_start(out=xq[r][:], in_=x_view[:, r * IMAGE : (r + 1) * IMAGE])
 
-        w_raw = {}
+        w_raw = {0: [], 1: []}
         w_view = W11.rearrange("(c p j) n -> c p j n", c=2, j=4)
 
-        def load_w(g, c, n):
-            tile = work.tile([P, 4, 512 * n], BF16, name=f"w_raw{n}", bufs=W_BUFS[n])
-            nc.sync.dma_start(out=tile[:], in_=w_view[c, :, :, 512 * g : 512 * (g + n)])
-            for i in range(n):
-                w_raw[g + i, c] = tile[:, :, 512 * i : 512 * (i + 1)]
-
-        def load_first(a, b):
-            tile = keep.tile([P, 4, b - a], BF16, name=f"w_first{a}")
-            nc.sync.dma_start(out=tile[:], in_=w_view[0, :, :, a:b])
-            w_first[a] = tile
+        def load_w(c, a, b, kept=False):
+            pool, bufs = (keep, 1) if kept else (work, W_BUFS)
+            tile = pool.tile([P, 4, b - a], BF16, name=f"w_raw{c}_{a}" if kept else "w_raw", bufs=bufs)
+            nc.sync.dma_start(out=tile[:], in_=w_view[c, :, :, a:b])
+            w_raw[c].append((a, b, tile))
 
         def w_src(g, c, a, b):
-            if (g, c) == (0, 0):
-                a0 = max(k for k in w_first if k <= a)
-                return w_first[a0][:, :, a - a0 : b - a0]
-            return w_raw[g, c][:, :, a:b]
+            a, b = 512 * g + a, 512 * g + b
+            a0, tile = [(lo, tile) for lo, hi, tile in w_raw[c] if lo <= a and b <= hi][0]
+            return tile[:, :, a - a0 : b - a0]
 
-        w3_raw, w_first = {}, {}
+        w3_raw = {}
         w3_view = [w.rearrange("(g p j) l -> p g (j l)", p=P, j=4) for w in (W31, W32)]
 
         def load_w3(a, b):
@@ -100,27 +96,27 @@ def tile_mae_pa_kernel(tc, x_bytes, x_scale, eps, W11, b11, W31, b31, W32, b32, 
             for g in range(a, b):
                 w3_raw[g] = tile[:, :, g - a, :]
 
-        load_first(0, 256)
+        load_w(0, 0, 256, True)
         load_x(0)
-        load_first(256, 512)
+        load_w(0, 256, 512, True)
         load_x(1)
-        load_w(0, 1, 1)
+        load_w(1, 0, 512, True)
         load_x(2)
         load_x(3)
-        load_w(1, 0, 1)
+        load_w(0, 512, 1024, True)
         nc.sync.dma_start(out=xq_rest[:], in_=x_view[:, 4 * IMAGE :])
-        load_w(1, 1, 1)
+        load_w(1, 512, 1024, True)
         bias = keep.tile([P, GROUPS, 4], BF16, name="bias")
         nc.sync.dma_start(out=bias[:], in_=b11.rearrange("(g p t) -> p g t", p=P, t=4))
-        load_w(2, 0, 2)
+        load_w(0, 1024, 2048)
         load_w3(0, 2)
-        load_w(2, 1, 2)
+        load_w(1, 1024, 2048)
         load_w3(2, 4)
-        load_w(4, 0, 2)
-        load_w(4, 1, 2)
+        load_w(0, 2048, 3072)
+        load_w(1, 2048, 3072)
         load_w3(4, 8)
-        load_w(6, 0, 2)
-        load_w(6, 1, 2)
+        load_w(0, 3072, 4096)
+        load_w(1, 3072, 4096)
         bias3 = keep.tile([P, 2 * LATENT], BF16, name="bias3")
         nc.sync.dma_start(out=bias3[:, :LATENT], in_=b31.partition_broadcast(P))
         nc.sync.dma_start(out=bias3[:, LATENT:], in_=b32.partition_broadcast(P))
@@ -129,6 +125,12 @@ def tile_mae_pa_kernel(tc, x_bytes, x_scale, eps, W11, b11, W31, b31, W32, b32, 
 
         ident_bf = keep.tile([P, P], BF16, name="ident_bf")
         nc.scalar.activation(out=ident_bf[:], in_=ident[:], func=COPY)
+
+        idle = accs.tile([P, 512], F32, name="acc0")
+
+        def warm_up(n):
+            for i in range(n):
+                nc.tensor.matmul(out=idle[:, :256], lhsT=zeros[:, :P], rhs=zeros[:], start=True, stop=True)
 
         scale = keep.tile([P, IMAGE], F32, name="scale")
 
@@ -276,11 +278,14 @@ def tile_mae_pa_kernel(tc, x_bytes, x_scale, eps, W11, b11, W31, b31, W32, b32, 
                 out=enc_codes[s][:, a:b].bitcast(FP8X4), scales=enc_planes[s][:, a:b], in_=encg[s][:, 4 * a : 4 * b]
             )
 
-        acc = [accs.tile([P, 2, 2 * LATENT], F32, name=f"acc{i}") for i in range(4)]
+        acc = {}
 
         def second_stage(s, only=None):
             h, g, r0, rows = UNITS[s]
             for r in range(rows) if only is None else [only]:
+                if 2 * h + (r0 + r) // 2 not in acc:
+                    i = 2 * h + (r0 + r) // 2
+                    acc[i] = accs.tile([P, 2, 2 * LATENT], F32, name=f"acc{i}")
                 nc.tensor.matmul_mx(
                     out=acc[2 * h + (r0 + r) // 2][:, r % 2, :],
                     lhsT=enc_codes[s][:, P * r : P * (r + 1)].bitcast(FP8X4),
@@ -325,24 +330,27 @@ def tile_mae_pa_kernel(tc, x_bytes, x_scale, eps, W11, b11, W31, b31, W32, b32, 
             if b == 2:
                 nc.sync.dma_start(out=views[2][:, 2 * i : 2 * i + 2, :], in_=z[i][:])
 
+        warm_up(2)
         spread_scale(0)
         spread_scale(1)
+        warm_up(1)
         w_vector(0, 0, 0, 256)
         w_tensor(0, 0, 256, 512)
         x_product(0, 0, 512)
         x_product(0, 512, IMAGE)
         x_product(1)
         x_turn(0)
-        w_scalar(0, 1, 256, 512)
-        x_product(2)
         w_tensor(0, 1, 0, 256)
+        x_product(2)
         x_turn(1)
+        warm_up(1)
+        w_scalar(0, 1, 256, 512)
         x_product(3)
         x_turn(2)
         x_turn(3)
         w_quant(0, 0)
-        w_quant(0, 1)
         x_product(4)
+        w_quant(0, 1)
         x_quant(0, 0)
         x_quant(0, 1)
         w_tensor(1, 0, 0, 256)

@@ -35,6 +35,7 @@ W37 = 0
 RL = 17
 RT = 1
 LS = 128
+MM_ROWS = (0, 1, 2, 3)
 LAG = 1
 
 SPLIT = 2
@@ -52,10 +53,17 @@ def tile_mae_pa_kernel(tc, x_bytes, x_scale, eps, W11, b11, W31, b31, W32, b32, 
         psum = ctx.enter_context(tc.psum_pool(name="psum", bufs=4))
         accs = ctx.enter_context(tc.psum_pool(name="accs", bufs=1))
 
-        zeros = keep.tile([P, 256], F32, name="zeros")
-        nc.vector.memset(zeros[:], 0.0)
+        zeros = keep.tile([P, 384], F32, name="zeros")
+        nc.gpsimd.memset(zeros[:], 0.0)
         ident = keep.tile([P, P], F32, name="ident")
         make_identity(nc, ident[:])
+        spread = keep.tile([P, 2, 2 * P], BF16, name="spread")
+        nc.gpsimd.memset(spread[:], 0.0)
+        for e in range(2):
+            nc.gpsimd.affine_select(
+                out=spread[:, e, :], in_=spread[:, e, :], compare_op=mybir.AluOpType.not_equal, fill=1.0,
+                base=e, pattern=[[-1, 2 * P]], channel_multiplier=2,
+            )
         ctx.enter_context(tc.manual_schedule())
         ctx.enter_context(nc.allow_non_contiguous_dma(reason="runs of four scales and of four biases"))
 
@@ -100,12 +108,12 @@ def tile_mae_pa_kernel(tc, x_bytes, x_scale, eps, W11, b11, W31, b31, W32, b32, 
         load_x(0)
         load_w(0, 256, 512, True)
         load_x(1)
-        load_w(1, 0, 512, True)
         load_x(2)
+        load_w(1, 0, 512, True)
         load_x(3)
         load_w(0, 512, 1024, True)
-        nc.sync.dma_start(out=xq_rest[:], in_=x_view[:, 4 * IMAGE :])
         load_w(1, 512, 1024, True)
+        nc.sync.dma_start(out=xq_rest[:], in_=x_view[:, 4 * IMAGE :])
         bias = keep.tile([P, GROUPS, 4], BF16, name="bias")
         nc.sync.dma_start(out=bias[:], in_=b11.rearrange("(g p t) -> p g t", p=P, t=4))
         load_w(0, 1024, 2048)
@@ -128,9 +136,8 @@ def tile_mae_pa_kernel(tc, x_bytes, x_scale, eps, W11, b11, W31, b31, W32, b32, 
 
         idle = accs.tile([P, 512], F32, name="acc0")
 
-        def warm_up(n):
-            for i in range(n):
-                nc.tensor.matmul(out=idle[:, :256], lhsT=zeros[:, :P], rhs=zeros[:], start=True, stop=True)
+        def warm_up(n, bank=idle):
+            nc.tensor.matmul(out=bank[:, :n], lhsT=zeros[:, :P], rhs=zeros[:, :n], start=True, stop=True)
 
         scale = keep.tile([P, IMAGE], F32, name="scale")
 
@@ -154,21 +161,37 @@ def tile_mae_pa_kernel(tc, x_bytes, x_scale, eps, W11, b11, W31, b31, W32, b32, 
                 out=xb[r][:, a:b], in0=x_row(r)[:, a:b].bitcast(FP8), in1=scale[:, a:b], op=MULT
             )
 
-        def x_turn(r):
-            h = r // 4
-            bank = psum.tile([P, 4, P], F32, name="bank")
-            words = xb[r][:].bitcast(F32)
-            for c in range(2):
-                for u in range(2):
-                    nc.tensor.transpose(
-                        bank[:, 2 * c + u, :], words[:, 256 * c + u : 256 * (c + 1) : 2], ident[:]
-                    )
+        def x_tile(h):
             if h not in xg:
                 xg[h] = work.tile([P, 2, 2 * HALF], F32, name="xg", bufs=2, align_bytes=64)
-            dst = xg[h][:].rearrange("p c (n u) -> p c n u", u=2)
+            return xg[h]
+
+        def x_turn(r):
+            if r in MM_ROWS:
+                pairs = psum.tile([P, 4, 2 * P], BF16, name="bank")
+                for c in range(2):
+                    for t in range(4):
+                        nc.tensor.matmul(
+                            out=pairs[:, 2 * c + t // 2, :],
+                            lhsT=xb[r][:, 512 * c + t : 512 * (c + 1) : 4],
+                            rhs=spread[:, t % 2, :],
+                            start=(t % 2 == 0),
+                            stop=(t % 2 == 1),
+                        )
+                turned = pairs[:].bitcast(F32)
+            else:
+                bank = psum.tile([P, 4, P], F32, name="bank")
+                words = xb[r][:].bitcast(F32)
+                for c in range(2):
+                    for u in range(2):
+                        nc.tensor.transpose(
+                            bank[:, 2 * c + u, :], words[:, 256 * c + u : 256 * (c + 1) : 2], ident[:]
+                        )
+                turned = bank[:]
+            dst = x_tile(r // 4)[:].rearrange("p c (n u) -> p c n u", u=2)
             nc.scalar.copy(
                 out=dst[:, :, P * (r % 4) : P * (r % 4 + 1), :],
-                in_=bank[:].rearrange("p (c u) n -> p c n u", u=2),
+                in_=turned.rearrange("p (c u) n -> p c n u", u=2),
             )
 
         def x_quant(h, c):
@@ -330,50 +353,45 @@ def tile_mae_pa_kernel(tc, x_bytes, x_scale, eps, W11, b11, W31, b31, W32, b32, 
             if b == 2:
                 nc.sync.dma_start(out=views[2][:, 2 * i : 2 * i + 2, :], in_=z[i][:])
 
-        warm_up(2)
+        warm_up(256)
+        warm_up(256)
         spread_scale(0)
         spread_scale(1)
-        warm_up(1)
+        warm_up(384)
         w_vector(0, 0, 0, 256)
-        w_tensor(0, 0, 256, 512)
+        w_scalar(0, 0, 256, 512)
         x_product(0, 0, 512)
         x_product(0, 512, IMAGE)
         x_product(1)
         x_turn(0)
-        w_tensor(0, 1, 0, 256)
+        w_scalar(0, 1, 0, 384)
         x_product(2)
         x_turn(1)
-        warm_up(1)
-        w_scalar(0, 1, 256, 512)
         x_product(3)
         x_turn(2)
         x_turn(3)
+        w_vector(0, 1, 384, 512)
         w_quant(0, 0)
-        x_product(4)
+        w_vector(1, 0, 384, 512)
         w_quant(0, 1)
         x_quant(0, 0)
         x_quant(0, 1)
         w_tensor(1, 0, 0, 256)
-        w_scalar(1, 0, 256, 512)
+        w_scalar(1, 0, 256, 384)
         w_tensor(1, 1, 0, 256)
         w_tensor(1, 1, 256, 512)
+        x_product(4)
         x_product(5)
         x_product(6)
         x_product(7)
-
-        first_stage(0, {
-            0: [lambda: x_turn(4), lambda: x_turn(5)],
-            1: [lambda: x_turn(6), lambda: x_turn(7)],
-            2: [lambda: w_tensor(2, 0, 0, 256)],
-            3: [lambda: w_scalar(2, 0, 256, 256 + H0)] if H0 else [],
-        })
+        first_stage(0, {t: [lambda t=t: x_turn(4 + t)] + ([lambda: w_scalar(2, 0, 256, 512)] if t == 3 else []) for t in range(4)})
         w_quant(1, 0)
         w_quant(1, 1)
-        w_vector(2, 0, 256 + H0, 512)
         w3_lay(0)
+        w3_lay(1)
+        w3_quant(0)
         x_quant(1, 0)
         x_quant(1, 1)
-        w3_quant(0)
 
         last = len(UNITS) - 1
         for s in range(1, last + 1):
@@ -387,6 +405,8 @@ def tile_mae_pa_kernel(tc, x_bytes, x_scale, eps, W11, b11, W31, b31, W32, b32, 
                     between[0].append(lambda: w_tensor(pg, pc, 0, n_pe))
                 if n_s:
                     between[1].append(lambda: w_scalar(pg, pc, n_pe, n_pe + n_s))
+            if s == 1:
+                between[0].append(lambda: w_tensor(2, 0, 0, 256))
             if s >= 2:
                 between[S2AT if s < 14 else S2T].insert(0, lambda: second_stage(s - 2))
             if share:
@@ -397,7 +417,7 @@ def tile_mae_pa_kernel(tc, x_bytes, x_scale, eps, W11, b11, W31, b31, W32, b32, 
                 between[RT].append(lambda: relu_out(s - RL))
             first_stage(s, between)
             qg, qc = (s + 3) // 2, (s + 1) % 2
-            if qg < GROUPS:
+            if qg < GROUPS and s > 1:
                 w_quant(qg, qc)
             enc_lay(s - 1, share, width)
             if pg < GROUPS:
@@ -405,7 +425,7 @@ def tile_mae_pa_kernel(tc, x_bytes, x_scale, eps, W11, b11, W31, b31, W32, b32, 
             if s < (12 if W37 else 14) and s % 2 == 0:
                 w3_lay((s + 2) // 2)
             if s == 1:
-                w3_lay(1)
+                w_quant(2, 0)
             if s == 15:
                 add_bias(0)
             if s == 16:
@@ -426,6 +446,7 @@ def tile_mae_pa_kernel(tc, x_bytes, x_scale, eps, W11, b11, W31, b31, W32, b32, 
         enc_lay(last, 2 * P - LS, 2 * P, nc.scalar.copy)
         add_bias(2)
         second_stage(last - 1)
+        warm_up(256, psum.tile([P, 512], F32, name="bank"))
         for i in range(last + 1 - RL, 3):
             relu_out(i)
         enc_lay(last, 0, 2 * P - LS)

@@ -15,34 +15,28 @@ FP8X4 = mybir.dt.float8_e4m3fn_x4
 ADD = mybir.AluOpType.add
 MULT = mybir.AluOpType.mult
 MAX = mybir.AluOpType.max
+NOT_EQUAL = mybir.AluOpType.not_equal
 RELU = mybir.ActivationFunctionType.Relu
 COPY = mybir.ActivationFunctionType.Copy
 
-P = 128
 FLOPS = 2 * TOKENS * IMAGE * HIDDEN + 2 * TOKENS * HIDDEN * 2 * LATENT
 
-GROUPS = 8
-HALF = 512
+P = 128
+PASS = 4 * P
+GROUPS = HIDDEN // PASS
 ROWS = TOKENS // P
-ENC_BUFS = 3
-W_BUFS = 6
-CUTS = ((256, 64), (0, 256))
-S2AT = 3
-S2T = 3
-H0 = 0
-SH = (128, 64)
-W37 = 0
-RL = 17
-RT = 1
-LS = 128
-MM_ROWS = (0, 1, 2, 3)
-LAG = 1
+HALF = TOKENS // 2
+BANK_CHANNELS = 256
 
-SPLIT = 2
+WIDE_UNITS = [(0, 0, 0, 4)] + [(h, g - h, 0, 4) for g in range(1, GROUPS) for h in range(2)][:-1]
+UNITS = WIDE_UNITS + [(1, g, r, 2) for r in (0, 2) for g in (GROUPS - 2, GROUPS - 1)]
+LAST = len(UNITS) - 1
+HALF0_CLOSED = UNITS.index((0, GROUPS - 1, 0, 4)) + 2
 
-UNITS = sorted(
-    [(h, g, 0, 4) for h in range(2) for g in range(GROUPS - SPLIT * h)], key=lambda u: (u[1] + LAG * u[0], u[0])
-) + [(1, g, r, 2) for r in (0, 2) for g in range(GROUPS - SPLIT, GROUPS)]
+SCALAR_CHANNELS = (64, 256)
+SCALAR_CHANNELS_STEP_1 = 384
+SCALAR_TAIL_SHARE = 4
+MATMUL_ROWS = (0, 1, 2, 3, 5)
 
 
 def tile_mae_pa_kernel(tc, x_bytes, x_scale, eps, W11, b11, W31, b31, W32, b32, out_0, out_1, out_2):
@@ -51,80 +45,75 @@ def tile_mae_pa_kernel(tc, x_bytes, x_scale, eps, W11, b11, W31, b31, W32, b32, 
         keep = ctx.enter_context(tc.tile_pool(name="keep", bufs=1))
         work = ctx.enter_context(tc.tile_pool(name="work", bufs=2))
         psum = ctx.enter_context(tc.psum_pool(name="psum", bufs=4))
-        accs = ctx.enter_context(tc.psum_pool(name="accs", bufs=1))
+        sums = ctx.enter_context(tc.psum_pool(name="sums", bufs=1))
 
         zeros = keep.tile([P, 384], F32, name="zeros")
         nc.gpsimd.memset(zeros[:], 0.0)
         ident = keep.tile([P, P], F32, name="ident")
         make_identity(nc, ident[:])
-        spread = keep.tile([P, 2, 2 * P], BF16, name="spread")
-        nc.gpsimd.memset(spread[:], 0.0)
+        wide_ident = keep.tile([P, 2, 2 * P], BF16, name="wide_ident")
+        nc.gpsimd.memset(wide_ident[:], 0.0)
         for e in range(2):
             nc.gpsimd.affine_select(
-                out=spread[:, e, :], in_=spread[:, e, :], compare_op=mybir.AluOpType.not_equal, fill=1.0,
+                out=wide_ident[:, e, :], in_=wide_ident[:, e, :], compare_op=NOT_EQUAL, fill=1.0,
                 base=e, pattern=[[-1, 2 * P]], channel_multiplier=2,
             )
         ctx.enter_context(tc.manual_schedule())
         ctx.enter_context(nc.allow_non_contiguous_dma(reason="runs of four scales and of four biases"))
 
+        x_view = x_bytes.rearrange("(p r) k -> p (r k)", r=ROWS)
+        w11_view = W11.rearrange("(c p j) n -> c p j n", c=2, j=4)
+        w3_views = [w.rearrange("(g p j) l -> p g (j l)", p=P, j=4) for w in (W31, W32)]
+        b11_view = b11.rearrange("(g p t) -> p g t", p=P, t=4)
+        x_raw, w11_raw, w3_raw, bias1 = {}, {0: [], 1: []}, {}, {}
+
+        def load_x(r0, r1):
+            tile = keep.tile([P, (r1 - r0) * IMAGE], U8, name=f"x_raw{r0}")
+            nc.sync.dma_start(out=tile[:], in_=x_view[:, r0 * IMAGE : r1 * IMAGE])
+            for r in range(r0, r1):
+                x_raw[r] = tile[:, (r - r0) * IMAGE : (r - r0 + 1) * IMAGE]
+
+        def load_w11(c, n0, n1):
+            tile = keep.tile([P, 4, n1 - n0], BF16, name=f"w11_raw{c}_{n0}")
+            nc.sync.dma_start(out=tile[:], in_=w11_view[c, :, :, n0:n1])
+            w11_raw[c].append((n0, n1, tile))
+
+        def load_w3(g0, g1):
+            tile = keep.tile([P, 2, g1 - g0, 4 * LATENT], BF16, name=f"w3_raw{g0}")
+            for w in range(2):
+                nc.sync.dma_start(out=tile[:, w, :, :], in_=w3_views[w][:, g0:g1, :])
+            for g in range(g0, g1):
+                w3_raw[g] = tile[:, :, g - g0, :]
+
+        def load_bias1(g0, g1):
+            tile = keep.tile([P, g1 - g0, 4], BF16, name=f"bias1_{g0}")
+            nc.sync.dma_start(out=tile[:], in_=b11_view[:, g0:g1, :])
+            for g in range(g0, g1):
+                bias1[g] = tile[:, g - g0, :]
+
         scale_cols = keep.tile([P, 2, 4], F32, name="scale_cols")
         nc.sync.dma_start(out=scale_cols[:], in_=x_scale.rearrange("o (c p t) -> p (o c) t", p=P, t=4))
-
-        xq = [keep.tile([P, IMAGE], U8, name=f"xq{r}") for r in range(4)]
-        xq_rest = keep.tile([P, 4 * IMAGE], U8, name="xq47")
-        x_view = x_bytes.rearrange("(p r) k -> p (r k)", r=ROWS)
-
-        def x_row(r):
-            return xq[r][:] if r < 4 else xq_rest[:, (r - 4) * IMAGE : (r - 3) * IMAGE]
-
-        def load_x(r):
-            nc.sync.dma_start(out=xq[r][:], in_=x_view[:, r * IMAGE : (r + 1) * IMAGE])
-
-        w_raw = {0: [], 1: []}
-        w_view = W11.rearrange("(c p j) n -> c p j n", c=2, j=4)
-
-        def load_w(c, a, b, kept=False):
-            pool, bufs = (keep, 1) if kept else (work, W_BUFS)
-            tile = pool.tile([P, 4, b - a], BF16, name=f"w_raw{c}_{a}" if kept else "w_raw", bufs=bufs)
-            nc.sync.dma_start(out=tile[:], in_=w_view[c, :, :, a:b])
-            w_raw[c].append((a, b, tile))
-
-        def w_src(g, c, a, b):
-            a, b = 512 * g + a, 512 * g + b
-            a0, tile = [(lo, tile) for lo, hi, tile in w_raw[c] if lo <= a and b <= hi][0]
-            return tile[:, :, a - a0 : b - a0]
-
-        w3_raw = {}
-        w3_view = [w.rearrange("(g p j) l -> p g (j l)", p=P, j=4) for w in (W31, W32)]
-
-        def load_w3(a, b):
-            tile = keep.tile([P, 2, b - a, 512], BF16, name=f"w3_raw{a}")
-            for i in range(2):
-                nc.sync.dma_start(out=tile[:, i, :, :], in_=w3_view[i][:, a:b, :])
-            for g in range(a, b):
-                w3_raw[g] = tile[:, :, g - a, :]
-
-        load_w(0, 0, 256, True)
-        load_x(0)
-        load_w(0, 256, 512, True)
-        load_x(1)
-        load_x(2)
-        load_w(1, 0, 512, True)
-        load_x(3)
-        load_w(0, 512, 1024, True)
-        load_w(1, 512, 1024, True)
-        nc.sync.dma_start(out=xq_rest[:], in_=x_view[:, 4 * IMAGE :])
-        bias = keep.tile([P, GROUPS, 4], BF16, name="bias")
-        nc.sync.dma_start(out=bias[:], in_=b11.rearrange("(g p t) -> p g t", p=P, t=4))
-        load_w(0, 1024, 2048)
+        load_w11(0, 0, PASS // 2)
+        load_w11(0, PASS // 2, PASS)
+        load_x(0, 1)
+        load_x(1, 2)
+        load_w11(1, 0, PASS)
+        load_x(2, 3)
+        load_x(3, 4)
+        load_w11(0, PASS, 2 * PASS)
+        load_w11(1, PASS, 2 * PASS)
+        load_x(4, ROWS)
+        load_bias1(0, 2)
+        load_w11(0, 2 * PASS, 3 * PASS)
         load_w3(0, 2)
-        load_w(1, 1024, 2048)
+        load_w11(1, 2 * PASS, 3 * PASS)
+        load_bias1(2, GROUPS)
         load_w3(2, 4)
-        load_w(0, 2048, 3072)
-        load_w(1, 2048, 3072)
-        load_w3(4, 8)
-        load_w(0, 3072, 4096)
-        load_w(1, 3072, 4096)
+        for g in range(3, GROUPS, 2):
+            for c in range(2):
+                load_w11(c, g * PASS, min(g + 2, GROUPS) * PASS)
+            if g == 3:
+                load_w3(4, GROUPS)
         bias3 = keep.tile([P, 2 * LATENT], BF16, name="bias3")
         nc.sync.dma_start(out=bias3[:, :LATENT], in_=b31.partition_broadcast(P))
         nc.sync.dma_start(out=bias3[:, LATENT:], in_=b32.partition_broadcast(P))
@@ -134,102 +123,100 @@ def tile_mae_pa_kernel(tc, x_bytes, x_scale, eps, W11, b11, W31, b31, W32, b32, 
         ident_bf = keep.tile([P, P], BF16, name="ident_bf")
         nc.scalar.activation(out=ident_bf[:], in_=ident[:], func=COPY)
 
-        idle = accs.tile([P, 512], F32, name="acc0")
-
-        def warm_up(n, bank=idle):
-            nc.tensor.matmul(out=bank[:, :n], lhsT=zeros[:, :P], rhs=zeros[:, :n], start=True, stop=True)
+        def warm_up(bank, columns):
+            nc.tensor.matmul(out=bank[:, :columns], lhsT=zeros[:, :P], rhs=zeros[:, :columns], start=True, stop=True)
 
         scale = keep.tile([P, IMAGE], F32, name="scale")
+        x_codes = [keep.tile([P, 2, HALF], U32, name=f"x_codes{h}", align_bytes=64) for h in range(2)]
+        x_scales = [keep.tile([P, 2, HALF], U8, name=f"x_scales{h}", align_bytes=64) for h in range(2)]
+        x_values, x_laid = {}, {}
 
         def spread_scale(c):
             bank = psum.tile([P, 4, P], F32, name="bank")
             for t in range(4):
                 nc.tensor.transpose(bank[:, t, :], scale_cols[:, c, t : t + 1].to_broadcast([P, P]), ident[:])
             nc.scalar.copy(
-                out=scale[:, 512 * c : 512 * (c + 1)].rearrange("p (m t) -> p m t", t=4),
+                out=scale[:, PASS * c : PASS * (c + 1)].rearrange("p (m t) -> p m t", t=4),
                 in_=bank[:].rearrange("p t m -> p m t"),
             )
 
-        xg, xb = {}, {}
-        x_codes = [keep.tile([P, 2, HALF], U32, name=f"x_codes{h}", align_bytes=64) for h in range(2)]
-        x_planes = [keep.tile([P, 2, HALF], U8, name=f"x_planes{h}", align_bytes=64) for h in range(2)]
-
-        def x_product(r, a=0, b=IMAGE):
-            if r not in xb:
-                xb[r] = work.tile([P, IMAGE], BF16, name="xb", bufs=5)
+        def x_product(r, k0=0, k1=IMAGE):
+            if r not in x_values:
+                x_values[r] = work.tile([P, IMAGE], BF16, name="x_values", bufs=5)
             nc.vector.tensor_tensor(
-                out=xb[r][:, a:b], in0=x_row(r)[:, a:b].bitcast(FP8), in1=scale[:, a:b], op=MULT
+                out=x_values[r][:, k0:k1], in0=x_raw[r][:, k0:k1].bitcast(FP8), in1=scale[:, k0:k1], op=MULT
             )
 
-        def x_tile(h):
-            if h not in xg:
-                xg[h] = work.tile([P, 2, 2 * HALF], F32, name="xg", bufs=2, align_bytes=64)
-            return xg[h]
-
         def x_turn(r):
-            if r in MM_ROWS:
+            if r in MATMUL_ROWS:
                 pairs = psum.tile([P, 4, 2 * P], BF16, name="bank")
                 for c in range(2):
                     for t in range(4):
                         nc.tensor.matmul(
                             out=pairs[:, 2 * c + t // 2, :],
-                            lhsT=xb[r][:, 512 * c + t : 512 * (c + 1) : 4],
-                            rhs=spread[:, t % 2, :],
+                            lhsT=x_values[r][:, PASS * c + t : PASS * (c + 1) : 4],
+                            rhs=wide_ident[:, t % 2, :],
                             start=(t % 2 == 0),
                             stop=(t % 2 == 1),
                         )
                 turned = pairs[:].bitcast(F32)
             else:
                 bank = psum.tile([P, 4, P], F32, name="bank")
-                words = xb[r][:].bitcast(F32)
+                words = x_values[r][:].bitcast(F32)
                 for c in range(2):
                     for u in range(2):
                         nc.tensor.transpose(
-                            bank[:, 2 * c + u, :], words[:, 256 * c + u : 256 * (c + 1) : 2], ident[:]
+                            bank[:, 2 * c + u, :], words[:, 2 * P * c + u : 2 * P * (c + 1) : 2], ident[:]
                         )
                 turned = bank[:]
-            dst = x_tile(r // 4)[:].rearrange("p c (n u) -> p c n u", u=2)
+            h, row = divmod(r, 4)
+            if h not in x_laid:
+                x_laid[h] = work.tile([P, 2, 2 * HALF], F32, name="x_laid", bufs=2, align_bytes=64)
             nc.scalar.copy(
-                out=dst[:, :, P * (r % 4) : P * (r % 4 + 1), :],
+                out=x_laid[h][:].rearrange("p c (n u) -> p c n u", u=2)[:, :, P * row : P * (row + 1), :],
                 in_=turned.rearrange("p (c u) n -> p c n u", u=2),
             )
 
-        def x_quant(h, c):
-            nc.vector.quantize_mx(
-                out=x_codes[h][:, c, :].bitcast(FP8X4),
-                scales=x_planes[h][:, c, :],
-                in_=xg[h][:, c, :].bitcast(BF16),
-            )
+        def x_quant(h):
+            for c in range(2):
+                nc.vector.quantize_mx(
+                    out=x_codes[h][:, c, :].bitcast(FP8X4),
+                    scales=x_scales[h][:, c, :],
+                    in_=x_laid[h][:, c, :].bitcast(BF16),
+                )
 
-        wg, w_codes, w_planes = {}, {}, {}
+        w_laid, w_codes, w_scales = {}, {}, {}
 
-        def w_tile(g, c):
-            if (g, c) not in wg:
-                wg[g, c] = work.tile([P, 1024], F32, name="wg", bufs=5, align_bytes=64)
-            return wg[g, c]
+        def w_source(g, c, a, b):
+            a, b = PASS * g + a, PASS * g + b
+            n0, tile = [(n0, tile) for n0, n1, tile in w11_raw[c] if n0 <= a and b <= n1][0]
+            return tile[:, :, a - n0 : b - n0]
 
-        def w_tensor(g, c, a, b):
-            bank = psum.tile([P, 4, P], F32, name="bank")
-            flat = bank[:].rearrange("p a b -> p (a b)")[:, : 2 * (b - a)]
-            for n0 in range(a, b, P):
-                n1 = min(b, n0 + P)
+        def w_target(g, c):
+            if (g, c) not in w_laid:
+                w_laid[g, c] = work.tile([P, 2 * PASS], F32, name="w_laid", bufs=5, align_bytes=64)
+            return w_laid[g, c]
+
+        def w_tensor(g, c):
+            bank = psum.tile([P, 2 * BANK_CHANNELS], F32, name="bank")
+            for n0 in range(0, BANK_CHANNELS, P):
                 nc.tensor.matmul(
-                    out=flat[:, 2 * (n0 - a) : 2 * (n1 - a)].bitcast(BF16),
+                    out=bank[:, 2 * n0 : 2 * (n0 + P)].bitcast(BF16),
                     lhsT=ident_bf[:],
-                    rhs=w_src(g, c, n0, n1).rearrange("p j n -> p n j"),
+                    rhs=w_source(g, c, n0, n0 + P).rearrange("p j n -> p n j"),
                     start=True,
                     stop=True,
                 )
-            dst = w_tile(g, c)[:].rearrange("p (t m u) -> p t m u", t=4, u=2)
             nc.scalar.copy(
-                out=dst[:, :, a // 4 : b // 4, :], in_=flat.rearrange("p (m t u) -> p t m u", t=4, u=2)
+                out=w_target(g, c)[:].rearrange("p (t m u) -> p t m u", t=4, u=2)[:, :, : BANK_CHANNELS // 4, :],
+                in_=bank[:].rearrange("p (m t u) -> p t m u", t=4, u=2),
             )
 
         def w_copy(engine_copy, g, c, a, b):
-            dst = w_tile(g, c)[:].bitcast(BF16).rearrange("p (t m i j) -> p m t j i", t=4, i=2, j=4)
+            target = w_target(g, c)[:].bitcast(BF16).rearrange("p (t m i j) -> p m t j i", t=4, i=2, j=4)
             engine_copy(
-                out=dst[:, a // 8 : b // 8, :, :, :],
-                in_=w_src(g, c, a, b).rearrange("p j (m i t) -> p m t j i", t=4, i=2),
+                out=target[:, a // 8 : b // 8, :, :, :],
+                in_=w_source(g, c, a, b).rearrange("p j (m i t) -> p m t j i", t=4, i=2),
             )
 
         def w_vector(g, c, a, b):
@@ -240,225 +227,232 @@ def tile_mae_pa_kernel(tc, x_bytes, x_scale, eps, W11, b11, W31, b31, W32, b32, 
 
         def w_quant(g, c):
             if g not in w_codes:
-                w_codes[g] = work.tile([P, 2, 512], U32, name="w_codes", bufs=LAG + 3, align_bytes=64)
-                w_planes[g] = work.tile([P, 2, 512], U8, name="w_planes", bufs=LAG + 3, align_bytes=64)
+                w_codes[g] = work.tile([P, 2, PASS], U32, name="w_codes", bufs=4, align_bytes=64)
+                w_scales[g] = work.tile([P, 2, PASS], U8, name="w_scales", bufs=4, align_bytes=64)
             nc.vector.quantize_mx(
-                out=w_codes[g][:, c, :].bitcast(FP8X4), scales=w_planes[g][:, c, :], in_=wg[g, c][:].bitcast(BF16)
+                out=w_codes[g][:, c, :].bitcast(FP8X4),
+                scales=w_scales[g][:, c, :],
+                in_=w_laid[g, c][:].bitcast(BF16),
             )
 
-        w3g = {}
+        w3_laid = {}
         w3_codes = keep.tile([P, GROUPS, 2 * LATENT], U32, name="w3_codes", align_bytes=64)
-        w3_planes = keep.tile([P, GROUPS, 2 * LATENT], U8, name="w3_planes", align_bytes=64)
+        w3_scales = keep.tile([P, GROUPS, 2 * LATENT], U8, name="w3_scales", align_bytes=64)
 
-        def w3_lay(g, engine_copy=nc.vector.tensor_copy):
-            w3g[g] = work.tile([P, 1024], BF16, name="w3g", bufs=2, align_bytes=64)
-            engine_copy(
-                out=w3g[g][:].rearrange("p (w c i j) -> p w c j i", w=2, i=4, j=4),
-                in_=w3_raw[g].rearrange("p w (j c i) -> p w c j i", j=4, i=4),
+        def w3_lay(g):
+            w3_laid[g] = work.tile([P, 8 * LATENT], BF16, name="w3_laid", bufs=2, align_bytes=64)
+            nc.vector.tensor_copy(
+                out=w3_laid[g][:].rearrange("p (w m i j) -> p w m j i", w=2, i=4, j=4),
+                in_=w3_raw[g].rearrange("p w (j m i) -> p w m j i", j=4, i=4),
             )
 
         def w3_quant(g):
             nc.vector.quantize_mx(
-                out=w3_codes[:, g, :].bitcast(FP8X4), scales=w3_planes[:, g, :], in_=w3g[g][:]
+                out=w3_codes[:, g, :].bitcast(FP8X4), scales=w3_scales[:, g, :], in_=w3_laid[g][:]
             )
 
-        enc, encg, enc_codes, enc_planes = {}, {}, {}, {}
+        enc, enc_laid, enc_codes, enc_scales = {}, {}, {}, {}
 
-        def first_stage(s, between):
-            h, g, r0, rows = UNITS[s]
-            a, b = P * r0, P * (r0 + rows)
-            enc[s] = work.tile([P, 4, b - a], BF16, name="enc", bufs=3)
+        def tokens(s):
+            return P * UNITS[s][3]
+
+        def first_stage(s, after_bank):
+            h, g, row0, rows = UNITS[s]
+            cols = slice(P * row0, P * (row0 + rows))
+            enc[s] = work.tile([P, 4, tokens(s)], BF16, name="enc", bufs=3)
             for t in range(4):
-                bank = psum.tile([P, 4, P], F32, name="bank")
-                flat = bank[:].rearrange("p a b -> p (a b)")[:, : b - a]
+                bank = psum.tile([P, HALF], F32, name="bank")
                 for c in range(2):
                     nc.tensor.matmul_mx(
-                        out=flat,
+                        out=bank[:, : tokens(s)],
                         lhsT=w_codes[g][:, c, P * t : P * (t + 1)].bitcast(FP8X4),
-                        lhsT_scale=w_planes[g][:, c, P * t : P * (t + 1)],
-                        rhs=x_codes[h][:, c, a:b].bitcast(FP8X4),
-                        rhs_scale=x_planes[h][:, c, a:b],
+                        lhsT_scale=w_scales[g][:, c, P * t : P * (t + 1)],
+                        rhs=x_codes[h][:, c, cols].bitcast(FP8X4),
+                        rhs_scale=x_scales[h][:, c, cols],
                         start=(c == 0),
                         stop=(c == 1),
                     )
-                nc.scalar.activation(out=enc[s][:, t, :], in_=flat, func=RELU, bias=bias[:, g, t : t + 1])
-                for job in between.get(t, []):
-                    job()
+                nc.scalar.activation(
+                    out=enc[s][:, t, :], in_=bank[:, : tokens(s)], func=RELU, bias=bias1[g][:, t : t + 1]
+                )
+                for job, *args in after_bank[t]:
+                    job(*args)
 
-        def enc_lay(s, a, b, engine_copy=nc.vector.tensor_copy):
-            if s not in encg:
-                encg[s] = work.tile([P, 4 * P * UNITS[s][3]], BF16, name="encg", bufs=3, align_bytes=64)
+        def enc_lay(engine_copy, s, a, b):
+            if s not in enc_laid:
+                enc_laid[s] = work.tile([P, 4 * tokens(s)], BF16, name="enc_laid", bufs=3, align_bytes=64)
             engine_copy(
-                out=encg[s][:, 4 * a : 4 * b].rearrange("p (c i t) -> p c t i", i=4, t=4),
-                in_=enc[s][:, :, a:b].rearrange("p t (c i) -> p c t i", i=4),
+                out=enc_laid[s][:, 4 * a : 4 * b].rearrange("p (m i t) -> p m t i", i=4, t=4),
+                in_=enc[s][:, :, a:b].rearrange("p t (m i) -> p m t i", i=4),
             )
 
         def enc_quant(s, a, b):
             if s not in enc_codes:
-                enc_codes[s] = work.tile([P, P * UNITS[s][3]], U32, name="enc_codes", bufs=ENC_BUFS, align_bytes=64)
-                enc_planes[s] = work.tile([P, P * UNITS[s][3]], U8, name="enc_planes", bufs=ENC_BUFS, align_bytes=64)
+                enc_codes[s] = work.tile([P, tokens(s)], U32, name="enc_codes", bufs=3, align_bytes=64)
+                enc_scales[s] = work.tile([P, tokens(s)], U8, name="enc_scales", bufs=3, align_bytes=64)
             nc.vector.quantize_mx(
-                out=enc_codes[s][:, a:b].bitcast(FP8X4), scales=enc_planes[s][:, a:b], in_=encg[s][:, 4 * a : 4 * b]
+                out=enc_codes[s][:, a:b].bitcast(FP8X4),
+                scales=enc_scales[s][:, a:b],
+                in_=enc_laid[s][:, 4 * a : 4 * b],
             )
 
         acc = {}
 
-        def second_stage(s, only=None):
-            h, g, r0, rows = UNITS[s]
-            for r in range(rows) if only is None else [only]:
-                if 2 * h + (r0 + r) // 2 not in acc:
-                    i = 2 * h + (r0 + r) // 2
-                    acc[i] = accs.tile([P, 2, 2 * LATENT], F32, name=f"acc{i}")
+        def second_stage(s):
+            h, g, row0, rows = UNITS[s]
+            for r in range(rows):
+                i = 2 * h + (row0 + r) // 2
+                if i not in acc:
+                    acc[i] = sums.tile([P, 2, 2 * LATENT], F32, name=f"sum{i}")
                 nc.tensor.matmul_mx(
-                    out=acc[2 * h + (r0 + r) // 2][:, r % 2, :],
+                    out=acc[i][:, r % 2, :],
                     lhsT=enc_codes[s][:, P * r : P * (r + 1)].bitcast(FP8X4),
-                    lhsT_scale=enc_planes[s][:, P * r : P * (r + 1)],
+                    lhsT_scale=enc_scales[s][:, P * r : P * (r + 1)],
                     rhs=w3_codes[:, g, :].bitcast(FP8X4),
-                    rhs_scale=w3_planes[:, g, :],
+                    rhs_scale=w3_scales[:, g, :],
                     start=(g == 0 and r % 2 == 0),
                     stop=(g == GROUPS - 1 and r % 2 == 1),
                 )
 
-        y, z, relus = {}, {}, {}
-        views = [o.rearrange("(p r) l -> p r l", r=ROWS) for o in (out_0, out_1, out_2)]
+        biased, z = {}, {}
+        out_views = [o.rearrange("(p r) l -> p r l", r=ROWS) for o in (out_0, out_1, out_2)]
 
         def add_bias(i, a=0, b=2):
-            if i not in y:
-                y[i] = work.tile([P, 2, 2 * LATENT], F32, name="y", bufs=3)
+            if i not in biased:
+                biased[i] = work.tile([P, 2, 2 * LATENT], F32, name="biased", bufs=3)
             nc.vector.tensor_tensor(
-                out=y[i][:, a:b, :], in0=acc[i][:, a:b, :],
+                out=biased[i][:, a:b, :], in0=acc[i][:, a:b, :],
                 in1=bias3[:].unsqueeze(1).to_broadcast([P, b - a, 2 * LATENT]), op=ADD,
             )
 
-        def relu_out(i):
-            relus[i] = work.tile([P, 2, 2, LATENT], F32, name="relu", bufs=3)
-            nc.scalar.activation(
-                out=relus[i][:], in_=y[i][:].rearrange("p r (w l) -> p w r l", w=2), func=RELU
-            )
+        def mu_sigma(i):
+            both = work.tile([P, 2, 2, LATENT], F32, name="mu_sigma", bufs=4)
+            nc.scalar.activation(out=both[:], in_=biased[i][:].rearrange("p r (w l) -> p w r l", w=2), func=RELU)
             for w in range(2):
-                nc.sync.dma_start(out=views[w][:, 2 * i : 2 * i + 2, :], in_=relus[i][:, w, :, :])
+                nc.sync.dma_start(out=out_views[w][:, 2 * i : 2 * i + 2, :], in_=both[:, w, :, :])
 
         def z_noise(i, a=0, b=2):
             if i not in z:
                 z[i] = work.tile([P, 2, LATENT], F32, name="z", bufs=4)
             nc.vector.scalar_tensor_tensor(
-                out=z[i][:, a:b, :], in0=y[i][:, a:b, LATENT:], scalar=0.0,
+                out=z[i][:, a:b, :], in0=biased[i][:, a:b, LATENT:], scalar=0.0,
                 in1=eps_sb[:, 2 * i + a : 2 * i + b, :], op0=MAX, op1=MULT,
             )
 
-        def z_out(i, a=0, b=2):
+        def z_add_mu(i, a=0, b=2):
             nc.vector.scalar_tensor_tensor(
-                out=z[i][:, a:b, :], in0=y[i][:, a:b, :LATENT], scalar=0.0, in1=z[i][:, a:b, :], op0=MAX, op1=ADD,
+                out=z[i][:, a:b, :], in0=biased[i][:, a:b, :LATENT], scalar=0.0,
+                in1=z[i][:, a:b, :], op0=MAX, op1=ADD,
             )
             if b == 2:
-                nc.sync.dma_start(out=views[2][:, 2 * i : 2 * i + 2, :], in_=z[i][:])
+                nc.sync.dma_start(out=out_views[2][:, 2 * i : 2 * i + 2, :], in_=z[i][:])
 
-        warm_up(256)
-        warm_up(256)
+        unused_sum = sums.tile([P, HALF], F32, name="sum0")
+        warm_up(unused_sum, 256)
+        warm_up(unused_sum, 256)
         spread_scale(0)
         spread_scale(1)
-        warm_up(384)
-        w_vector(0, 0, 0, 256)
-        w_scalar(0, 0, 256, 512)
-        x_product(0, 0, 512)
-        x_product(0, 512, IMAGE)
+        warm_up(unused_sum, 384)
+        w_vector(0, 0, 0, PASS // 2)
+        w_vector(0, 0, PASS // 2, PASS)
+        x_product(0, 0, PASS)
+        x_product(0, PASS, IMAGE)
         x_product(1)
+        w_scalar(0, 1, 0, PASS // 2)
         x_turn(0)
-        w_scalar(0, 1, 0, 384)
+        w_scalar(0, 1, PASS // 2, PASS)
         x_product(2)
         x_turn(1)
         x_product(3)
         x_turn(2)
         x_turn(3)
-        w_vector(0, 1, 384, 512)
         w_quant(0, 0)
-        w_vector(1, 0, 384, 512)
+        for c in range(2):
+            w_vector(1, c, BANK_CHANNELS, PASS)
         w_quant(0, 1)
-        x_quant(0, 0)
-        x_quant(0, 1)
-        w_tensor(1, 0, 0, 256)
-        w_scalar(1, 0, 256, 384)
-        w_tensor(1, 1, 0, 256)
-        w_tensor(1, 1, 256, 512)
-        x_product(4)
-        x_product(5)
-        x_product(6)
-        x_product(7)
-        first_stage(0, {t: [lambda t=t: x_turn(4 + t)] + ([lambda: w_scalar(2, 0, 256, 512)] if t == 3 else []) for t in range(4)})
-        w_quant(1, 0)
-        w_quant(1, 1)
+        x_quant(0)
+        for c in range(2):
+            w_tensor(1, c)
+
+        for r in range(4, ROWS):
+            x_product(r)
+        first_stage(0, [
+            [(w_scalar, 2, 0, BANK_CHANNELS, PASS)],
+            [(x_turn, 4)],
+            [(x_turn, 5)],
+            [(x_turn, 6), (w_tensor, 2, 0)],
+        ])
+        for c in range(2):
+            w_quant(1, c)
         w3_lay(0)
         w3_lay(1)
         w3_quant(0)
-        x_quant(1, 0)
-        x_quant(1, 1)
 
-        last = len(UNITS) - 1
-        for s in range(1, last + 1):
-            pg, pc = (s + 4) // 2, s % 2
-            n_pe, n_s = CUTS[pc]
-            width = P * UNITS[s - 1][3]
-            share = SH[0] if s == 14 else (SH[1] if s > 14 else 0)
-            between = {t: [] for t in range(4)}
-            if pg < GROUPS:
-                if n_pe:
-                    between[0].append(lambda: w_tensor(pg, pc, 0, n_pe))
-                if n_s:
-                    between[1].append(lambda: w_scalar(pg, pc, n_pe, n_pe + n_s))
+        for s in range(1, LAST + 1):
+            g, c = divmod(s + 4, 2)
+            tensor_end = BANK_CHANNELS if c == 0 else 0
+            scalar_end = tensor_end + (SCALAR_CHANNELS_STEP_1 if s == 1 else SCALAR_CHANNELS[c])
+            share = tokens(s - 1) // SCALAR_TAIL_SHARE if s >= len(WIDE_UNITS) else 0
+            after_bank = [[], [], [], []]
+            if g < GROUPS:
+                if c == 0:
+                    after_bank[0].append((w_tensor, g, c))
+                after_bank[1].append((w_scalar, g, c, tensor_end, scalar_end))
             if s == 1:
-                between[0].append(lambda: w_tensor(2, 0, 0, 256))
-            if s >= 2:
-                between[S2AT if s < 14 else S2T].insert(0, lambda: second_stage(s - 2))
+                after_bank[0].append((x_turn, ROWS - 1))
+            else:
+                after_bank[3].append((second_stage, s - 2))
             if share:
-                between[0].append(lambda: enc_lay(s - 1, 0, share, nc.scalar.copy))
-            if s == W37:
-                between[1].append(lambda: w3_lay(GROUPS - 1, nc.scalar.copy))
-            if s >= RL:
-                between[RT].append(lambda: relu_out(s - RL))
-            first_stage(s, between)
-            qg, qc = (s + 3) // 2, (s + 1) % 2
-            if qg < GROUPS and s > 1:
-                w_quant(qg, qc)
-            enc_lay(s - 1, share, width)
-            if pg < GROUPS:
-                w_vector(pg, pc, n_pe + n_s, 512)
-            if s < (12 if W37 else 14) and s % 2 == 0:
-                w3_lay((s + 2) // 2)
+                after_bank[0].append((enc_lay, nc.scalar.copy, s - 1, 0, share))
+            if s == LAST:
+                after_bank[3].append((mu_sigma, 0))
+            first_stage(s, after_bank)
+
+            w3_group, w3_phase = divmod(s + 2, 2)
+            if s > 1 and (s + 3) // 2 < GROUPS:
+                w_quant(*divmod(s + 3, 2))
+            enc_lay(nc.vector.tensor_copy, s - 1, share, tokens(s - 1))
+            if g < GROUPS:
+                w_vector(g, c, scalar_end, PASS)
+            if w3_phase == 0 and w3_group < GROUPS:
+                w3_lay(w3_group)
             if s == 1:
                 w_quant(2, 0)
-            if s == 15:
+                x_quant(1)
+            if s == HALF0_CLOSED:
                 add_bias(0)
-            if s == 16:
+            if s == HALF0_CLOSED + 1:
                 z_noise(0)
                 z_noise(1)
-            if s == 17:
-                z_out(1)
-            if s == max(W37, 13):
-                w3_quant(GROUPS - 1)
-            enc_quant(s - 1, 0, width)
-            if s < 13 and s % 2 == 1:
-                w3_quant((s + 1) // 2)
-            if s == 15:
+            if s == HALF0_CLOSED + 2:
+                z_add_mu(1)
+            if w3_phase == 1 and w3_group == GROUPS - 1:
+                w3_quant(w3_group)
+            enc_quant(s - 1, 0, tokens(s - 1))
+            if w3_phase == 1 and w3_group < GROUPS - 1:
+                w3_quant(w3_group)
+            if s == HALF0_CLOSED:
                 add_bias(1)
-            if s == 16:
-                z_out(0)
+            if s == HALF0_CLOSED + 1:
+                z_add_mu(0)
 
-        enc_lay(last, 2 * P - LS, 2 * P, nc.scalar.copy)
+        enc_lay(nc.scalar.copy, LAST, P, 2 * P)
         add_bias(2)
-        second_stage(last - 1)
-        warm_up(256, psum.tile([P, 512], F32, name="bank"))
-        for i in range(last + 1 - RL, 3):
-            relu_out(i)
-        enc_lay(last, 0, 2 * P - LS)
+        second_stage(LAST - 1)
+        unused_bank = psum.tile([P, HALF], F32, name="bank")
+        warm_up(unused_bank, 256)
+        mu_sigma(1)
+        mu_sigma(2)
+        enc_lay(nc.vector.tensor_copy, LAST, 0, P)
         z_noise(2)
-        enc_quant(last, 0, P)
-        enc_quant(last, P, 2 * P)
-        second_stage(last)
-        z_out(2)
+        for r in range(2):
+            enc_quant(LAST, P * r, P * (r + 1))
+        second_stage(LAST)
+        z_add_mu(2)
         for r in range(2):
             add_bias(3, r, r + 1)
-        relu_out(3)
+        mu_sigma(3)
         for r in range(2):
             z_noise(3, r, r + 1)
         for r in range(2):
-            z_out(3, r, r + 1)
+            z_add_mu(3, r, r + 1)

@@ -36,7 +36,7 @@ HALF0_CLOSED = UNITS.index((0, GROUPS - 1, 0, 4)) + 2
 SCALAR_CHANNELS = (64, 256)
 SCALAR_CHANNELS_STEP_1 = 384
 SCALAR_TAIL_SHARE = 4
-MATMUL_ROWS = (0, 1, 2, 3, 5)
+MATMUL_ROWS = (0, 1, 3, 5)
 
 
 def tile_mae_pa_kernel(tc, x_bytes, x_scale, eps, W11, b11, W31, b31, W32, b32, out_0, out_1, out_2):
@@ -47,19 +47,17 @@ def tile_mae_pa_kernel(tc, x_bytes, x_scale, eps, W11, b11, W31, b31, W32, b32, 
         psum = ctx.enter_context(tc.psum_pool(name="psum", bufs=4))
         sums = ctx.enter_context(tc.psum_pool(name="sums", bufs=1))
 
-        zeros = keep.tile([P, 384], F32, name="zeros")
-        nc.gpsimd.memset(zeros[:], 0.0)
         ident = keep.tile([P, P], F32, name="ident")
         make_identity(nc, ident[:])
-        wide_ident = keep.tile([P, 2, 2 * P], BF16, name="wide_ident")
-        nc.gpsimd.memset(wide_ident[:], 0.0)
-        for e in range(2):
-            nc.gpsimd.affine_select(
-                out=wide_ident[:, e, :], in_=wide_ident[:, e, :], compare_op=NOT_EQUAL, fill=1.0,
-                base=e, pattern=[[-1, 2 * P]], channel_multiplier=2,
-            )
         ctx.enter_context(tc.manual_schedule())
         ctx.enter_context(nc.allow_non_contiguous_dma(reason="runs of four scales and of four biases"))
+
+        zeros = keep.tile([P, 256], F32, name="zeros")
+        nc.vector.memset(zeros[:], 0.0)
+        wide_ident = keep.tile([P, 2, 2 * P], BF16, name="wide_ident")
+        nc.vector.memset(wide_ident[:], 0.0)
+        for e in range(2):
+            nc.vector.tensor_copy(out=wide_ident[:, e, e : 2 * P : 2], in_=ident[:])
 
         x_view = x_bytes.rearrange("(p r) k -> p (r k)", r=ROWS)
         w11_view = W11.rearrange("(c p j) n -> c p j n", c=2, j=4)
@@ -79,11 +77,10 @@ def tile_mae_pa_kernel(tc, x_bytes, x_scale, eps, W11, b11, W31, b31, W32, b32, 
             w11_raw[c].append((n0, n1, tile))
 
         def load_w3(g0, g1):
-            tile = keep.tile([P, 2, g1 - g0, 4 * LATENT], BF16, name=f"w3_raw{g0}")
+            tile = keep.tile([P, g1 - g0, 2, 4 * LATENT], BF16, name=f"w3_raw{g0}")
             for w in range(2):
-                nc.sync.dma_start(out=tile[:, w, :, :], in_=w3_views[w][:, g0:g1, :])
-            for g in range(g0, g1):
-                w3_raw[g] = tile[:, :, g - g0, :]
+                nc.sync.dma_start(out=tile[:, :, w, :], in_=w3_views[w][:, g0:g1, :])
+            w3_raw[g0, g1] = tile
 
         def load_bias1(g0, g1):
             tile = keep.tile([P, g1 - g0, 4], BF16, name=f"bias1_{g0}")
@@ -91,29 +88,29 @@ def tile_mae_pa_kernel(tc, x_bytes, x_scale, eps, W11, b11, W31, b31, W32, b32, 
             for g in range(g0, g1):
                 bias1[g] = tile[:, g - g0, :]
 
-        scale_cols = keep.tile([P, 2, 4], F32, name="scale_cols")
-        nc.sync.dma_start(out=scale_cols[:], in_=x_scale.rearrange("o (c p t) -> p (o c) t", p=P, t=4))
-        load_w11(0, 0, PASS // 2)
-        load_w11(0, PASS // 2, PASS)
         load_x(0, 1)
+        load_w11(0, 0, PASS // 2)
         load_x(1, 2)
-        load_w11(1, 0, PASS)
-        load_x(2, 3)
-        load_x(3, 4)
-        load_w11(0, PASS, 2 * PASS)
-        load_w11(1, PASS, 2 * PASS)
-        load_x(4, ROWS)
+        scale = keep.tile([P, 2, 4], F32, name="scale")
+        nc.sync.dma_start(out=scale[:], in_=x_scale.rearrange("o (c p t) -> p (o c) t", p=P, t=4))
+        load_w11(0, PASS // 2, PASS)
+        load_x(2, 4)
+        load_x(4, 6)
+        load_w11(1, 0, PASS // 2)
+        load_w11(1, PASS // 2, PASS)
+        load_x(6, ROWS)
         load_bias1(0, 2)
+        load_w11(0, PASS, 2 * PASS)
+        load_w3(0, 3)
+        load_w11(1, PASS, 2 * PASS)
         load_w11(0, 2 * PASS, 3 * PASS)
-        load_w3(0, 2)
         load_w11(1, 2 * PASS, 3 * PASS)
         load_bias1(2, GROUPS)
-        load_w3(2, 4)
         for g in range(3, GROUPS, 2):
             for c in range(2):
                 load_w11(c, g * PASS, min(g + 2, GROUPS) * PASS)
             if g == 3:
-                load_w3(4, GROUPS)
+                load_w3(3, GROUPS)
         bias3 = keep.tile([P, 2 * LATENT], BF16, name="bias3")
         nc.sync.dma_start(out=bias3[:, :LATENT], in_=b31.partition_broadcast(P))
         nc.sync.dma_start(out=bias3[:, LATENT:], in_=b32.partition_broadcast(P))
@@ -126,55 +123,52 @@ def tile_mae_pa_kernel(tc, x_bytes, x_scale, eps, W11, b11, W31, b31, W32, b32, 
         def warm_up(bank, columns):
             nc.tensor.matmul(out=bank[:, :columns], lhsT=zeros[:, :P], rhs=zeros[:, :columns], start=True, stop=True)
 
-        scale = keep.tile([P, IMAGE], F32, name="scale")
         x_codes = [keep.tile([P, 2, HALF], U32, name=f"x_codes{h}", align_bytes=64) for h in range(2)]
         x_scales = [keep.tile([P, 2, HALF], U8, name=f"x_scales{h}", align_bytes=64) for h in range(2)]
-        x_values, x_laid = {}, {}
+        x_wide, x_turned, x_laid = {}, {}, {}
 
-        def spread_scale(c):
-            bank = psum.tile([P, 4, P], F32, name="bank")
-            for t in range(4):
-                nc.tensor.transpose(bank[:, t, :], scale_cols[:, c, t : t + 1].to_broadcast([P, P]), ident[:])
+        def x_widen(r, c0=0, c1=2):
+            if r not in x_wide:
+                x_wide[r] = work.tile([P, IMAGE], BF16, name="x_wide", bufs=4)
             nc.scalar.copy(
-                out=scale[:, PASS * c : PASS * (c + 1)].rearrange("p (m t) -> p m t", t=4),
-                in_=bank[:].rearrange("p t m -> p m t"),
+                out=x_wide[r][:, PASS * c0 : PASS * c1], in_=x_raw[r][:, PASS * c0 : PASS * c1].bitcast(FP8)
             )
 
-        def x_product(r, k0=0, k1=IMAGE):
-            if r not in x_values:
-                x_values[r] = work.tile([P, IMAGE], BF16, name="x_values", bufs=5)
-            nc.vector.tensor_tensor(
-                out=x_values[r][:, k0:k1], in0=x_raw[r][:, k0:k1].bitcast(FP8), in1=scale[:, k0:k1], op=MULT
-            )
-
-        def x_turn(r):
+        def x_turn(r, c0=0, c1=2):
+            pool, tag = (psum, "bank") if c1 - c0 == 1 else (sums, f"sum{r % 4}")
             if r in MATMUL_ROWS:
-                pairs = psum.tile([P, 4, 2 * P], BF16, name="bank")
-                for c in range(2):
+                pairs = pool.tile([P, 2, c1 - c0, 2 * P], BF16, name=tag)
+                for c in range(c0, c1):
                     for t in range(4):
                         nc.tensor.matmul(
-                            out=pairs[:, 2 * c + t // 2, :],
-                            lhsT=x_values[r][:, PASS * c + t : PASS * (c + 1) : 4],
+                            out=pairs[:, t // 2, c - c0, :],
+                            lhsT=x_wide[r][:, PASS * c + t : PASS * (c + 1) : 4],
                             rhs=wide_ident[:, t % 2, :],
                             start=(t % 2 == 0),
                             stop=(t % 2 == 1),
                         )
-                turned = pairs[:].bitcast(F32)
+                x_turned[r, c0] = pairs[:]
             else:
-                bank = psum.tile([P, 4, P], F32, name="bank")
-                words = x_values[r][:].bitcast(F32)
-                for c in range(2):
+                bank = pool.tile([P, 2, c1 - c0, P], F32, name=tag)
+                words = x_wide[r][:].bitcast(F32)
+                for c in range(c0, c1):
                     for u in range(2):
                         nc.tensor.transpose(
-                            bank[:, 2 * c + u, :], words[:, 2 * P * c + u : 2 * P * (c + 1) : 2], ident[:]
+                            bank[:, u, c - c0, :], words[:, 2 * P * c + u : 2 * P * (c + 1) : 2], ident[:]
                         )
-                turned = bank[:]
+                x_turned[r, c0] = bank[:].bitcast(BF16)
+
+        def x_product(r, c0=0, c1=2):
             h, row = divmod(r, 4)
             if h not in x_laid:
-                x_laid[h] = work.tile([P, 2, 2 * HALF], F32, name="x_laid", bufs=2, align_bytes=64)
-            nc.scalar.copy(
-                out=x_laid[h][:].rearrange("p c (n u) -> p c n u", u=2)[:, :, P * row : P * (row + 1), :],
-                in_=turned.rearrange("p (c u) n -> p c n u", u=2),
+                x_laid[h] = work.tile([P, 2, HALF, 4], BF16, name="x_laid", bufs=2, align_bytes=64)
+            nc.vector.tensor_tensor(
+                out=x_laid[h][:, c0:c1, P * row : P * (row + 1), :].rearrange("p c n (u e) -> p c n u e", u=2),
+                in0=x_turned[r, c0].rearrange("p u c (n e) -> p c n u e", e=2),
+                in1=scale[:, c0:c1, :].rearrange("p c (u e) -> p c u e", u=2).unsqueeze(2).to_broadcast(
+                    [P, c1 - c0, P, 2, 2]
+                ),
+                op=MULT,
             )
 
         def x_quant(h):
@@ -182,10 +176,10 @@ def tile_mae_pa_kernel(tc, x_bytes, x_scale, eps, W11, b11, W31, b31, W32, b32, 
                 nc.vector.quantize_mx(
                     out=x_codes[h][:, c, :].bitcast(FP8X4),
                     scales=x_scales[h][:, c, :],
-                    in_=x_laid[h][:, c, :].bitcast(BF16),
+                    in_=x_laid[h][:, c, :, :].rearrange("p n t -> p (n t)"),
                 )
 
-        w_laid, w_codes, w_scales = {}, {}, {}
+        w_laid, w_banks, w_codes, w_scales = {}, {}, {}, {}
 
         def w_source(g, c, a, b):
             a, b = PASS * g + a, PASS * g + b
@@ -194,23 +188,34 @@ def tile_mae_pa_kernel(tc, x_bytes, x_scale, eps, W11, b11, W31, b31, W32, b32, 
 
         def w_target(g, c):
             if (g, c) not in w_laid:
-                w_laid[g, c] = work.tile([P, 2 * PASS], F32, name="w_laid", bufs=5, align_bytes=64)
+                if g == 0:
+                    w_laid[g, c] = keep.tile([P, 2 * PASS], F32, name=f"head_laid{c}", align_bytes=64)
+                else:
+                    w_laid[g, c] = work.tile([P, 2 * PASS], F32, name="w_laid", bufs=4, align_bytes=64)
             return w_laid[g, c]
 
-        def w_tensor(g, c):
-            bank = psum.tile([P, 2 * BANK_CHANNELS], F32, name="bank")
+        def w_matmuls(g, c, a=0):
+            w_banks[g, c, a] = bank = psum.tile([P, 2 * BANK_CHANNELS], F32, name="bank")
             for n0 in range(0, BANK_CHANNELS, P):
                 nc.tensor.matmul(
                     out=bank[:, 2 * n0 : 2 * (n0 + P)].bitcast(BF16),
                     lhsT=ident_bf[:],
-                    rhs=w_source(g, c, n0, n0 + P).rearrange("p j n -> p n j"),
+                    rhs=w_source(g, c, a + n0, a + n0 + P).rearrange("p j n -> p n j"),
                     start=True,
                     stop=True,
                 )
+
+        def w_empty(g, c, a=0):
             nc.scalar.copy(
-                out=w_target(g, c)[:].rearrange("p (t m u) -> p t m u", t=4, u=2)[:, :, : BANK_CHANNELS // 4, :],
-                in_=bank[:].rearrange("p (m t u) -> p t m u", t=4, u=2),
+                out=w_target(g, c)[:].rearrange("p (t m u) -> p t m u", t=4, u=2)[
+                    :, :, a // 4 : (a + BANK_CHANNELS) // 4, :
+                ],
+                in_=w_banks[g, c, a][:].rearrange("p (m t u) -> p t m u", t=4, u=2),
             )
+
+        def w_tensor(g, c, a=0):
+            w_matmuls(g, c, a)
+            w_empty(g, c, a)
 
         def w_copy(engine_copy, g, c, a, b):
             target = w_target(g, c)[:].bitcast(BF16).rearrange("p (t m i j) -> p m t j i", t=4, i=2, j=4)
@@ -240,15 +245,26 @@ def tile_mae_pa_kernel(tc, x_bytes, x_scale, eps, W11, b11, W31, b31, W32, b32, 
         w3_scales = keep.tile([P, GROUPS, 2 * LATENT], U8, name="w3_scales", align_bytes=64)
 
         def w3_lay(g):
-            w3_laid[g] = work.tile([P, 8 * LATENT], BF16, name="w3_laid", bufs=2, align_bytes=64)
+            g0, g1 = [k for k in w3_raw if k[0] <= g < k[1]][0]
+            w3_laid[g] = work.tile([P, 8 * LATENT], BF16, name="w3_laid", bufs=1, align_bytes=64)[:]
             nc.vector.tensor_copy(
-                out=w3_laid[g][:].rearrange("p (w m i j) -> p w m j i", w=2, i=4, j=4),
-                in_=w3_raw[g].rearrange("p w (j m i) -> p w m j i", j=4, i=4),
+                out=w3_laid[g].rearrange("p (w m i j) -> p w m j i", w=2, i=4, j=4),
+                in_=w3_raw[g0, g1][:, g - g0, :, :].rearrange("p w (j m i) -> p w m j i", j=4, i=4),
             )
+
+        def w3_gpsimd(g0, g1, c):
+            tile = keep.tile([P, g1 - g0, 8 * LATENT], BF16, name=f"head_laid{c}", align_bytes=64)
+            nc.gpsimd.tensor_scalar(
+                out=tile[:].rearrange("p g (w l j) -> p (g w) l j", w=2, j=4),
+                in0=w3_raw[g0, g1][:].rearrange("p g w (j l) -> p (g w) l j", j=4),
+                scalar1=1.0, scalar2=0.0, op0=MULT, op1=ADD,
+            )
+            for g in range(g0, g1):
+                w3_laid[g] = tile[:, g - g0, :]
 
         def w3_quant(g):
             nc.vector.quantize_mx(
-                out=w3_codes[:, g, :].bitcast(FP8X4), scales=w3_scales[:, g, :], in_=w3_laid[g][:]
+                out=w3_codes[:, g, :].bitcast(FP8X4), scales=w3_scales[:, g, :], in_=w3_laid[g]
             )
 
         enc, enc_laid, enc_codes, enc_scales = {}, {}, {}, {}
@@ -347,46 +363,49 @@ def tile_mae_pa_kernel(tc, x_bytes, x_scale, eps, W11, b11, W31, b31, W32, b32, 
             if b == 2:
                 nc.sync.dma_start(out=out_views[2][:, 2 * i : 2 * i + 2, :], in_=z[i][:])
 
-        unused_sum = sums.tile([P, HALF], F32, name="sum0")
-        warm_up(unused_sum, 256)
-        warm_up(unused_sum, 256)
-        spread_scale(0)
-        spread_scale(1)
-        warm_up(unused_sum, 384)
+        unused_bank = psum.tile([P, HALF], F32, name="bank")
+        warm_up(unused_bank, 256)
+        warm_up(unused_bank, 256)
+        for c in range(2):
+            x_widen(0, c, c + 1)
+            x_turn(0, c, c + 1)
+        for r in range(1, 4):
+            x_widen(r)
+            x_turn(r)
         w_vector(0, 0, 0, PASS // 2)
+        x_product(0, 0, 1)
         w_vector(0, 0, PASS // 2, PASS)
-        x_product(0, 0, PASS)
-        x_product(0, PASS, IMAGE)
-        x_product(1)
-        w_scalar(0, 1, 0, PASS // 2)
-        x_turn(0)
-        w_scalar(0, 1, PASS // 2, PASS)
-        x_product(2)
-        x_turn(1)
-        x_product(3)
-        x_turn(2)
-        x_turn(3)
+        x_product(0, 1, 2)
+        for r in range(1, 4):
+            x_product(r)
+        x_widen(4)
+        w_scalar(0, 1, 0, BANK_CHANNELS)
+        w_matmuls(0, 1, BANK_CHANNELS)
+        for r in range(5, 7):
+            x_widen(r)
+        w_empty(0, 1, BANK_CHANNELS)
+        for r in range(4, 7):
+            x_turn(r)
+        x_widen(7)
+        x_turn(7)
         w_quant(0, 0)
-        for c in range(2):
-            w_vector(1, c, BANK_CHANNELS, PASS)
-        w_quant(0, 1)
         x_quant(0)
-        for c in range(2):
-            w_tensor(1, c)
+        w_quant(0, 1)
+        w3_gpsimd(0, 3, 1)
+        w_scalar(1, 0, BANK_CHANNELS, PASS)
 
         for r in range(4, ROWS):
             x_product(r)
         first_stage(0, [
-            [(w_scalar, 2, 0, BANK_CHANNELS, PASS)],
-            [(x_turn, 4)],
-            [(x_turn, 5)],
-            [(x_turn, 6), (w_tensor, 2, 0)],
+            [(w_tensor, 1, 0)],
+            [(w_matmuls, 1, 1), (w_scalar, 2, 0, BANK_CHANNELS, PASS), (w_empty, 1, 1)],
+            [],
+            [(w_tensor, 2, 0)],
         ])
-        for c in range(2):
-            w_quant(1, c)
-        w3_lay(0)
-        w3_lay(1)
+        w_vector(1, 1, BANK_CHANNELS, PASS)
+        w_quant(1, 0)
         w3_quant(0)
+        w_quant(1, 1)
 
         for s in range(1, LAST + 1):
             g, c = divmod(s + 4, 2)
@@ -398,9 +417,7 @@ def tile_mae_pa_kernel(tc, x_bytes, x_scale, eps, W11, b11, W31, b31, W32, b32, 
                 if c == 0:
                     after_bank[0].append((w_tensor, g, c))
                 after_bank[1].append((w_scalar, g, c, tensor_end, scalar_end))
-            if s == 1:
-                after_bank[0].append((x_turn, ROWS - 1))
-            else:
+            if s > 1:
                 after_bank[3].append((second_stage, s - 2))
             if share:
                 after_bank[0].append((enc_lay, nc.scalar.copy, s - 1, 0, share))
@@ -414,7 +431,7 @@ def tile_mae_pa_kernel(tc, x_bytes, x_scale, eps, W11, b11, W31, b31, W32, b32, 
             enc_lay(nc.vector.tensor_copy, s - 1, share, tokens(s - 1))
             if g < GROUPS:
                 w_vector(g, c, scalar_end, PASS)
-            if w3_phase == 0 and w3_group < GROUPS:
+            if w3_phase == 0 and 3 <= w3_group < GROUPS:
                 w3_lay(w3_group)
             if s == 1:
                 w_quant(2, 0)

@@ -36,7 +36,7 @@ HALF0_CLOSED = UNITS.index((0, GROUPS - 1, 0, 4)) + 2
 SCALAR_CHANNELS = (64, 256)
 SCALAR_CHANNELS_STEP_1 = 384
 SCALAR_TAIL_SHARE = 4
-MATMUL_ROWS = (0, 1, 3, 5)
+MATMUL_ROWS = (0, 2)
 
 
 def tile_mae_pa_kernel(tc, x_bytes, x_scale, eps, W11, b11, W31, b31, W32, b32, out_0, out_1, out_2):
@@ -88,21 +88,21 @@ def tile_mae_pa_kernel(tc, x_bytes, x_scale, eps, W11, b11, W31, b31, W32, b32, 
             for g in range(g0, g1):
                 bias1[g] = tile[:, g - g0, :]
 
+        scale_cols = keep.tile([P, 2, 4], F32, name="scale_cols")
         load_x(0, 1)
-        load_w11(0, 0, PASS // 2)
+        nc.sync.dma_start(out=scale_cols[:], in_=x_scale.rearrange("o (c p t) -> p (o c) t", p=P, t=4))
+        scale = keep.tile([P, 2, P, 4], F32, name="scale")
         load_x(1, 2)
-        scale = keep.tile([P, 2, 4], F32, name="scale")
-        nc.sync.dma_start(out=scale[:], in_=x_scale.rearrange("o (c p t) -> p (o c) t", p=P, t=4))
-        load_w11(0, PASS // 2, PASS)
         load_x(2, 4)
-        load_x(4, 6)
-        load_w11(1, 0, PASS // 2)
-        load_w11(1, PASS // 2, PASS)
-        load_x(6, ROWS)
-        load_bias1(0, 2)
+        for c in range(2):
+            load_w11(c, 0, PASS // 2)
+            load_w11(c, PASS // 2, PASS)
         load_w11(0, PASS, 2 * PASS)
-        load_w3(0, 3)
         load_w11(1, PASS, 2 * PASS)
+        load_x(4, 6)
+        load_bias1(0, 2)
+        load_x(6, ROWS)
+        load_w3(0, 3)
         load_w11(0, 2 * PASS, 3 * PASS)
         load_w11(1, 2 * PASS, 3 * PASS)
         load_bias1(2, GROUPS)
@@ -165,9 +165,7 @@ def tile_mae_pa_kernel(tc, x_bytes, x_scale, eps, W11, b11, W31, b31, W32, b32, 
             nc.vector.tensor_tensor(
                 out=x_laid[h][:, c0:c1, P * row : P * (row + 1), :].rearrange("p c n (u e) -> p c n u e", u=2),
                 in0=x_turned[r, c0].rearrange("p u c (n e) -> p c n u e", e=2),
-                in1=scale[:, c0:c1, :].rearrange("p c (u e) -> p c u e", u=2).unsqueeze(2).to_broadcast(
-                    [P, c1 - c0, P, 2, 2]
-                ),
+                in1=scale[:, c0:c1, :, :].rearrange("p c n (u e) -> p c n u e", u=2),
                 op=MULT,
             )
 
@@ -188,10 +186,10 @@ def tile_mae_pa_kernel(tc, x_bytes, x_scale, eps, W11, b11, W31, b31, W32, b32, 
 
         def w_target(g, c):
             if (g, c) not in w_laid:
-                if g == 0:
-                    w_laid[g, c] = keep.tile([P, 2 * PASS], F32, name=f"head_laid{c}", align_bytes=64)
+                if (g, c) == (1, 1):
+                    w_laid[g, c] = keep.tile([P, 2 * PASS], F32, name="head_laid", align_bytes=64)
                 else:
-                    w_laid[g, c] = work.tile([P, 2 * PASS], F32, name="w_laid", bufs=4, align_bytes=64)
+                    w_laid[g, c] = work.tile([P, 2 * PASS], F32, name="w_laid", bufs=5, align_bytes=64)
             return w_laid[g, c]
 
         def w_matmuls(g, c, a=0):
@@ -252,8 +250,8 @@ def tile_mae_pa_kernel(tc, x_bytes, x_scale, eps, W11, b11, W31, b31, W32, b32, 
                 in_=w3_raw[g0, g1][:, g - g0, :, :].rearrange("p w (j m i) -> p w m j i", j=4, i=4),
             )
 
-        def w3_gpsimd(g0, g1, c):
-            tile = keep.tile([P, g1 - g0, 8 * LATENT], BF16, name=f"head_laid{c}", align_bytes=64)
+        def w3_gpsimd(g0, g1):
+            tile = keep.tile([P, g1 - g0, 8 * LATENT], BF16, name="head_laid", align_bytes=64)
             nc.gpsimd.tensor_scalar(
                 out=tile[:].rearrange("p g (w l j) -> p (g w) l j", w=2, j=4),
                 in0=w3_raw[g0, g1][:].rearrange("p g w (j l) -> p (g w) l j", j=4),
@@ -363,49 +361,46 @@ def tile_mae_pa_kernel(tc, x_bytes, x_scale, eps, W11, b11, W31, b31, W32, b32, 
             if b == 2:
                 nc.sync.dma_start(out=out_views[2][:, 2 * i : 2 * i + 2, :], in_=z[i][:])
 
-        unused_bank = psum.tile([P, HALF], F32, name="bank")
+        unused_bank = sums.tile([P, HALF], F32, name="sum0")
         warm_up(unused_bank, 256)
         warm_up(unused_bank, 256)
+        nc.vector.tensor_copy(out=scale[:], in_=scale_cols[:].unsqueeze(2).to_broadcast([P, 2, P, 4]))
         for c in range(2):
             x_widen(0, c, c + 1)
             x_turn(0, c, c + 1)
+            x_product(0, c, c + 1)
         for r in range(1, 4):
             x_widen(r)
             x_turn(r)
-        w_vector(0, 0, 0, PASS // 2)
-        x_product(0, 0, 1)
-        w_vector(0, 0, PASS // 2, PASS)
-        x_product(0, 1, 2)
-        for r in range(1, 4):
             x_product(r)
-        x_widen(4)
-        w_scalar(0, 1, 0, BANK_CHANNELS)
+        w_scalar(0, 0, 0, BANK_CHANNELS)
+        w_scalar(0, 0, BANK_CHANNELS, PASS)
+        w_tensor(0, 1, 0)
         w_matmuls(0, 1, BANK_CHANNELS)
-        for r in range(5, 7):
-            x_widen(r)
+        w_scalar(1, 0, BANK_CHANNELS, PASS)
         w_empty(0, 1, BANK_CHANNELS)
-        for r in range(4, 7):
-            x_turn(r)
-        x_widen(7)
-        x_turn(7)
+        w_tensor(1, 0)
+        w_matmuls(1, 1)
+        x_widen(4)
+        w_empty(1, 1)
+        x_widen(5)
         w_quant(0, 0)
         x_quant(0)
         w_quant(0, 1)
-        w3_gpsimd(0, 3, 1)
-        w_scalar(1, 0, BANK_CHANNELS, PASS)
-
-        for r in range(4, ROWS):
-            x_product(r)
-        first_stage(0, [
-            [(w_tensor, 1, 0)],
-            [(w_matmuls, 1, 1), (w_scalar, 2, 0, BANK_CHANNELS, PASS), (w_empty, 1, 1)],
-            [],
-            [(w_tensor, 2, 0)],
-        ])
         w_vector(1, 1, BANK_CHANNELS, PASS)
         w_quant(1, 0)
-        w3_quant(0)
         w_quant(1, 1)
+        w3_gpsimd(0, 3)
+
+        first_stage(0, [
+            [(x_widen, 6)],
+            [(x_turn, 4), (x_turn, 5), (x_widen, 7)],
+            [(x_turn, 6)],
+            [(x_turn, 7), (w_matmuls, 2, 0), (w_scalar, 2, 0, BANK_CHANNELS, PASS), (w_empty, 2, 0)],
+        ])
+        for r in range(4, ROWS):
+            x_product(r)
+        w3_quant(0)
 
         for s in range(1, LAST + 1):
             g, c = divmod(s + 4, 2)
@@ -428,6 +423,8 @@ def tile_mae_pa_kernel(tc, x_bytes, x_scale, eps, W11, b11, W31, b31, W32, b32, 
             w3_group, w3_phase = divmod(s + 2, 2)
             if s > 1 and (s + 3) // 2 < GROUPS:
                 w_quant(*divmod(s + 3, 2))
+            if s == 1:
+                x_quant(1)
             enc_lay(nc.vector.tensor_copy, s - 1, share, tokens(s - 1))
             if g < GROUPS:
                 w_vector(g, c, scalar_end, PASS)
@@ -435,7 +432,6 @@ def tile_mae_pa_kernel(tc, x_bytes, x_scale, eps, W11, b11, W31, b31, W32, b32, 
                 w3_lay(w3_group)
             if s == 1:
                 w_quant(2, 0)
-                x_quant(1)
             if s == HALF0_CLOSED:
                 add_bias(0)
             if s == HALF0_CLOSED + 1:

@@ -36,7 +36,7 @@ HALF0_CLOSED = UNITS.index((0, GROUPS - 1, 0, 4)) + 2
 SCALAR_CHANNELS = (64, 256)
 SCALAR_CHANNELS_STEP_1 = 384
 SCALAR_TAIL_SHARE = 4
-MATMUL_ROWS = (0, 2)
+MATMUL_ROWS = (0, 2, 4, 6)
 
 
 def tile_mae_pa_kernel(tc, x_bytes, x_scale, eps, W11, b11, W31, b31, W32, b32, out_0, out_1, out_2):
@@ -72,7 +72,7 @@ def tile_mae_pa_kernel(tc, x_bytes, x_scale, eps, W11, b11, W31, b31, W32, b32, 
                 x_raw[r] = tile[:, (r - r0) * IMAGE : (r - r0 + 1) * IMAGE]
 
         def load_w11(c, n0, n1):
-            tile = keep.tile([P, 4, n1 - n0], BF16, name=f"w11_raw{c}_{n0}")
+            tile = keep.tile([P, 4, n1 - n0], BF16, name=f"w11_raw{c}_{n0}", align_bytes=64)
             nc.sync.dma_start(out=tile[:], in_=w11_view[c, :, :, n0:n1])
             w11_raw[c].append((n0, n1, tile))
 
@@ -94,23 +94,24 @@ def tile_mae_pa_kernel(tc, x_bytes, x_scale, eps, W11, b11, W31, b31, W32, b32, 
         scale = keep.tile([P, 2, P, 4], F32, name="scale")
         load_x(1, 2)
         load_x(2, 4)
-        for c in range(2):
-            load_w11(c, 0, PASS // 2)
-            load_w11(c, PASS // 2, PASS)
+        load_w11(0, 0, PASS)
+        load_x(4, 6)
+        load_w11(1, 0, PASS)
+        load_x(6, ROWS)
+        load_bias1(0, 2)
         load_w11(0, PASS, 2 * PASS)
         load_w11(1, PASS, 2 * PASS)
-        load_x(4, 6)
-        load_bias1(0, 2)
-        load_x(6, ROWS)
-        load_w3(0, 3)
+        load_w3(0, 4)
         load_w11(0, 2 * PASS, 3 * PASS)
         load_w11(1, 2 * PASS, 3 * PASS)
         load_bias1(2, GROUPS)
-        for g in range(3, GROUPS, 2):
+        for c in range(2):
+            load_w11(c, 3 * PASS, 4 * PASS)
+        for g in range(4, GROUPS, 2):
             for c in range(2):
-                load_w11(c, g * PASS, min(g + 2, GROUPS) * PASS)
-            if g == 3:
-                load_w3(3, GROUPS)
+                load_w11(c, g * PASS, (g + 2) * PASS)
+            if g == 4:
+                load_w3(4, GROUPS)
         bias3 = keep.tile([P, 2 * LATENT], BF16, name="bias3")
         nc.sync.dma_start(out=bias3[:, :LATENT], in_=b31.partition_broadcast(P))
         nc.sync.dma_start(out=bias3[:, LATENT:], in_=b32.partition_broadcast(P))
@@ -187,7 +188,7 @@ def tile_mae_pa_kernel(tc, x_bytes, x_scale, eps, W11, b11, W31, b31, W32, b32, 
         def w_target(g, c):
             if (g, c) not in w_laid:
                 if (g, c) == (1, 1):
-                    w_laid[g, c] = keep.tile([P, 2 * PASS], F32, name="head_laid", align_bytes=64)
+                    w_laid[g, c] = keep.tile([P, 2 * PASS], F32, name="w11_raw0_0", align_bytes=64)
                 else:
                     w_laid[g, c] = work.tile([P, 2 * PASS], F32, name="w_laid", bufs=5, align_bytes=64)
             return w_laid[g, c]
@@ -228,6 +229,14 @@ def tile_mae_pa_kernel(tc, x_bytes, x_scale, eps, W11, b11, W31, b31, W32, b32, 
         def w_scalar(g, c, a, b):
             w_copy(nc.scalar.copy, g, c, a, b)
 
+        def w_gpsimd(g, c, a, b):
+            target = w_target(g, c)[:].bitcast(BF16).rearrange("p (t m j) -> p m t j", t=4, j=4)
+            nc.gpsimd.tensor_scalar(
+                out=target[:, a // 4 : b // 4, :, :],
+                in0=w_source(g, c, a, b).rearrange("p j (m t) -> p m t j", t=4),
+                scalar1=1.0, scalar2=0.0, op0=MULT, op1=ADD,
+            )
+
         def w_quant(g, c):
             if g not in w_codes:
                 w_codes[g] = work.tile([P, 2, PASS], U32, name="w_codes", bufs=4, align_bytes=64)
@@ -242,23 +251,25 @@ def tile_mae_pa_kernel(tc, x_bytes, x_scale, eps, W11, b11, W31, b31, W32, b32, 
         w3_codes = keep.tile([P, GROUPS, 2 * LATENT], U32, name="w3_codes", align_bytes=64)
         w3_scales = keep.tile([P, GROUPS, 2 * LATENT], U8, name="w3_scales", align_bytes=64)
 
-        def w3_lay(g):
+        def w3_lay(g, w0=0):
             g0, g1 = [k for k in w3_raw if k[0] <= g < k[1]][0]
-            w3_laid[g] = work.tile([P, 8 * LATENT], BF16, name="w3_laid", bufs=1, align_bytes=64)[:]
+            if g not in w3_laid:
+                w3_laid[g] = work.tile([P, 8 * LATENT], BF16, name="w3_laid", bufs=1, align_bytes=64)[:]
             nc.vector.tensor_copy(
-                out=w3_laid[g].rearrange("p (w m i j) -> p w m j i", w=2, i=4, j=4),
-                in_=w3_raw[g0, g1][:, g - g0, :, :].rearrange("p w (j m i) -> p w m j i", j=4, i=4),
+                out=w3_laid[g].rearrange("p (w m i j) -> p w m j i", w=2, i=4, j=4)[:, w0:, :, :, :],
+                in_=w3_raw[g0, g1][:, g - g0, w0:, :].rearrange("p w (j m i) -> p w m j i", j=4, i=4),
             )
 
-        def w3_gpsimd(g0, g1):
-            tile = keep.tile([P, g1 - g0, 8 * LATENT], BF16, name="head_laid", align_bytes=64)
-            nc.gpsimd.tensor_scalar(
-                out=tile[:].rearrange("p g (w l j) -> p (g w) l j", w=2, j=4),
-                in0=w3_raw[g0, g1][:].rearrange("p g w (j l) -> p (g w) l j", j=4),
-                scalar1=1.0, scalar2=0.0, op0=MULT, op1=ADD,
-            )
-            for g in range(g0, g1):
-                w3_laid[g] = tile[:, g - g0, :]
+        def w3_gpsimd():
+            tile = keep.tile([P, 4, 8 * LATENT], BF16, name="w11_raw0_0", align_bytes=64)
+            for w in range(2):
+                nc.gpsimd.tensor_scalar(
+                    out=tile[:, : 4 - w, :].rearrange("p g (w l j) -> p g w l j", w=2, j=4)[:, :, w, :, :],
+                    in0=w3_raw[0, 4][:, : 4 - w, w, :].rearrange("p g (j l) -> p g l j", j=4),
+                    scalar1=1.0, scalar2=0.0, op0=MULT, op1=ADD,
+                )
+            for g in range(4):
+                w3_laid[g] = tile[:, g, :]
 
         def w3_quant(g):
             nc.vector.quantize_mx(
@@ -373,34 +384,33 @@ def tile_mae_pa_kernel(tc, x_bytes, x_scale, eps, W11, b11, W31, b31, W32, b32, 
             x_widen(r)
             x_turn(r)
             x_product(r)
-        w_scalar(0, 0, 0, BANK_CHANNELS)
-        w_scalar(0, 0, BANK_CHANNELS, PASS)
-        w_tensor(0, 1, 0)
-        w_matmuls(0, 1, BANK_CHANNELS)
-        w_scalar(1, 0, BANK_CHANNELS, PASS)
-        w_empty(0, 1, BANK_CHANNELS)
-        w_tensor(1, 0)
-        w_matmuls(1, 1)
+        w_gpsimd(0, 0, 0, PASS)
+        w_gpsimd(0, 1, 0, 128)
         x_widen(4)
-        w_empty(1, 1)
+        x_turn(4)
         x_widen(5)
+        w_matmuls(0, 1, BANK_CHANNELS)
+        w_scalar(0, 1, 128, BANK_CHANNELS)
+        x_turn(5)
+        x_widen(6)
+        x_widen(7)
+        w_empty(0, 1, BANK_CHANNELS)
+        w_matmuls(1, 0)
+        x_turn(6)
+        x_turn(7)
+        w_scalar(1, 0, BANK_CHANNELS, PASS)
+        w_empty(1, 0)
+        w_scalar(1, 1, 0, 128)
         w_quant(0, 0)
         x_quant(0)
         w_quant(0, 1)
-        w_vector(1, 1, BANK_CHANNELS, PASS)
+        first_stage(0, [[], [], [], []])
+        w_vector(1, 1, 128, PASS)
         w_quant(1, 0)
         w_quant(1, 1)
-        w3_gpsimd(0, 3)
-
-        first_stage(0, [
-            [(x_widen, 6)],
-            [(x_turn, 4), (x_turn, 5), (x_widen, 7)],
-            [(x_turn, 6)],
-            [(x_turn, 7), (w_matmuls, 2, 0), (w_scalar, 2, 0, BANK_CHANNELS, PASS), (w_empty, 2, 0)],
-        ])
+        w3_gpsimd()
         for r in range(4, ROWS):
             x_product(r)
-        w3_quant(0)
 
         for s in range(1, LAST + 1):
             g, c = divmod(s + 4, 2)
@@ -408,13 +418,19 @@ def tile_mae_pa_kernel(tc, x_bytes, x_scale, eps, W11, b11, W31, b31, W32, b32, 
             scalar_end = tensor_end + (SCALAR_CHANNELS_STEP_1 if s == 1 else SCALAR_CHANNELS[c])
             share = tokens(s - 1) // SCALAR_TAIL_SHARE if s >= len(WIDE_UNITS) else 0
             after_bank = [[], [], [], []]
+            if s == 1:
+                share = 256
+                after_bank[3] = [(w_matmuls, 2, 0, 0), (enc_lay, nc.scalar.copy, 0, 0, share), (w_empty, 2, 0, 0), (w_tensor, 2, 0, BANK_CHANNELS), (w_tensor, 2, 1, 0)]
+                tensor_end, scalar_end = BANK_CHANNELS, PASS
+            if s == 2:
+                scalar_end = BANK_CHANNELS + 64
             if g < GROUPS:
                 if c == 0:
                     after_bank[0].append((w_tensor, g, c))
-                after_bank[1].append((w_scalar, g, c, tensor_end, scalar_end))
+                after_bank[3 if s == 1 else 1].append((w_scalar, g, c, tensor_end, scalar_end))
             if s > 1:
                 after_bank[3].append((second_stage, s - 2))
-            if share:
+            if share and s > 1:
                 after_bank[0].append((enc_lay, nc.scalar.copy, s - 1, 0, share))
             if s == LAST:
                 after_bank[3].append((mu_sigma, 0))
@@ -425,11 +441,12 @@ def tile_mae_pa_kernel(tc, x_bytes, x_scale, eps, W11, b11, W31, b31, W32, b32, 
                 w_quant(*divmod(s + 3, 2))
             if s == 1:
                 x_quant(1)
+                w3_quant(0)
             enc_lay(nc.vector.tensor_copy, s - 1, share, tokens(s - 1))
-            if g < GROUPS:
+            if g < GROUPS and scalar_end < PASS:
                 w_vector(g, c, scalar_end, PASS)
             if w3_phase == 0 and 3 <= w3_group < GROUPS:
-                w3_lay(w3_group)
+                w3_lay(w3_group, 1 if w3_group == 3 else 0)
             if s == 1:
                 w_quant(2, 0)
             if s == HALF0_CLOSED:

@@ -37,6 +37,11 @@ SCALAR_CHANNELS = (64, 256)
 SCALAR_CHANNELS_STEP_1 = 384
 SCALAR_TAIL_SHARE = 4
 MATMUL_ROWS = (0, 2, 4, 6)
+VECTOR_UNITS = (2, 4, 6, 8, 10)
+GPSIMD_TOKENS = 384
+TENSOR_CHANNELS = 192
+SCALAR_PASS1 = 480
+SCALAR_PASS1_FIRST = 384
 
 
 def tile_mae_pa_kernel(tc, x_bytes, x_scale, eps, W11, b11, W31, b31, W32, b32, out_0, out_1, out_2):
@@ -162,7 +167,7 @@ def tile_mae_pa_kernel(tc, x_bytes, x_scale, eps, W11, b11, W31, b31, W32, b32, 
         def x_product(r, c0=0, c1=2):
             h, row = divmod(r, 4)
             if h not in x_laid:
-                x_laid[h] = work.tile([P, 2, HALF, 4], BF16, name="x_laid", bufs=2, align_bytes=64)
+                x_laid[h] = keep.tile([P, 2, HALF, 4], BF16, name=f"x_laid{h}", align_bytes=64)
             nc.vector.tensor_tensor(
                 out=x_laid[h][:, c0:c1, P * row : P * (row + 1), :].rearrange("p c n (u e) -> p c n u e", u=2),
                 in0=x_turned[r, c0].rearrange("p u c (n e) -> p c n u e", e=2),
@@ -193,23 +198,24 @@ def tile_mae_pa_kernel(tc, x_bytes, x_scale, eps, W11, b11, W31, b31, W32, b32, 
                     w_laid[g, c] = work.tile([P, 2 * PASS], F32, name="w_laid", bufs=5, align_bytes=64)
             return w_laid[g, c]
 
-        def w_matmuls(g, c, a=0):
+        def w_matmuls(g, c, a=0, width=BANK_CHANNELS):
             w_banks[g, c, a] = bank = psum.tile([P, 2 * BANK_CHANNELS], F32, name="bank")
-            for n0 in range(0, BANK_CHANNELS, P):
+            for n0 in range(0, width, P):
+                n1 = min(n0 + P, width)
                 nc.tensor.matmul(
-                    out=bank[:, 2 * n0 : 2 * (n0 + P)].bitcast(BF16),
+                    out=bank[:, 2 * n0 : 2 * n1].bitcast(BF16),
                     lhsT=ident_bf[:],
-                    rhs=w_source(g, c, a + n0, a + n0 + P).rearrange("p j n -> p n j"),
+                    rhs=w_source(g, c, a + n0, a + n1).rearrange("p j n -> p n j"),
                     start=True,
                     stop=True,
                 )
 
-        def w_empty(g, c, a=0):
+        def w_empty(g, c, a=0, width=BANK_CHANNELS):
             nc.scalar.copy(
                 out=w_target(g, c)[:].rearrange("p (t m u) -> p t m u", t=4, u=2)[
-                    :, :, a // 4 : (a + BANK_CHANNELS) // 4, :
+                    :, :, a // 4 : (a + width) // 4, :
                 ],
-                in_=w_banks[g, c, a][:].rearrange("p (m t u) -> p t m u", t=4, u=2),
+                in_=w_banks[g, c, a][:, : 2 * width].rearrange("p (m t u) -> p t m u", t=4, u=2),
             )
 
         def w_tensor(g, c, a=0):
@@ -303,9 +309,52 @@ def tile_mae_pa_kernel(tc, x_bytes, x_scale, eps, W11, b11, W31, b31, W32, b32, 
                 for job, *args in after_bank[t]:
                     job(*args)
 
-        def enc_lay(engine_copy, s, a, b):
+        def first_stage_rows(s):
+            h, g, row0, rows = UNITS[s]
+            enc[s] = work.tile([P, tokens(s), 4], BF16, name="enc", bufs=3)
+            for r in range(rows):
+                cols = slice(P * (row0 + r), P * (row0 + r + 1))
+                bank = psum.tile([P, 4, P], F32, name="bank")
+                for t in range(4):
+                    for c in range(2):
+                        nc.tensor.matmul_mx(
+                            out=bank[:, t, :],
+                            lhsT=w_codes[g][:, c, P * t : P * (t + 1)].bitcast(FP8X4),
+                            lhsT_scale=w_scales[g][:, c, P * t : P * (t + 1)],
+                            rhs=x_codes[h][:, c, cols].bitcast(FP8X4),
+                            rhs_scale=x_scales[h][:, c, cols],
+                            start=(c == 0),
+                            stop=(c == 1),
+                        )
+                nc.vector.tensor_tensor(
+                    out=enc[s][:, P * r : P * (r + 1), :],
+                    in0=bank[:].rearrange("p t n -> p n t"),
+                    in1=bias1[g].unsqueeze(1).to_broadcast([P, P, 4]),
+                    op=ADD,
+                )
+
+        def laid_tile(s):
             if s not in enc_laid:
-                enc_laid[s] = work.tile([P, 4 * tokens(s)], BF16, name="enc_laid", bufs=3, align_bytes=64)
+                if s <= VECTOR_UNITS[-1]:
+                    enc_laid[s] = keep.tile([P, 4 * HALF], BF16, name="x_laid0", align_bytes=64)
+                else:
+                    enc_laid[s] = work.tile([P, 4 * tokens(s)], BF16, name="enc_laid", bufs=3, align_bytes=64)
+            return enc_laid[s]
+
+        def enc_relu(s):
+            nc.vector.tensor_scalar(
+                out=laid_tile(s)[:], in0=enc[s][:].rearrange("p n t -> p (n t)"), scalar1=0.0, scalar2=None, op0=MAX
+            )
+
+        def enc_gpsimd(s, a, b):
+            nc.gpsimd.tensor_scalar(
+                out=laid_tile(s)[:, 4 * a : 4 * b].rearrange("p (n t) -> p n t", t=4),
+                in0=enc[s][:, :, a:b].rearrange("p t n -> p n t"),
+                scalar1=1.0, scalar2=0.0, op0=MULT, op1=ADD,
+            )
+
+        def enc_lay(engine_copy, s, a, b):
+            laid_tile(s)
             engine_copy(
                 out=enc_laid[s][:, 4 * a : 4 * b].rearrange("p (m i t) -> p m t i", i=4, t=4),
                 in_=enc[s][:, :, a:b].rearrange("p t (m i) -> p m t i", i=4),
@@ -412,43 +461,61 @@ def tile_mae_pa_kernel(tc, x_bytes, x_scale, eps, W11, b11, W31, b31, W32, b32, 
         for r in range(4, ROWS):
             x_product(r)
 
-        for s in range(1, LAST + 1):
-            g, c = divmod(s + 4, 2)
-            tensor_end = BANK_CHANNELS if c == 0 else 0
-            scalar_end = tensor_end + (SCALAR_CHANNELS_STEP_1 if s == 1 else SCALAR_CHANNELS[c])
+        first_stage(1, [[], [], [], [
+            (w_matmuls, 2, 0, 0), (w_scalar, 2, 1, BANK_CHANNELS, PASS), (w_empty, 2, 0, 0),
+            (w_tensor, 2, 0, BANK_CHANNELS), (w_tensor, 2, 1, 0),
+        ]])
+        enc_lay(nc.vector.tensor_copy, 0, 0, HALF)
+        x_quant(1)
+        w_quant(2, 0)
+        w3_quant(0)
+        w3_quant(1)
+        enc_quant(0, 0, HALF)
+        w_quant(2, 1)
+
+        for s in VECTOR_UNITS:
+            g = s // 2 + 2
+            share = SCALAR_PASS1_FIRST if s == 2 else SCALAR_PASS1
+            w_matmuls(g, 0, 0, TENSOR_CHANNELS)
+            if s > 2:
+                second_stage(s - 3)
+            w_scalar(g, 0, TENSOR_CHANNELS, PASS)
+            w_empty(g, 0, 0, TENSOR_CHANNELS)
+            w_scalar(g, 1, 0, share)
+            enc_gpsimd(s - 1, 0, GPSIMD_TOKENS)
+            first_stage_rows(s)
+            second_stage(s - 2)
+            enc_lay(nc.vector.tensor_copy, s - 1, GPSIMD_TOKENS, HALF)
+            if share < PASS:
+                w_vector(g, 1, share, PASS)
+            w_quant(g, 0)
+            enc_quant(s - 1, 0, HALF)
+            first_stage(s + 1, [[], [], [], [(second_stage, s - 1)] if s == VECTOR_UNITS[-1] else []])
+            if g - 1 >= 3:
+                w3_lay(g - 1, 1 if g - 1 == 3 else 0)
+            else:
+                w3_quant(g - 1)
+            enc_relu(s)
+            if g - 1 >= 3:
+                w3_quant(g - 1)
+            if s == VECTOR_UNITS[-1] or g - 1 < 3:
+                w_quant(g, 1)
+                enc_quant(s, 0, HALF)
+            else:
+                enc_quant(s, 0, HALF)
+                w_quant(g, 1)
+
+        for s in range(VECTOR_UNITS[-1] + 2, LAST + 1):
             share = tokens(s - 1) // SCALAR_TAIL_SHARE if s >= len(WIDE_UNITS) else 0
-            after_bank = [[], [], [], []]
-            if s == 1:
-                share = 256
-                after_bank[3] = [(w_matmuls, 2, 0, 0), (enc_lay, nc.scalar.copy, 0, 0, share), (w_empty, 2, 0, 0), (w_tensor, 2, 0, BANK_CHANNELS), (w_tensor, 2, 1, 0)]
-                tensor_end, scalar_end = BANK_CHANNELS, PASS
-            if s == 2:
-                scalar_end = BANK_CHANNELS + 64
-            if g < GROUPS:
-                if c == 0:
-                    after_bank[0].append((w_tensor, g, c))
-                after_bank[3 if s == 1 else 1].append((w_scalar, g, c, tensor_end, scalar_end))
-            if s > 1:
-                after_bank[3].append((second_stage, s - 2))
-            if share and s > 1:
+            after_bank = [[], [], [], [(second_stage, s - 2)]]
+            if share:
                 after_bank[0].append((enc_lay, nc.scalar.copy, s - 1, 0, share))
             if s == LAST:
                 after_bank[3].append((mu_sigma, 0))
             first_stage(s, after_bank)
-
-            w3_group, w3_phase = divmod(s + 2, 2)
-            if s > 1 and (s + 3) // 2 < GROUPS:
-                w_quant(*divmod(s + 3, 2))
-            if s == 1:
-                x_quant(1)
-                w3_quant(0)
             enc_lay(nc.vector.tensor_copy, s - 1, share, tokens(s - 1))
-            if g < GROUPS and scalar_end < PASS:
-                w_vector(g, c, scalar_end, PASS)
-            if w3_phase == 0 and 3 <= w3_group < GROUPS:
-                w3_lay(w3_group, 1 if w3_group == 3 else 0)
-            if s == 1:
-                w_quant(2, 0)
+            if s == 12:
+                w3_lay(GROUPS - 1)
             if s == HALF0_CLOSED:
                 add_bias(0)
             if s == HALF0_CLOSED + 1:
@@ -456,11 +523,9 @@ def tile_mae_pa_kernel(tc, x_bytes, x_scale, eps, W11, b11, W31, b31, W32, b32, 
                 z_noise(1)
             if s == HALF0_CLOSED + 2:
                 z_add_mu(1)
-            if w3_phase == 1 and w3_group == GROUPS - 1:
-                w3_quant(w3_group)
+            if s == 13:
+                w3_quant(GROUPS - 1)
             enc_quant(s - 1, 0, tokens(s - 1))
-            if w3_phase == 1 and w3_group < GROUPS - 1:
-                w3_quant(w3_group)
             if s == HALF0_CLOSED:
                 add_bias(1)
             if s == HALF0_CLOSED + 1:

@@ -38,10 +38,10 @@ SCALAR_CHANNELS_STEP_1 = 384
 SCALAR_TAIL_SHARE = 4
 MATMUL_ROWS = (0, 2, 4, 6)
 VECTOR_UNITS = (2, 4, 6, 8, 10)
-GPSIMD_TOKENS = 384
-TENSOR_CHANNELS = 192
+GPSIMD_TOKENS = 448
+TENSOR_CHANNELS = 160
 SCALAR_PASS1 = 480
-SCALAR_PASS1_FIRST = 384
+SCALAR_PASS1_FIRST = 448
 
 
 def tile_mae_pa_kernel(tc, x_bytes, x_scale, eps, W11, b11, W31, b31, W32, b32, out_0, out_1, out_2):
@@ -170,18 +170,17 @@ def tile_mae_pa_kernel(tc, x_bytes, x_scale, eps, W11, b11, W31, b31, W32, b32, 
                 x_laid[h] = keep.tile([P, 2, HALF, 4], BF16, name=f"x_laid{h}", align_bytes=64)
             nc.vector.tensor_tensor(
                 out=x_laid[h][:, c0:c1, P * row : P * (row + 1), :].rearrange("p c n (u e) -> p c n u e", u=2),
-                in0=x_turned[r, c0].rearrange("p u c (n e) -> p c n u e", e=2),
-                in1=scale[:, c0:c1, :, :].rearrange("p c n (u e) -> p c n u e", u=2),
+                in0=scale[:, c0:c1, :, :].rearrange("p c n (u e) -> p c n u e", u=2),
+                in1=x_turned[r, c0].rearrange("p u c (n e) -> p c n u e", e=2),
                 op=MULT,
             )
 
         def x_quant(h):
-            for c in range(2):
-                nc.vector.quantize_mx(
-                    out=x_codes[h][:, c, :].bitcast(FP8X4),
-                    scales=x_scales[h][:, c, :],
-                    in_=x_laid[h][:, c, :, :].rearrange("p n t -> p (n t)"),
-                )
+            nc.vector.quantize_mx(
+                out=x_codes[h][:].rearrange("p c n -> p (c n)").bitcast(FP8X4),
+                scales=x_scales[h][:].rearrange("p c n -> p (c n)"),
+                in_=x_laid[h][:].rearrange("p c n t -> p (c n t)"),
+            )
 
         w_laid, w_banks, w_codes, w_scales = {}, {}, {}, {}
 
@@ -257,13 +256,13 @@ def tile_mae_pa_kernel(tc, x_bytes, x_scale, eps, W11, b11, W31, b31, W32, b32, 
         w3_codes = keep.tile([P, GROUPS, 2 * LATENT], U32, name="w3_codes", align_bytes=64)
         w3_scales = keep.tile([P, GROUPS, 2 * LATENT], U8, name="w3_scales", align_bytes=64)
 
-        def w3_lay(g, w0=0):
+        def w3_lay(g, w0=0, w1=2):
             g0, g1 = [k for k in w3_raw if k[0] <= g < k[1]][0]
             if g not in w3_laid:
                 w3_laid[g] = work.tile([P, 8 * LATENT], BF16, name="w3_laid", bufs=1, align_bytes=64)[:]
             nc.vector.tensor_copy(
-                out=w3_laid[g].rearrange("p (w m i j) -> p w m j i", w=2, i=4, j=4)[:, w0:, :, :, :],
-                in_=w3_raw[g0, g1][:, g - g0, w0:, :].rearrange("p w (j m i) -> p w m j i", j=4, i=4),
+                out=w3_laid[g].rearrange("p (w m i j) -> p w m j i", w=2, i=4, j=4)[:, w0:w1, :, :, :],
+                in_=w3_raw[g0, g1][:, g - g0, w0:w1, :].rearrange("p w (j m i) -> p w m j i", j=4, i=4),
             )
 
         def w3_gpsimd():
@@ -328,8 +327,8 @@ def tile_mae_pa_kernel(tc, x_bytes, x_scale, eps, W11, b11, W31, b31, W32, b32, 
                         )
                 nc.vector.tensor_tensor(
                     out=enc[s][:, P * r : P * (r + 1), :],
-                    in0=bank[:].rearrange("p t n -> p n t"),
-                    in1=bias1[g].unsqueeze(1).to_broadcast([P, P, 4]),
+                    in0=bias1[g].unsqueeze(1).to_broadcast([P, P, 4]),
+                    in1=bank[:].rearrange("p t n -> p n t"),
                     op=ADD,
                 )
 
@@ -388,22 +387,26 @@ def tile_mae_pa_kernel(tc, x_bytes, x_scale, eps, W11, b11, W31, b31, W32, b32, 
                     stop=(g == GROUPS - 1 and r % 2 == 1),
                 )
 
-        biased, z = {}, {}
+        biased, both, z = {}, {}, {}
         out_views = [o.rearrange("(p r) l -> p r l", r=ROWS) for o in (out_0, out_1, out_2)]
 
         def add_bias(i, a=0, b=2):
             if i not in biased:
                 biased[i] = work.tile([P, 2, 2 * LATENT], F32, name="biased", bufs=3)
             nc.vector.tensor_tensor(
-                out=biased[i][:, a:b, :], in0=acc[i][:, a:b, :],
-                in1=bias3[:].unsqueeze(1).to_broadcast([P, b - a, 2 * LATENT]), op=ADD,
+                out=biased[i][:, a:b, :], in0=bias3[:].unsqueeze(1).to_broadcast([P, b - a, 2 * LATENT]),
+                in1=acc[i][:, a:b, :], op=ADD,
             )
 
-        def mu_sigma(i):
-            both = work.tile([P, 2, 2, LATENT], F32, name="mu_sigma", bufs=4)
-            nc.scalar.activation(out=both[:], in_=biased[i][:].rearrange("p r (w l) -> p w r l", w=2), func=RELU)
-            for w in range(2):
-                nc.sync.dma_start(out=out_views[w][:, 2 * i : 2 * i + 2, :], in_=both[:, w, :, :])
+        def mu_sigma(i, a=0, b=2, queue=nc.sync):
+            if i not in both:
+                both[i] = work.tile([P, 2, 2, LATENT], F32, name="mu_sigma", bufs=4)
+            nc.scalar.activation(
+                out=both[i][:, :, a:b, :], in_=biased[i][:, a:b, :].rearrange("p r (w l) -> p w r l", w=2), func=RELU
+            )
+            if b == 2:
+                for w in range(2):
+                    queue.dma_start(out=out_views[w][:, 2 * i : 2 * i + 2, :], in_=both[i][:, w, :, :])
 
         def z_noise(i, a=0, b=2):
             if i not in z:
@@ -506,16 +509,14 @@ def tile_mae_pa_kernel(tc, x_bytes, x_scale, eps, W11, b11, W31, b31, W32, b32, 
                 w_quant(g, 1)
 
         for s in range(VECTOR_UNITS[-1] + 2, LAST + 1):
-            share = tokens(s - 1) // SCALAR_TAIL_SHARE if s >= len(WIDE_UNITS) else 0
+            share = {13:96,14:0,15:96,16:64}.get(s - 1, 0)
             after_bank = [[], [], [], [(second_stage, s - 2)]]
             if share:
                 after_bank[0].append((enc_lay, nc.scalar.copy, s - 1, 0, share))
-            if s == LAST:
-                after_bank[3].append((mu_sigma, 0))
             first_stage(s, after_bank)
             enc_lay(nc.vector.tensor_copy, s - 1, share, tokens(s - 1))
-            if s == 12:
-                w3_lay(GROUPS - 1)
+            if s in (12, 13):
+                w3_lay(GROUPS - 1, s - 12, s - 11)
             if s == HALF0_CLOSED:
                 add_bias(0)
             if s == HALF0_CLOSED + 1:
@@ -523,7 +524,7 @@ def tile_mae_pa_kernel(tc, x_bytes, x_scale, eps, W11, b11, W31, b31, W32, b32, 
                 z_noise(1)
             if s == HALF0_CLOSED + 2:
                 z_add_mu(1)
-            if s == 13:
+            if s == 14:
                 w3_quant(GROUPS - 1)
             enc_quant(s - 1, 0, tokens(s - 1))
             if s == HALF0_CLOSED:
@@ -531,22 +532,24 @@ def tile_mae_pa_kernel(tc, x_bytes, x_scale, eps, W11, b11, W31, b31, W32, b32, 
             if s == HALF0_CLOSED + 1:
                 z_add_mu(0)
 
+        mu_sigma(0)
         enc_lay(nc.scalar.copy, LAST, P, 2 * P)
-        add_bias(2)
+        enc_lay(nc.vector.tensor_copy, LAST, 0, P)
         second_stage(LAST - 1)
         unused_bank = psum.tile([P, HALF], F32, name="bank")
         warm_up(unused_bank, 256)
+        add_bias(2)
         mu_sigma(1)
-        mu_sigma(2)
-        enc_lay(nc.vector.tensor_copy, LAST, 0, P)
-        z_noise(2)
         for r in range(2):
             enc_quant(LAST, P * r, P * (r + 1))
         second_stage(LAST)
+        z_noise(2)
+        mu_sigma(2)
         z_add_mu(2)
+        add_bias(3, 0, 1)
+        add_bias(3, 1, 2)
         for r in range(2):
-            add_bias(3, r, r + 1)
-        mu_sigma(3)
+            mu_sigma(3, r, r + 1, nc.scalar)
         for r in range(2):
             z_noise(3, r, r + 1)
         for r in range(2):

@@ -38,7 +38,7 @@ SCALAR_CHANNELS_STEP_1 = 384
 SCALAR_TAIL_SHARE = 4
 MATMUL_ROWS = (0, 2, 4, 6)
 VECTOR_UNITS = (2, 4, 6, 8, 10)
-GPSIMD_TOKENS = 448
+GPSIMD_TOKENS = 464
 TENSOR_CHANNELS = 160
 SCALAR_PASS1 = 480
 SCALAR_PASS1_FIRST = 448
@@ -261,8 +261,8 @@ def tile_mae_pa_kernel(tc, x_bytes, x_scale, eps, W11, b11, W31, b31, W32, b32, 
             if g not in w3_laid:
                 w3_laid[g] = work.tile([P, 8 * LATENT], BF16, name="w3_laid", bufs=1, align_bytes=64)[:]
             nc.vector.tensor_copy(
-                out=w3_laid[g].rearrange("p (w m i j) -> p w m j i", w=2, i=4, j=4)[:, w0:w1, :, :, :],
-                in_=w3_raw[g0, g1][:, g - g0, w0:w1, :].rearrange("p w (j m i) -> p w m j i", j=4, i=4),
+                out=w3_laid[g].rearrange("p (w m i j) -> p w m j i", w=2, i=2, j=4)[:, w0:w1, :, :, :],
+                in_=w3_raw[g0, g1][:, g - g0, w0:w1, :].rearrange("p w (j m i) -> p w m j i", j=4, i=2),
             )
 
         def w3_gpsimd():
@@ -347,16 +347,16 @@ def tile_mae_pa_kernel(tc, x_bytes, x_scale, eps, W11, b11, W31, b31, W32, b32, 
 
         def enc_gpsimd(s, a, b):
             nc.gpsimd.tensor_scalar(
-                out=laid_tile(s)[:, 4 * a : 4 * b].rearrange("p (n t) -> p n t", t=4),
-                in0=enc[s][:, :, a:b].rearrange("p t n -> p n t"),
+                out=laid_tile(s)[:, 4 * a : 4 * b].rearrange("p (m i t) -> p m t i", t=4, i=2),
+                in0=enc[s][:, :, a:b].rearrange("p t (m i) -> p m t i", i=2),
                 scalar1=1.0, scalar2=0.0, op0=MULT, op1=ADD,
             )
 
         def enc_lay(engine_copy, s, a, b):
             laid_tile(s)
             engine_copy(
-                out=enc_laid[s][:, 4 * a : 4 * b].rearrange("p (m i t) -> p m t i", i=4, t=4),
-                in_=enc[s][:, :, a:b].rearrange("p t (m i) -> p m t i", i=4),
+                out=enc_laid[s][:, 4 * a : 4 * b].rearrange("p (m i t) -> p m t i", i=2, t=4),
+                in_=enc[s][:, :, a:b].rearrange("p t (m i) -> p m t i", i=2),
             )
 
         def enc_quant(s, a, b):

@@ -15,7 +15,6 @@ FP8X4 = mybir.dt.float8_e4m3fn_x4
 ADD = mybir.AluOpType.add
 MULT = mybir.AluOpType.mult
 MAX = mybir.AluOpType.max
-NOT_EQUAL = mybir.AluOpType.not_equal
 RELU = mybir.ActivationFunctionType.Relu
 COPY = mybir.ActivationFunctionType.Copy
 
@@ -33,15 +32,15 @@ UNITS = WIDE_UNITS + [(1, g, r, 2) for r in (0, 2) for g in (GROUPS - 2, GROUPS 
 LAST = len(UNITS) - 1
 HALF0_CLOSED = UNITS.index((0, GROUPS - 1, 0, 4)) + 2
 
-SCALAR_CHANNELS = (64, 256)
-SCALAR_CHANNELS_STEP_1 = 384
-SCALAR_TAIL_SHARE = 4
-MATMUL_ROWS = (0, 2, 4, 6)
-VECTOR_UNITS = (2, 4, 6, 8, 10)
-GPSIMD_TOKENS = 464
+W3_FIRST = 4
+
+VECTOR_UNITS = range(2, 2 * GROUPS - 5, 2)
+GPSIMD_TOKENS = 448
 TENSOR_CHANNELS = 160
-SCALAR_PASS1 = 480
-SCALAR_PASS1_FIRST = 448
+SCALAR_CHANNELS = 480
+HEAD_CHANNELS = 128
+SCALAR_TAIL_SHARE = 4
+MATMUL_ROWS = range(0, ROWS, 2)
 
 
 def tile_mae_pa_kernel(tc, x_bytes, x_scale, eps, W11, b11, W31, b31, W32, b32, out_0, out_1, out_2):
@@ -103,10 +102,10 @@ def tile_mae_pa_kernel(tc, x_bytes, x_scale, eps, W11, b11, W31, b31, W32, b32, 
         load_x(4, 6)
         load_w11(1, 0, PASS)
         load_x(6, ROWS)
-        load_bias1(0, 2)
         load_w11(0, PASS, 2 * PASS)
         load_w11(1, PASS, 2 * PASS)
-        load_w3(0, 4)
+        load_bias1(0, 2)
+        load_w3(0, W3_FIRST)
         load_w11(0, 2 * PASS, 3 * PASS)
         load_w11(1, 2 * PASS, 3 * PASS)
         load_bias1(2, GROUPS)
@@ -116,7 +115,7 @@ def tile_mae_pa_kernel(tc, x_bytes, x_scale, eps, W11, b11, W31, b31, W32, b32, 
             for c in range(2):
                 load_w11(c, g * PASS, (g + 2) * PASS)
             if g == 4:
-                load_w3(4, GROUPS)
+                load_w3(W3_FIRST, GROUPS)
         bias3 = keep.tile([P, 2 * LATENT], BF16, name="bias3")
         nc.sync.dma_start(out=bias3[:, :LATENT], in_=b31.partition_broadcast(P))
         nc.sync.dma_start(out=bias3[:, LATENT:], in_=b32.partition_broadcast(P))
@@ -266,14 +265,15 @@ def tile_mae_pa_kernel(tc, x_bytes, x_scale, eps, W11, b11, W31, b31, W32, b32, 
             )
 
         def w3_gpsimd():
-            tile = keep.tile([P, 4, 8 * LATENT], BF16, name="w11_raw0_0", align_bytes=64)
+            tile = keep.tile([P, W3_FIRST, 8 * LATENT], BF16, name="w11_raw0_0", align_bytes=64)
             for w in range(2):
+                groups = W3_FIRST - w
                 nc.gpsimd.tensor_scalar(
-                    out=tile[:, : 4 - w, :].rearrange("p g (w l j) -> p g w l j", w=2, j=4)[:, :, w, :, :],
-                    in0=w3_raw[0, 4][:, : 4 - w, w, :].rearrange("p g (j l) -> p g l j", j=4),
+                    out=tile[:, :groups, :].rearrange("p g (w l j) -> p g w l j", w=2, j=4)[:, :, w, :, :],
+                    in0=w3_raw[0, W3_FIRST][:, :groups, w, :].rearrange("p g (j l) -> p g l j", j=4),
                     scalar1=1.0, scalar2=0.0, op0=MULT, op1=ADD,
                 )
-            for g in range(4):
+            for g in range(W3_FIRST):
                 w3_laid[g] = tile[:, g, :]
 
         def w3_quant(g):
@@ -286,7 +286,7 @@ def tile_mae_pa_kernel(tc, x_bytes, x_scale, eps, W11, b11, W31, b31, W32, b32, 
         def tokens(s):
             return P * UNITS[s][3]
 
-        def first_stage(s, after_bank):
+        def first_stage(s, scalar_share=0):
             h, g, row0, rows = UNITS[s]
             cols = slice(P * row0, P * (row0 + rows))
             enc[s] = work.tile([P, 4, tokens(s)], BF16, name="enc", bufs=3)
@@ -305,8 +305,8 @@ def tile_mae_pa_kernel(tc, x_bytes, x_scale, eps, W11, b11, W31, b31, W32, b32, 
                 nc.scalar.activation(
                     out=enc[s][:, t, :], in_=bank[:, : tokens(s)], func=RELU, bias=bias1[g][:, t : t + 1]
                 )
-                for job, *args in after_bank[t]:
-                    job(*args)
+                if t == 0 and scalar_share:
+                    enc_lay(nc.scalar.copy, s - 1, 0, scalar_share)
 
         def first_stage_rows(s):
             h, g, row0, rows = UNITS[s]
@@ -347,8 +347,8 @@ def tile_mae_pa_kernel(tc, x_bytes, x_scale, eps, W11, b11, W31, b31, W32, b32, 
 
         def enc_gpsimd(s, a, b):
             nc.gpsimd.tensor_scalar(
-                out=laid_tile(s)[:, 4 * a : 4 * b].rearrange("p (m i t) -> p m t i", t=4, i=2),
-                in0=enc[s][:, :, a:b].rearrange("p t (m i) -> p m t i", i=2),
+                out=laid_tile(s)[:, 4 * a : 4 * b].rearrange("p (n t) -> p n t", t=4),
+                in0=enc[s][:, :, a:b].rearrange("p t n -> p n t"),
                 scalar1=1.0, scalar2=0.0, op0=MULT, op1=ADD,
             )
 
@@ -437,12 +437,12 @@ def tile_mae_pa_kernel(tc, x_bytes, x_scale, eps, W11, b11, W31, b31, W32, b32, 
             x_turn(r)
             x_product(r)
         w_gpsimd(0, 0, 0, PASS)
-        w_gpsimd(0, 1, 0, 128)
+        w_gpsimd(0, 1, 0, HEAD_CHANNELS)
         x_widen(4)
         x_turn(4)
         x_widen(5)
         w_matmuls(0, 1, BANK_CHANNELS)
-        w_scalar(0, 1, 128, BANK_CHANNELS)
+        w_scalar(0, 1, HEAD_CHANNELS, BANK_CHANNELS)
         x_turn(5)
         x_widen(6)
         x_widen(7)
@@ -452,22 +452,24 @@ def tile_mae_pa_kernel(tc, x_bytes, x_scale, eps, W11, b11, W31, b31, W32, b32, 
         x_turn(7)
         w_scalar(1, 0, BANK_CHANNELS, PASS)
         w_empty(1, 0)
-        w_scalar(1, 1, 0, 128)
+        w_scalar(1, 1, 0, HEAD_CHANNELS)
         w_quant(0, 0)
         x_quant(0)
         w_quant(0, 1)
-        first_stage(0, [[], [], [], []])
-        w_vector(1, 1, 128, PASS)
+
+        first_stage(0)
+        w_vector(1, 1, HEAD_CHANNELS, PASS)
         w_quant(1, 0)
         w_quant(1, 1)
         w3_gpsimd()
         for r in range(4, ROWS):
             x_product(r)
-
-        first_stage(1, [[], [], [], [
-            (w_matmuls, 2, 0, 0), (w_scalar, 2, 1, BANK_CHANNELS, PASS), (w_empty, 2, 0, 0),
-            (w_tensor, 2, 0, BANK_CHANNELS), (w_tensor, 2, 1, 0),
-        ]])
+        first_stage(1)
+        w_matmuls(2, 0)
+        w_scalar(2, 1, BANK_CHANNELS, PASS)
+        w_empty(2, 0)
+        w_tensor(2, 0, BANK_CHANNELS)
+        w_tensor(2, 1)
         enc_lay(nc.vector.tensor_copy, 0, 0, HALF)
         x_quant(1)
         w_quant(2, 0)
@@ -478,45 +480,48 @@ def tile_mae_pa_kernel(tc, x_bytes, x_scale, eps, W11, b11, W31, b31, W32, b32, 
 
         for s in VECTOR_UNITS:
             g = s // 2 + 2
-            share = SCALAR_PASS1_FIRST if s == 2 else SCALAR_PASS1
+            last_pair = s == VECTOR_UNITS[-1]
+            w3_is_laid = g - 1 < W3_FIRST - 1
             w_matmuls(g, 0, 0, TENSOR_CHANNELS)
-            if s > 2:
+            if s > VECTOR_UNITS[0]:
                 second_stage(s - 3)
             w_scalar(g, 0, TENSOR_CHANNELS, PASS)
             w_empty(g, 0, 0, TENSOR_CHANNELS)
-            w_scalar(g, 1, 0, share)
+            w_scalar(g, 1, 0, SCALAR_CHANNELS)
             enc_gpsimd(s - 1, 0, GPSIMD_TOKENS)
             first_stage_rows(s)
             second_stage(s - 2)
             enc_lay(nc.vector.tensor_copy, s - 1, GPSIMD_TOKENS, HALF)
-            if share < PASS:
-                w_vector(g, 1, share, PASS)
+            w_vector(g, 1, SCALAR_CHANNELS, PASS)
             w_quant(g, 0)
             enc_quant(s - 1, 0, HALF)
-            first_stage(s + 1, [[], [], [], [(second_stage, s - 1)] if s == VECTOR_UNITS[-1] else []])
-            if g - 1 >= 3:
-                w3_lay(g - 1, 1 if g - 1 == 3 else 0)
+            first_stage(s + 1)
+            if last_pair:
+                second_stage(s - 1)
+            if w3_is_laid:
+                w3_quant(g - 1)
+                enc_relu(s)
             else:
+                w3_lay(g - 1, 1 if g - 1 == W3_FIRST - 1 else 0)
+                enc_relu(s)
                 w3_quant(g - 1)
-            enc_relu(s)
-            if g - 1 >= 3:
-                w3_quant(g - 1)
-            if s == VECTOR_UNITS[-1] or g - 1 < 3:
+            if last_pair or w3_is_laid:
                 w_quant(g, 1)
                 enc_quant(s, 0, HALF)
             else:
                 enc_quant(s, 0, HALF)
                 w_quant(g, 1)
 
-        for s in range(VECTOR_UNITS[-1] + 2, LAST + 1):
-            share = {13:96,14:0,15:96,16:64}.get(s - 1, 0)
-            after_bank = [[], [], [], [(second_stage, s - 2)]]
-            if share:
-                after_bank[0].append((enc_lay, nc.scalar.copy, s - 1, 0, share))
-            first_stage(s, after_bank)
+        first_step = VECTOR_UNITS[-1] + 2
+        for s in range(first_step, LAST + 1):
+            share = tokens(s - 1) // SCALAR_TAIL_SHARE if s >= len(WIDE_UNITS) else 0
+            first_stage(s, share)
+            second_stage(s - 2)
             enc_lay(nc.vector.tensor_copy, s - 1, share, tokens(s - 1))
-            if s in (12, 13):
-                w3_lay(GROUPS - 1, s - 12, s - 11)
+            if s - first_step < 2:
+                w3_lay(GROUPS - 1, s - first_step, s - first_step + 1)
+            if s - first_step == 2:
+                w3_quant(GROUPS - 1)
             if s == HALF0_CLOSED:
                 add_bias(0)
             if s == HALF0_CLOSED + 1:
@@ -524,8 +529,6 @@ def tile_mae_pa_kernel(tc, x_bytes, x_scale, eps, W11, b11, W31, b31, W32, b32, 
                 z_noise(1)
             if s == HALF0_CLOSED + 2:
                 z_add_mu(1)
-            if s == 14:
-                w3_quant(GROUPS - 1)
             enc_quant(s - 1, 0, tokens(s - 1))
             if s == HALF0_CLOSED:
                 add_bias(1)
@@ -546,8 +549,8 @@ def tile_mae_pa_kernel(tc, x_bytes, x_scale, eps, W11, b11, W31, b31, W32, b32, 
         z_noise(2)
         mu_sigma(2)
         z_add_mu(2)
-        add_bias(3, 0, 1)
-        add_bias(3, 1, 2)
+        for r in range(2):
+            add_bias(3, r, r + 1)
         for r in range(2):
             mu_sigma(3, r, r + 1, nc.scalar)
         for r in range(2):

@@ -35,11 +35,11 @@ HALF0_CLOSED = UNITS.index((0, GROUPS - 1, 0, 4)) + 2
 W3_FIRST = 4
 
 VECTOR_UNITS = range(2, 2 * GROUPS - 5, 2)
-GPSIMD_TOKENS = 448
-TENSOR_CHANNELS = 160
+GPSIMD_TOKENS = 464
+TENSOR_CHANNELS = 144
 SCALAR_CHANNELS = 480
 HEAD_CHANNELS = 128
-SCALAR_TAIL_SHARE = 4
+SCALAR_TAIL_TOKENS = 64
 MATMUL_ROWS = range(0, ROWS, 2)
 
 
@@ -334,7 +334,7 @@ def tile_mae_pa_kernel(tc, x_bytes, x_scale, eps, W11, b11, W31, b31, W32, b32, 
 
         def laid_tile(s):
             if s not in enc_laid:
-                if s <= VECTOR_UNITS[-1]:
+                if s <= VECTOR_UNITS[-1] or s in (HALF0_CLOSED - 1, HALF0_CLOSED):
                     enc_laid[s] = keep.tile([P, 4 * HALF], BF16, name="x_laid0", align_bytes=64)
                 else:
                     enc_laid[s] = work.tile([P, 4 * tokens(s)], BF16, name="enc_laid", bufs=3, align_bytes=64)
@@ -485,8 +485,8 @@ def tile_mae_pa_kernel(tc, x_bytes, x_scale, eps, W11, b11, W31, b31, W32, b32, 
             w_matmuls(g, 0, 0, TENSOR_CHANNELS)
             if s > VECTOR_UNITS[0]:
                 second_stage(s - 3)
-            w_scalar(g, 0, TENSOR_CHANNELS, PASS)
             w_empty(g, 0, 0, TENSOR_CHANNELS)
+            w_scalar(g, 0, TENSOR_CHANNELS, PASS)
             w_scalar(g, 1, 0, SCALAR_CHANNELS)
             enc_gpsimd(s - 1, 0, GPSIMD_TOKENS)
             first_stage_rows(s)
@@ -514,26 +514,26 @@ def tile_mae_pa_kernel(tc, x_bytes, x_scale, eps, W11, b11, W31, b31, W32, b32, 
 
         first_step = VECTOR_UNITS[-1] + 2
         for s in range(first_step, LAST + 1):
-            share = tokens(s - 1) // SCALAR_TAIL_SHARE if s >= len(WIDE_UNITS) else 0
+            share = SCALAR_TAIL_TOKENS if s >= len(WIDE_UNITS) else 0
             first_stage(s, share)
             second_stage(s - 2)
-            enc_lay(nc.vector.tensor_copy, s - 1, share, tokens(s - 1))
+            if s == HALF0_CLOSED + 1:
+                z_noise(0)
+                z_noise(1)
+            enc_lay(nc.vector.tensor_copy, s - 1, share, tokens(s - 1) - (P if s == HALF0_CLOSED + 1 else 0))
             if s - first_step < 2:
                 w3_lay(GROUPS - 1, s - first_step, s - first_step + 1)
             if s - first_step == 2:
                 w3_quant(GROUPS - 1)
-            if s == HALF0_CLOSED:
-                add_bias(0)
             if s == HALF0_CLOSED + 1:
-                z_noise(0)
-                z_noise(1)
+                z_add_mu(0)
             if s == HALF0_CLOSED + 2:
                 z_add_mu(1)
             enc_quant(s - 1, 0, tokens(s - 1))
             if s == HALF0_CLOSED:
+                enc_gpsimd(s, tokens(s) - P, tokens(s))
+                add_bias(0)
                 add_bias(1)
-            if s == HALF0_CLOSED + 1:
-                z_add_mu(0)
 
         mu_sigma(0)
         enc_lay(nc.scalar.copy, LAST, P, 2 * P)

@@ -25,21 +25,13 @@ PASS = 4 * P
 GROUPS = HIDDEN // PASS
 ROWS = TOKENS // P
 HALF = TOKENS // 2
+PAIR = 2 * P
 BANK_CHANNELS = 256
+PERIODS = 6
 
-WIDE_UNITS = [(0, 0, 0, 4)] + [(h, g - h, 0, 4) for g in range(1, GROUPS) for h in range(2)][:-1]
-UNITS = WIDE_UNITS + [(1, g, r, 2) for r in (0, 2) for g in (GROUPS - 2, GROUPS - 1)]
-LAST = len(UNITS) - 1
-HALF0_CLOSED = UNITS.index((0, GROUPS - 1, 0, 4)) + 2
-
-W3_FIRST = 4
-
-VECTOR_UNITS = range(2, 2 * GROUPS - 5, 2)
-GPSIMD_TOKENS = 464
-TENSOR_CHANNELS = 144
-SCALAR_CHANNELS = 480
+GPSIMD_CHANNELS = 432
+VECTOR_CHANNELS = 48
 HEAD_CHANNELS = 128
-SCALAR_TAIL_TOKENS = 64
 MATMUL_ROWS = range(0, ROWS, 2)
 
 
@@ -66,8 +58,7 @@ def tile_mae_pa_kernel(tc, x_bytes, x_scale, eps, W11, b11, W31, b31, W32, b32, 
         x_view = x_bytes.rearrange("(p r) k -> p (r k)", r=ROWS)
         w11_view = W11.rearrange("(c p j) n -> c p j n", c=2, j=4)
         w3_views = [w.rearrange("(g p j) l -> p g (j l)", p=P, j=4) for w in (W31, W32)]
-        b11_view = b11.rearrange("(g p t) -> p g t", p=P, t=4)
-        x_raw, w11_raw, w3_raw, bias1 = {}, {0: [], 1: []}, {}, {}
+        x_raw, w11_raw, w3_raw = {}, {}, {}
 
         def load_x(r0, r1):
             tile = keep.tile([P, (r1 - r0) * IMAGE], U8, name=f"x_raw{r0}")
@@ -75,47 +66,47 @@ def tile_mae_pa_kernel(tc, x_bytes, x_scale, eps, W11, b11, W31, b31, W32, b32, 
             for r in range(r0, r1):
                 x_raw[r] = tile[:, (r - r0) * IMAGE : (r - r0 + 1) * IMAGE]
 
-        def load_w11(c, n0, n1):
-            tile = keep.tile([P, 4, n1 - n0], BF16, name=f"w11_raw{c}_{n0}", align_bytes=64)
-            nc.sync.dma_start(out=tile[:], in_=w11_view[c, :, :, n0:n1])
-            w11_raw[c].append((n0, n1, tile))
+        def load_w11(c, g0, g1):
+            tile = keep.tile([P, 4, (g1 - g0) * PASS], BF16, name=f"w11_raw{c}_{g0}")
+            nc.sync.dma_start(out=tile[:], in_=w11_view[c, :, :, g0 * PASS : g1 * PASS])
+            for g in range(g0, g1):
+                w11_raw[g, c] = tile[:, :, (g - g0) * PASS : (g - g0 + 1) * PASS]
 
         def load_w3(g0, g1):
-            tile = keep.tile([P, g1 - g0, 2, 4 * LATENT], BF16, name=f"w3_raw{g0}")
             for w in range(2):
-                nc.sync.dma_start(out=tile[:, :, w, :], in_=w3_views[w][:, g0:g1, :])
-            w3_raw[g0, g1] = tile
+                tile = keep.tile([P, g1 - g0, 4 * LATENT], BF16, name=f"w3_raw{w}_{g0}")
+                nc.sync.dma_start(out=tile[:], in_=w3_views[w][:, g0:g1, :])
+                for g in range(g0, g1):
+                    w3_raw[g, w] = tile[:, g - g0, :]
 
-        def load_bias1(g0, g1):
-            tile = keep.tile([P, g1 - g0, 4], BF16, name=f"bias1_{g0}")
-            nc.sync.dma_start(out=tile[:], in_=b11_view[:, g0:g1, :])
-            for g in range(g0, g1):
-                bias1[g] = tile[:, g - g0, :]
-
-        scale_cols = keep.tile([P, 2, 4], F32, name="scale_cols")
+        scale = keep.tile([P, 2, 4], F32, name="scale")
+        bias1 = keep.tile([P, GROUPS, 4], BF16, name="bias1")
+        b11_view = b11.rearrange("(g p t) -> p g t", p=P, t=4)
         load_x(0, 1)
-        nc.sync.dma_start(out=scale_cols[:], in_=x_scale.rearrange("o (c p t) -> p (o c) t", p=P, t=4))
-        scale = keep.tile([P, 2, P, 4], F32, name="scale")
+        nc.sync.dma_start(out=scale[:], in_=x_scale.rearrange("o (c p t) -> p (o c) t", p=P, t=4))
         load_x(1, 2)
         load_x(2, 4)
-        load_w11(0, 0, PASS)
+        load_w11(0, 0, 1)
         load_x(4, 6)
-        load_w11(1, 0, PASS)
+        load_w11(1, 0, 1)
         load_x(6, ROWS)
-        load_w11(0, PASS, 2 * PASS)
-        load_w11(1, PASS, 2 * PASS)
-        load_bias1(0, 2)
-        load_w3(0, W3_FIRST)
-        load_w11(0, 2 * PASS, 3 * PASS)
-        load_w11(1, 2 * PASS, 3 * PASS)
-        load_bias1(2, GROUPS)
-        for c in range(2):
-            load_w11(c, 3 * PASS, 4 * PASS)
-        for g in range(4, GROUPS, 2):
-            for c in range(2):
-                load_w11(c, g * PASS, (g + 2) * PASS)
-            if g == 4:
-                load_w3(W3_FIRST, GROUPS)
+        load_w11(0, 1, 2)
+        load_w11(1, 1, 2)
+        nc.sync.dma_start(out=bias1[:, :4, :], in_=b11_view[:, :4, :])
+        load_w3(0, 1)
+        load_w11(0, 2, 3)
+        load_w3(1, 3)
+        load_w11(0, 3, 4)
+        load_w11(1, 2, 3)
+        load_w3(3, 5)
+        load_w11(0, 4, 5)
+        load_w11(1, 3, 4)
+        nc.sync.dma_start(out=bias1[:, 4:, :], in_=b11_view[:, 4:, :])
+        load_w11(0, 5, 7)
+        load_w11(1, 4, 6)
+        load_w3(5, GROUPS)
+        load_w11(0, 7, 8)
+        load_w11(1, 6, 8)
         bias3 = keep.tile([P, 2 * LATENT], BF16, name="bias3")
         nc.sync.dma_start(out=bias3[:, :LATENT], in_=b31.partition_broadcast(P))
         nc.sync.dma_start(out=bias3[:, LATENT:], in_=b32.partition_broadcast(P))
@@ -134,7 +125,7 @@ def tile_mae_pa_kernel(tc, x_bytes, x_scale, eps, W11, b11, W31, b31, W32, b32, 
 
         def x_widen(r, c0=0, c1=2):
             if r not in x_wide:
-                x_wide[r] = work.tile([P, IMAGE], BF16, name="x_wide", bufs=4)
+                x_wide[r] = work.tile([P, IMAGE], BF16, name="x_wide", bufs=8, align_bytes=64)
             nc.scalar.copy(
                 out=x_wide[r][:, PASS * c0 : PASS * c1], in_=x_raw[r][:, PASS * c0 : PASS * c1].bitcast(FP8)
             )
@@ -142,17 +133,17 @@ def tile_mae_pa_kernel(tc, x_bytes, x_scale, eps, W11, b11, W31, b31, W32, b32, 
         def x_turn(r, c0=0, c1=2):
             pool, tag = (psum, "bank") if c1 - c0 == 1 else (sums, f"sum{r % 4}")
             if r in MATMUL_ROWS:
-                pairs = pool.tile([P, 2, c1 - c0, 2 * P], BF16, name=tag)
+                turned = pool.tile([P, 2, c1 - c0, 2 * P], BF16, name=tag)
                 for c in range(c0, c1):
                     for t in range(4):
                         nc.tensor.matmul(
-                            out=pairs[:, t // 2, c - c0, :],
+                            out=turned[:, t // 2, c - c0, :],
                             lhsT=x_wide[r][:, PASS * c + t : PASS * (c + 1) : 4],
                             rhs=wide_ident[:, t % 2, :],
                             start=(t % 2 == 0),
                             stop=(t % 2 == 1),
                         )
-                x_turned[r, c0] = pairs[:]
+                x_turned[r, c0] = turned[:]
             else:
                 bank = pool.tile([P, 2, c1 - c0, P], F32, name=tag)
                 words = x_wide[r][:].bitcast(F32)
@@ -169,7 +160,10 @@ def tile_mae_pa_kernel(tc, x_bytes, x_scale, eps, W11, b11, W31, b31, W32, b32, 
                 x_laid[h] = keep.tile([P, 2, HALF, 4], BF16, name=f"x_laid{h}", align_bytes=64)
             nc.vector.tensor_tensor(
                 out=x_laid[h][:, c0:c1, P * row : P * (row + 1), :].rearrange("p c n (u e) -> p c n u e", u=2),
-                in0=scale[:, c0:c1, :, :].rearrange("p c n (u e) -> p c n u e", u=2),
+                in0=scale[:, c0:c1, :]
+                .rearrange("p c (u e) -> p c u e", u=2)
+                .unsqueeze(2)
+                .to_broadcast([P, c1 - c0, P, 2, 2]),
                 in1=x_turned[r, c0].rearrange("p u c (n e) -> p c n u e", e=2),
                 op=MULT,
             )
@@ -181,50 +175,37 @@ def tile_mae_pa_kernel(tc, x_bytes, x_scale, eps, W11, b11, W31, b31, W32, b32, 
                 in_=x_laid[h][:].rearrange("p c n t -> p (c n t)"),
             )
 
-        w_laid, w_banks, w_codes, w_scales = {}, {}, {}, {}
+        w_laid, w3_laid, w_banks, w_codes, w_scales = {}, {}, {}, {}, {}
 
-        def w_source(g, c, a, b):
-            a, b = PASS * g + a, PASS * g + b
-            n0, tile = [(n0, tile) for n0, n1, tile in w11_raw[c] if n0 <= a and b <= n1][0]
-            return tile[:, :, a - n0 : b - n0]
-
-        def w_target(g, c):
+        def w_target(g, c, tag=None):
             if (g, c) not in w_laid:
-                if (g, c) == (1, 1):
-                    w_laid[g, c] = keep.tile([P, 2 * PASS], F32, name="w11_raw0_0", align_bytes=64)
-                else:
-                    w_laid[g, c] = work.tile([P, 2 * PASS], F32, name="w_laid", bufs=5, align_bytes=64)
+                w_laid[g, c] = keep.tile([P, 4 * PASS], BF16, name=tag or f"w_laid{g % 2}", align_bytes=64)[:]
             return w_laid[g, c]
 
-        def w_matmuls(g, c, a=0, width=BANK_CHANNELS):
+        def w_matmuls(g, c, a, width=BANK_CHANNELS):
             w_banks[g, c, a] = bank = psum.tile([P, 2 * BANK_CHANNELS], F32, name="bank")
             for n0 in range(0, width, P):
-                n1 = min(n0 + P, width)
                 nc.tensor.matmul(
-                    out=bank[:, 2 * n0 : 2 * n1].bitcast(BF16),
+                    out=bank[:, 2 * n0 : 2 * (n0 + P)].bitcast(BF16),
                     lhsT=ident_bf[:],
-                    rhs=w_source(g, c, a + n0, a + n1).rearrange("p j n -> p n j"),
+                    rhs=w11_raw[g, c][:, :, a + n0 : a + n0 + P].rearrange("p j n -> p n j"),
                     start=True,
                     stop=True,
                 )
 
-        def w_empty(g, c, a=0, width=BANK_CHANNELS):
+        def w_empty(g, c, a, width=BANK_CHANNELS):
             nc.scalar.copy(
-                out=w_target(g, c)[:].rearrange("p (t m u) -> p t m u", t=4, u=2)[
+                out=w_target(g, c).bitcast(F32).rearrange("p (t m u) -> p t m u", t=4, u=2)[
                     :, :, a // 4 : (a + width) // 4, :
                 ],
                 in_=w_banks[g, c, a][:, : 2 * width].rearrange("p (m t u) -> p t m u", t=4, u=2),
             )
 
-        def w_tensor(g, c, a=0):
-            w_matmuls(g, c, a)
-            w_empty(g, c, a)
-
         def w_copy(engine_copy, g, c, a, b):
-            target = w_target(g, c)[:].bitcast(BF16).rearrange("p (t m i j) -> p m t j i", t=4, i=2, j=4)
+            target = w_target(g, c).rearrange("p (t m i j) -> p m t j i", t=4, i=2, j=4)
             engine_copy(
                 out=target[:, a // 8 : b // 8, :, :, :],
-                in_=w_source(g, c, a, b).rearrange("p j (m i t) -> p m t j i", t=4, i=2),
+                in_=w11_raw[g, c][:, :, a:b].rearrange("p j (m i t) -> p m t j i", t=4, i=2),
             )
 
         def w_vector(g, c, a, b):
@@ -234,10 +215,10 @@ def tile_mae_pa_kernel(tc, x_bytes, x_scale, eps, W11, b11, W31, b31, W32, b32, 
             w_copy(nc.scalar.copy, g, c, a, b)
 
         def w_gpsimd(g, c, a, b):
-            target = w_target(g, c)[:].bitcast(BF16).rearrange("p (t m j) -> p m t j", t=4, j=4)
+            target = w_target(g, c).rearrange("p (t m j) -> p m t j", t=4, j=4)
             nc.gpsimd.tensor_scalar(
                 out=target[:, a // 4 : b // 4, :, :],
-                in0=w_source(g, c, a, b).rearrange("p j (m t) -> p m t j", t=4),
+                in0=w11_raw[g, c][:, :, a:b].rearrange("p j (m t) -> p m t j", t=4),
                 scalar1=1.0, scalar2=0.0, op0=MULT, op1=ADD,
             )
 
@@ -246,141 +227,154 @@ def tile_mae_pa_kernel(tc, x_bytes, x_scale, eps, W11, b11, W31, b31, W32, b32, 
                 w_codes[g] = work.tile([P, 2, PASS], U32, name="w_codes", bufs=4, align_bytes=64)
                 w_scales[g] = work.tile([P, 2, PASS], U8, name="w_scales", bufs=4, align_bytes=64)
             nc.vector.quantize_mx(
-                out=w_codes[g][:, c, :].bitcast(FP8X4),
-                scales=w_scales[g][:, c, :],
-                in_=w_laid[g, c][:].bitcast(BF16),
+                out=w_codes[g][:, c, :].bitcast(FP8X4), scales=w_scales[g][:, c, :], in_=w_laid[g, c]
             )
 
-        w3_laid = {}
         w3_codes = keep.tile([P, GROUPS, 2 * LATENT], U32, name="w3_codes", align_bytes=64)
         w3_scales = keep.tile([P, GROUPS, 2 * LATENT], U8, name="w3_scales", align_bytes=64)
 
-        def w3_lay(g, w0=0, w1=2):
-            g0, g1 = [k for k in w3_raw if k[0] <= g < k[1]][0]
+        def w3_target(g, w):
             if g not in w3_laid:
-                w3_laid[g] = work.tile([P, 8 * LATENT], BF16, name="w3_laid", bufs=1, align_bytes=64)[:]
-            nc.vector.tensor_copy(
-                out=w3_laid[g].rearrange("p (w m i j) -> p w m j i", w=2, i=2, j=4)[:, w0:w1, :, :, :],
-                in_=w3_raw[g0, g1][:, g - g0, w0:w1, :].rearrange("p w (j m i) -> p w m j i", j=4, i=2),
+                w3_laid[g] = work.tile([P, 8 * LATENT], BF16, name="w3_laid", bufs=3, align_bytes=64)[:]
+            return w3_laid[g][:, 4 * LATENT * w : 4 * LATENT * (w + 1)]
+
+        def w3_copy(engine_copy, g, w):
+            engine_copy(
+                out=w3_target(g, w).rearrange("p (m i j) -> p m j i", i=2, j=4),
+                in_=w3_raw[g, w].rearrange("p (j m i) -> p m j i", j=4, i=2),
             )
 
-        def w3_gpsimd():
-            tile = keep.tile([P, W3_FIRST, 8 * LATENT], BF16, name="w11_raw0_0", align_bytes=64)
-            for w in range(2):
-                groups = W3_FIRST - w
-                nc.gpsimd.tensor_scalar(
-                    out=tile[:, :groups, :].rearrange("p g (w l j) -> p g w l j", w=2, j=4)[:, :, w, :, :],
-                    in0=w3_raw[0, W3_FIRST][:, :groups, w, :].rearrange("p g (j l) -> p g l j", j=4),
-                    scalar1=1.0, scalar2=0.0, op0=MULT, op1=ADD,
-                )
-            for g in range(W3_FIRST):
-                w3_laid[g] = tile[:, g, :]
-
-        def w3_quant(g):
-            nc.vector.quantize_mx(
-                out=w3_codes[:, g, :].bitcast(FP8X4), scales=w3_scales[:, g, :], in_=w3_laid[g]
-            )
-
-        enc, enc_laid, enc_codes, enc_scales = {}, {}, {}, {}
-
-        def tokens(s):
-            return P * UNITS[s][3]
-
-        def first_stage(s, scalar_share=0):
-            h, g, row0, rows = UNITS[s]
-            cols = slice(P * row0, P * (row0 + rows))
-            enc[s] = work.tile([P, 4, tokens(s)], BF16, name="enc", bufs=3)
-            for t in range(4):
-                bank = psum.tile([P, HALF], F32, name="bank")
-                for c in range(2):
-                    nc.tensor.matmul_mx(
-                        out=bank[:, : tokens(s)],
-                        lhsT=w_codes[g][:, c, P * t : P * (t + 1)].bitcast(FP8X4),
-                        lhsT_scale=w_scales[g][:, c, P * t : P * (t + 1)],
-                        rhs=x_codes[h][:, c, cols].bitcast(FP8X4),
-                        rhs_scale=x_scales[h][:, c, cols],
-                        start=(c == 0),
-                        stop=(c == 1),
-                    )
-                nc.scalar.activation(
-                    out=enc[s][:, t, :], in_=bank[:, : tokens(s)], func=RELU, bias=bias1[g][:, t : t + 1]
-                )
-                if t == 0 and scalar_share:
-                    enc_lay(nc.scalar.copy, s - 1, 0, scalar_share)
-
-        def first_stage_rows(s):
-            h, g, row0, rows = UNITS[s]
-            enc[s] = work.tile([P, tokens(s), 4], BF16, name="enc", bufs=3)
-            for r in range(rows):
-                cols = slice(P * (row0 + r), P * (row0 + r + 1))
-                bank = psum.tile([P, 4, P], F32, name="bank")
-                for t in range(4):
-                    for c in range(2):
-                        nc.tensor.matmul_mx(
-                            out=bank[:, t, :],
-                            lhsT=w_codes[g][:, c, P * t : P * (t + 1)].bitcast(FP8X4),
-                            lhsT_scale=w_scales[g][:, c, P * t : P * (t + 1)],
-                            rhs=x_codes[h][:, c, cols].bitcast(FP8X4),
-                            rhs_scale=x_scales[h][:, c, cols],
-                            start=(c == 0),
-                            stop=(c == 1),
-                        )
-                nc.vector.tensor_tensor(
-                    out=enc[s][:, P * r : P * (r + 1), :],
-                    in0=bias1[g].unsqueeze(1).to_broadcast([P, P, 4]),
-                    in1=bank[:].rearrange("p t n -> p n t"),
-                    op=ADD,
-                )
-
-        def laid_tile(s):
-            if s not in enc_laid:
-                if s <= VECTOR_UNITS[-1] or s in (HALF0_CLOSED - 1, HALF0_CLOSED):
-                    enc_laid[s] = keep.tile([P, 4 * HALF], BF16, name="x_laid0", align_bytes=64)
-                else:
-                    enc_laid[s] = work.tile([P, 4 * tokens(s)], BF16, name="enc_laid", bufs=3, align_bytes=64)
-            return enc_laid[s]
-
-        def enc_relu(s):
-            nc.vector.tensor_scalar(
-                out=laid_tile(s)[:], in0=enc[s][:].rearrange("p n t -> p (n t)"), scalar1=0.0, scalar2=None, op0=MAX
-            )
-
-        def enc_gpsimd(s, a, b):
+        def w3_gpsimd(g, w):
             nc.gpsimd.tensor_scalar(
-                out=laid_tile(s)[:, 4 * a : 4 * b].rearrange("p (n t) -> p n t", t=4),
-                in0=enc[s][:, :, a:b].rearrange("p t n -> p n t"),
+                out=w3_target(g, w).rearrange("p (l j) -> p l j", j=4),
+                in0=w3_raw[g, w].rearrange("p (j l) -> p l j", j=4),
                 scalar1=1.0, scalar2=0.0, op0=MULT, op1=ADD,
             )
 
-        def enc_lay(engine_copy, s, a, b):
-            laid_tile(s)
-            engine_copy(
-                out=enc_laid[s][:, 4 * a : 4 * b].rearrange("p (m i t) -> p m t i", i=2, t=4),
-                in_=enc[s][:, :, a:b].rearrange("p t (m i) -> p m t i", i=2),
+        def w3_matmuls(g, w0, w1):
+            w_banks[g, w0] = bank = psum.tile([P, 4 * LATENT], F32, name="bank")
+            for w in range(w0, w1):
+                nc.tensor.matmul(
+                    out=bank[:, 2 * LATENT * (w - w0) : 2 * LATENT * (w - w0 + 1)].bitcast(BF16),
+                    lhsT=ident_bf[:],
+                    rhs=w3_raw[g, w].rearrange("p (j l) -> p l j", j=4),
+                    start=True,
+                    stop=True,
+                )
+
+        def w3_empty(g, w0, w1):
+            w3_target(g, w0)
+            nc.scalar.copy(
+                out=w3_laid[g][:, 4 * LATENT * w0 : 4 * LATENT * w1].bitcast(F32),
+                in_=w_banks[g, w0][:, : 2 * LATENT * (w1 - w0)],
             )
 
-        def enc_quant(s, a, b):
-            if s not in enc_codes:
-                enc_codes[s] = work.tile([P, tokens(s)], U32, name="enc_codes", bufs=3, align_bytes=64)
-                enc_scales[s] = work.tile([P, tokens(s)], U8, name="enc_scales", bufs=3, align_bytes=64)
+        def w3_quant(g, w0=0, w1=2):
+            cols = slice(LATENT * w0, LATENT * w1)
             nc.vector.quantize_mx(
-                out=enc_codes[s][:, a:b].bitcast(FP8X4),
-                scales=enc_scales[s][:, a:b],
-                in_=enc_laid[s][:, 4 * a : 4 * b],
+                out=w3_codes[:, g, cols].bitcast(FP8X4), scales=w3_scales[:, g, cols],
+                in_=w3_laid[g][:, 4 * LATENT * w0 : 4 * LATENT * w1],
+            )
+
+        planes, v_banks, enc_laid, enc_codes, enc_scales = {}, {}, {}, {}, {}
+
+        def passes(out, unit, t, cols):
+            h, g = unit[:2]
+            for c in range(2):
+                nc.tensor.matmul_mx(
+                    out=out,
+                    lhsT=w_codes[g][:, c, P * t : P * (t + 1)].bitcast(FP8X4),
+                    lhsT_scale=w_scales[g][:, c, P * t : P * (t + 1)],
+                    rhs=x_codes[h][:, c, cols].bitcast(FP8X4),
+                    rhs_scale=x_scales[h][:, c, cols],
+                    start=(c == 0),
+                    stop=(c == 1),
+                )
+
+        def plane_tile(unit, tag):
+            if unit not in planes:
+                planes[unit] = work.tile([P, 2, P * unit[3], 2], BF16, name=tag)
+            return planes[unit]
+
+        def scalar_bank(unit, t):
+            bank = psum.tile([P, HALF], F32, name="bank")
+            passes(bank[:], unit, t, slice(0, HALF))
+            scalar_empty(unit, t, bank[:])
+
+        def scalar_empty(unit, t, sums_of_t):
+            nc.scalar.activation(
+                out=plane_tile(unit, "planes_s")[:, t // 2, :, t % 2],
+                in_=sums_of_t, func=RELU, bias=bias1[:, unit[1], t : t + 1],
+            )
+
+        def scalar_unit(unit):
+            for t in (0, 2, 1, 3):
+                scalar_bank(unit, t)
+
+        def scalar_pair_bank(unit, e):
+            bank = psum.tile([P, 2, PAIR], F32, name="bank")
+            for u in range(2):
+                passes(bank[:, u, :], unit, 2 * u + e, slice(P * unit[2], P * unit[2] + PAIR))
+            for u in range(2):
+                scalar_empty(unit, 2 * u + e, bank[:, u, :])
+
+        def vector_bank(unit, i):
+            q, u = divmod(i, 2)
+            n0 = P * unit[2] + PAIR * q
+            v_banks[unit, i] = bank = psum.tile([P, 2, PAIR], F32, name="bank")
+            for e in range(2):
+                passes(bank[:, e, :], unit, 2 * u + e, slice(n0, n0 + PAIR))
+
+        def vector_add(unit, i):
+            q, u = divmod(i, 2)
+            nc.vector.tensor_tensor(
+                out=plane_tile(unit, "planes_v")[:, u, PAIR * q : PAIR * (q + 1), :],
+                in0=bias1[:, unit[1], 2 * u : 2 * u + 2].unsqueeze(1).to_broadcast([P, PAIR, 2]),
+                in1=v_banks[unit, i][:].rearrange("p e n -> p n e"),
+                op=ADD,
+            )
+
+        def laid_tile(unit):
+            if unit not in enc_laid:
+                enc_laid[unit] = work.tile([P, P * unit[3], 2, 2], BF16, name="enc_laid", bufs=3, align_bytes=64)
+            return enc_laid[unit]
+
+        def join(unit, a=0, b=None):
+            b = b or unit[3]
+            nc.vector.tensor_copy(
+                out=laid_tile(unit)[:, P * a : P * b, :, :],
+                in_=planes[unit][:, :, P * a : P * b, :].rearrange("p u n e -> p n u e"),
+            )
+
+        def join_relu(unit):
+            nc.vector.tensor_scalar(
+                out=laid_tile(unit)[:], in0=planes[unit][:].rearrange("p u n e -> p n u e"),
+                scalar1=0.0, scalar2=None, op0=MAX,
+            )
+
+        def enc_quant(unit, a=0, b=None):
+            b = b or unit[3]
+            if unit not in enc_codes:
+                enc_codes[unit] = work.tile([P, P * unit[3]], U32, name="x_wide", bufs=8, align_bytes=64)
+                enc_scales[unit] = work.tile([P, P * unit[3]], U8, name="enc_scales", bufs=8, align_bytes=64)
+            nc.vector.quantize_mx(
+                out=enc_codes[unit][:, P * a : P * b].bitcast(FP8X4),
+                scales=enc_scales[unit][:, P * a : P * b],
+                in_=enc_laid[unit][:, P * a : P * b, :, :].rearrange("p n u e -> p (n u e)"),
             )
 
         acc = {}
 
-        def second_stage(s):
-            h, g, row0, rows = UNITS[s]
-            for r in range(rows):
+        def second_stage(unit, a=0, b=None):
+            h, g, row0, rows = unit
+            for r in range(a, b or rows):
                 i = 2 * h + (row0 + r) // 2
                 if i not in acc:
                     acc[i] = sums.tile([P, 2, 2 * LATENT], F32, name=f"sum{i}")
                 nc.tensor.matmul_mx(
                     out=acc[i][:, r % 2, :],
-                    lhsT=enc_codes[s][:, P * r : P * (r + 1)].bitcast(FP8X4),
-                    lhsT_scale=enc_scales[s][:, P * r : P * (r + 1)],
+                    lhsT=enc_codes[unit][:, P * r : P * (r + 1)].bitcast(FP8X4),
+                    lhsT_scale=enc_scales[unit][:, P * r : P * (r + 1)],
                     rhs=w3_codes[:, g, :].bitcast(FP8X4),
                     rhs_scale=w3_scales[:, g, :],
                     start=(g == 0 and r % 2 == 0),
@@ -392,7 +386,7 @@ def tile_mae_pa_kernel(tc, x_bytes, x_scale, eps, W11, b11, W31, b31, W32, b32, 
 
         def add_bias(i, a=0, b=2):
             if i not in biased:
-                biased[i] = work.tile([P, 2, 2 * LATENT], F32, name="biased", bufs=3)
+                biased[i] = work.tile([P, 2, 2 * LATENT], F32, name="biased", bufs=4)
             nc.vector.tensor_tensor(
                 out=biased[i][:, a:b, :], in0=bias3[:].unsqueeze(1).to_broadcast([P, b - a, 2 * LATENT]),
                 in1=acc[i][:, a:b, :], op=ADD,
@@ -427,7 +421,6 @@ def tile_mae_pa_kernel(tc, x_bytes, x_scale, eps, W11, b11, W31, b31, W32, b32, 
         unused_bank = sums.tile([P, HALF], F32, name="sum0")
         warm_up(unused_bank, 256)
         warm_up(unused_bank, 256)
-        nc.vector.tensor_copy(out=scale[:], in_=scale_cols[:].unsqueeze(2).to_broadcast([P, 2, P, 4]))
         for c in range(2):
             x_widen(0, c, c + 1)
             x_turn(0, c, c + 1)
@@ -436,6 +429,8 @@ def tile_mae_pa_kernel(tc, x_bytes, x_scale, eps, W11, b11, W31, b31, W32, b32, 
             x_widen(r)
             x_turn(r)
             x_product(r)
+        w_target(0, 1, "w_laid1")
+        w_target(1, 0, "w_laid2")
         w_gpsimd(0, 0, 0, PASS)
         w_gpsimd(0, 1, 0, HEAD_CHANNELS)
         x_widen(4)
@@ -447,113 +442,137 @@ def tile_mae_pa_kernel(tc, x_bytes, x_scale, eps, W11, b11, W31, b31, W32, b32, 
         x_widen(6)
         x_widen(7)
         w_empty(0, 1, BANK_CHANNELS)
-        w_matmuls(1, 0)
         x_turn(6)
-        x_turn(7)
-        w_scalar(1, 0, BANK_CHANNELS, PASS)
-        w_empty(1, 0)
-        w_scalar(1, 1, 0, HEAD_CHANNELS)
+        w_matmuls(1, 0, 0, P)
+        w_scalar(1, 0, P, PASS)
+        w_empty(1, 0, 0, P)
         w_quant(0, 0)
         x_quant(0)
         w_quant(0, 1)
 
-        first_stage(0)
-        w_vector(1, 1, HEAD_CHANNELS, PASS)
-        w_quant(1, 0)
-        w_quant(1, 1)
-        w3_gpsimd()
+        released = keep.tile([P, 2, 4 * PASS], BF16, name="x_laid0", align_bytes=64)
+        w_laid[1, 1] = released[:, 0, :]
+        w3_laid[0] = released[:, 1, : 8 * LATENT]
+        w_gpsimd(1, 1, 0, PASS)
+        for w in range(2):
+            w3_gpsimd(0, w)
+        scalar_unit((0, 0, 0, 4))
+        x_turn(7)
         for r in range(4, ROWS):
             x_product(r)
-        first_stage(1)
-        w_matmuls(2, 0)
-        w_scalar(2, 1, BANK_CHANNELS, PASS)
-        w_empty(2, 0)
-        w_tensor(2, 0, BANK_CHANNELS)
-        w_tensor(2, 1)
-        enc_lay(nc.vector.tensor_copy, 0, 0, HALF)
+        for a in (0, BANK_CHANNELS):
+            w_matmuls(2, 0, a)
+            w_empty(2, 0, a)
+        w3_matmuls(1, 0, 2)
+        w3_empty(1, 0, 2)
+        w3_matmuls(2, 0, 1)
+        w3_empty(2, 0, 1)
+        w_quant(1, 0)
         x_quant(1)
         w_quant(2, 0)
-        w3_quant(0)
-        w3_quant(1)
-        enc_quant(0, 0, HALF)
-        w_quant(2, 1)
+        w_quant(1, 1)
+        for i in range(4):
+            vector_bank((1, 0, 0, 4), i)
 
-        for s in VECTOR_UNITS:
-            g = s // 2 + 2
-            last_pair = s == VECTOR_UNITS[-1]
-            w3_is_laid = g - 1 < W3_FIRST - 1
-            w_matmuls(g, 0, 0, TENSOR_CHANNELS)
-            if s > VECTOR_UNITS[0]:
-                second_stage(s - 3)
-            w_empty(g, 0, 0, TENSOR_CHANNELS)
-            w_scalar(g, 0, TENSOR_CHANNELS, PASS)
-            w_scalar(g, 1, 0, SCALAR_CHANNELS)
-            enc_gpsimd(s - 1, 0, GPSIMD_TOKENS)
-            first_stage_rows(s)
-            second_stage(s - 2)
-            enc_lay(nc.vector.tensor_copy, s - 1, GPSIMD_TOKENS, HALF)
-            w_vector(g, 1, SCALAR_CHANNELS, PASS)
-            w_quant(g, 0)
-            enc_quant(s - 1, 0, HALF)
-            first_stage(s + 1)
-            if last_pair:
-                second_stage(s - 1)
-            if w3_is_laid:
-                w3_quant(g - 1)
-                enc_relu(s)
+        g5, g6, g7 = GROUPS - 3, GROUPS - 2, GROUPS - 1
+        for j in range(PERIODS):
+            v_unit, s_unit = (1, j, 0, 4), (0, j + 1, 0, 4)
+            last = j == PERIODS - 1
+            if last:
+                for m in range(10, 14):
+                    w3_copy(nc.scalar.copy, m // 2, m % 2)
             else:
-                w3_lay(g - 1, 1 if g - 1 == W3_FIRST - 1 else 0)
-                enc_relu(s)
-                w3_quant(g - 1)
-            if last_pair or w3_is_laid:
-                w_quant(g, 1)
-                enc_quant(s, 0, HALF)
+                w_scalar(j + 3, 0, 0, PASS - VECTOR_CHANNELS)
+            w_scalar(j + 2, 1, GPSIMD_CHANNELS, PASS)
+            w_gpsimd(j + 2, 1, 0, GPSIMD_CHANNELS)
+            for i in range(4):
+                vector_add(v_unit, i)
+            m = 15 if last else 5 + j
+            w3_matmuls(m // 2, m % 2, m % 2 + 1)
+            w3_empty(m // 2, m % 2, m % 2 + 1)
+            scalar_unit(s_unit)
+            if 0 < j < PERIODS - 1:
+                second_stage((1, j - 1, 0, 4))
+            join((0, j, 0, 4))
+            if last:
+                join_relu(v_unit)
+                w_quant(g7, 1)
+                w3_quant(j)
             else:
-                enc_quant(s, 0, HALF)
-                w_quant(g, 1)
+                w_vector(j + 3, 0, PASS - VECTOR_CHANNELS, PASS)
+                join_relu(v_unit)
+                w3_quant(j)
+                w_quant(j + 2, 1)
+            enc_quant((0, j, 0, 4))
+            if not last:
+                for i in range(4):
+                    vector_bank((1, j + 1, 0, 4), i)
+                second_stage((0, j, 0, 4))
+                w_quant(j + 3, 0)
+                enc_quant(v_unit)
 
-        first_step = VECTOR_UNITS[-1] + 2
-        for s in range(first_step, LAST + 1):
-            share = SCALAR_TAIL_TOKENS if s >= len(WIDE_UNITS) else 0
-            first_stage(s, share)
-            second_stage(s - 2)
-            if s == HALF0_CLOSED + 1:
-                z_noise(0)
-                z_noise(1)
-            enc_lay(nc.vector.tensor_copy, s - 1, share, tokens(s - 1) - (P if s == HALF0_CLOSED + 1 else 0))
-            if s - first_step < 2:
-                w3_lay(GROUPS - 1, s - first_step, s - first_step + 1)
-            if s - first_step == 2:
-                w3_quant(GROUPS - 1)
-            if s == HALF0_CLOSED + 1:
-                z_add_mu(0)
-            if s == HALF0_CLOSED + 2:
-                z_add_mu(1)
-            enc_quant(s - 1, 0, tokens(s - 1))
-            if s == HALF0_CLOSED:
-                enc_gpsimd(s, tokens(s) - P, tokens(s))
-                add_bias(0)
-                add_bias(1)
-
+        s6, s7 = (0, g6, 0, 4), (0, g7, 0, 4)
+        v6 = [(1, g6, 0, 2), (1, g6, 2, 2)]
+        s7b = [(1, g7, 0, 2), (1, g7, 2, 2)]
+        w3_copy(nc.vector.tensor_copy, g7, 0)
+        w3_quant(g6)
+        enc_quant((1, g5, 0, 4))
+        vector_bank(v6[0], 0)
+        scalar_bank(s7, 0)
+        second_stage((0, g5, 0, 4))
+        scalar_bank(s7, 2)
+        vector_bank(v6[0], 1)
+        vector_add(v6[0], 0)
+        w3_quant(g7)
+        join(s6)
+        vector_add(v6[0], 1)
+        enc_quant(s6)
+        scalar_bank(s7, 1)
+        scalar_bank(s7, 3)
+        vector_bank(v6[1], 0)
+        scalar_pair_bank(s7b[0], 0)
+        second_stage(s6)
+        join_relu(v6[0])
+        vector_add(v6[1], 0)
+        enc_quant(v6[0])
+        scalar_pair_bank(s7b[0], 1)
+        vector_bank(v6[1], 1)
+        join(s7, 0, 2)
+        join(s7, 2, 4)
+        enc_quant(s7, 0, 2)
+        enc_quant(s7, 2, 4)
+        vector_add(v6[1], 1)
+        scalar_pair_bank(s7b[1], 0)
+        second_stage(s7)
+        scalar_pair_bank(s7b[1], 1)
+        join(s7b[0])
+        join_relu(v6[1])
+        enc_quant(s7b[0])
+        add_bias(0)
+        enc_quant(v6[1])
+        for g in (g5 - 1, g5):
+            second_stage((1, g, 0, 4), 0, 2)
+        second_stage(v6[0])
+        second_stage(s7b[0])
+        for g in (g5 - 1, g5):
+            second_stage((1, g, 0, 4), 2, 4)
+        second_stage(v6[1])
+        add_bias(1)
+        join(s7b[1])
+        z_noise(0)
+        enc_quant(s7b[1])
+        second_stage(s7b[1])
         mu_sigma(0)
-        enc_lay(nc.scalar.copy, LAST, P, 2 * P)
-        enc_lay(nc.vector.tensor_copy, LAST, 0, P)
-        second_stage(LAST - 1)
-        unused_bank = psum.tile([P, HALF], F32, name="bank")
-        warm_up(unused_bank, 256)
-        add_bias(2)
         mu_sigma(1)
-        for r in range(2):
-            enc_quant(LAST, P * r, P * (r + 1))
-        second_stage(LAST)
-        z_noise(2)
+        add_bias(2)
+        z_add_mu(0)
+        z_noise(1)
         mu_sigma(2)
-        z_add_mu(2)
         for r in range(2):
             add_bias(3, r, r + 1)
-        for r in range(2):
-            mu_sigma(3, r, r + 1, nc.scalar)
-        for r in range(2):
-            z_noise(3, r, r + 1)
-        for r in range(2):
-            z_add_mu(3, r, r + 1)
+        z_add_mu(1)
+        z_noise(2)
+        mu_sigma(3, 0, 2, nc.scalar)
+        z_noise(3)
+        z_add_mu(2)
+        z_add_mu(3)

@@ -29,8 +29,10 @@ PAIR = 2 * P
 BANK_CHANNELS = 256
 PERIODS = 6
 
-GPSIMD_CHANNELS = 432
-VECTOR_CHANNELS = 48
+GPSIMD_TOKENS = 424
+SCALAR_CHANNELS = 264
+TAIL_TOKENS = 192
+PAIRED = [(0, 7, 0, 4), (1, 7, 0, 2)]
 HEAD_CHANNELS = 128
 MATMUL_ROWS = range(0, ROWS, 2)
 
@@ -125,7 +127,7 @@ def tile_mae_pa_kernel(tc, x_bytes, x_scale, eps, W11, b11, W31, b31, W32, b32, 
 
         def x_widen(r, c0=0, c1=2):
             if r not in x_wide:
-                x_wide[r] = work.tile([P, IMAGE], BF16, name="x_wide", bufs=8, align_bytes=64)
+                x_wide[r] = work.tile([P, IMAGE], BF16, name="x_wide", bufs=9, align_bytes=64)
             nc.scalar.copy(
                 out=x_wide[r][:, PASS * c0 : PASS * c1], in_=x_raw[r][:, PASS * c0 : PASS * c1].bitcast(FP8)
             )
@@ -177,9 +179,9 @@ def tile_mae_pa_kernel(tc, x_bytes, x_scale, eps, W11, b11, W31, b31, W32, b32, 
 
         w_laid, w3_laid, w_banks, w_codes, w_scales = {}, {}, {}, {}, {}
 
-        def w_target(g, c, tag=None):
+        def w_target(g, c):
             if (g, c) not in w_laid:
-                w_laid[g, c] = keep.tile([P, 4 * PASS], BF16, name=tag or f"w_laid{g % 2}", align_bytes=64)[:]
+                w_laid[g, c] = work.tile([P, 4 * PASS], BF16, name="w_laid", bufs=3, align_bytes=64)[:]
             return w_laid[g, c]
 
         def w_matmuls(g, c, a, width=BANK_CHANNELS):
@@ -235,7 +237,7 @@ def tile_mae_pa_kernel(tc, x_bytes, x_scale, eps, W11, b11, W31, b31, W32, b32, 
 
         def w3_target(g, w):
             if g not in w3_laid:
-                w3_laid[g] = work.tile([P, 8 * LATENT], BF16, name="w3_laid", bufs=3, align_bytes=64)[:]
+                w3_laid[g] = work.tile([P, 8 * LATENT], BF16, name="w3_laid", bufs=4, align_bytes=64)[:]
             return w3_laid[g][:, 4 * LATENT * w : 4 * LATENT * (w + 1)]
 
         def w3_copy(engine_copy, g, w):
@@ -293,7 +295,8 @@ def tile_mae_pa_kernel(tc, x_bytes, x_scale, eps, W11, b11, W31, b31, W32, b32, 
 
         def plane_tile(unit, tag):
             if unit not in planes:
-                planes[unit] = work.tile([P, 2, P * unit[3], 2], BF16, name=tag)
+                tag, bufs = (tag, 2 if unit[0] == 0 else 1) if unit[3] == 4 else ("planes_of_pair", 3)
+                planes[unit] = work.tile([P, 2, P * unit[3], 2], BF16, name=tag, bufs=bufs)
             return planes[unit]
 
         def scalar_bank(unit, t):
@@ -302,8 +305,11 @@ def tile_mae_pa_kernel(tc, x_bytes, x_scale, eps, W11, b11, W31, b31, W32, b32, 
             scalar_empty(unit, t, bank[:])
 
         def scalar_empty(unit, t, sums_of_t):
+            tile = plane_tile(unit, "planes_s")
             nc.scalar.activation(
-                out=plane_tile(unit, "planes_s")[:, t // 2, :, t % 2],
+                out=tile[:, t // 2, :, t % 2] if unit in PAIRED else tile[:].rearrange("p u n e -> p (u n e)")[
+                    :, P * unit[3] * t : P * unit[3] * (t + 1)
+                ],
                 in_=sums_of_t, func=RELU, bias=bias1[:, unit[1], t : t + 1],
             )
 
@@ -334,16 +340,37 @@ def tile_mae_pa_kernel(tc, x_bytes, x_scale, eps, W11, b11, W31, b31, W32, b32, 
                 op=ADD,
             )
 
-        def laid_tile(unit):
+        def laid_tile(unit, slot=None):
             if unit not in enc_laid:
-                enc_laid[unit] = work.tile([P, P * unit[3], 2, 2], BF16, name="enc_laid", bufs=3, align_bytes=64)
+                slot = (unit[0] + unit[1]) % 2 if slot is None else slot
+                enc_laid[unit] = keep.tile([P, P * unit[3], 2, 2], BF16, name=f"enc_laid{slot}", align_bytes=64)
             return enc_laid[unit]
 
-        def join(unit, a=0, b=None):
+        def join(unit, a=0, b=None, engine_copy=nc.vector.tensor_copy):
             b = b or unit[3]
-            nc.vector.tensor_copy(
+            engine_copy(
                 out=laid_tile(unit)[:, P * a : P * b, :, :],
                 in_=planes[unit][:, :, P * a : P * b, :].rearrange("p u n e -> p n u e"),
+            )
+
+        def four_planes(unit):
+            return planes[unit][:].rearrange("p u n e -> p (u n e)").rearrange("p (t n) -> p t n", t=4)
+
+        def laid_tokens(unit, a, b, into):
+            n0 = P * (into[2] - unit[2])
+            return laid_tile(into)[:, a - n0 : b - n0, :, :]
+
+        def lay(engine_copy, unit, a, b, into=None):
+            engine_copy(
+                out=laid_tokens(unit, a, b, into or unit).rearrange("p (m i) u e -> p m (u e) i", i=2),
+                in_=four_planes(unit)[:, :, a:b].rearrange("p t (m i) -> p m t i", i=2),
+            )
+
+        def lay_gpsimd(unit, a, b, into=None):
+            nc.gpsimd.tensor_scalar(
+                out=laid_tokens(unit, a, b, into or unit).rearrange("p n u e -> p n (u e)"),
+                in0=four_planes(unit)[:, :, a:b].rearrange("p t n -> p n t"),
+                scalar1=1.0, scalar2=0.0, op0=MULT, op1=ADD,
             )
 
         def join_relu(unit):
@@ -355,8 +382,8 @@ def tile_mae_pa_kernel(tc, x_bytes, x_scale, eps, W11, b11, W31, b31, W32, b32, 
         def enc_quant(unit, a=0, b=None):
             b = b or unit[3]
             if unit not in enc_codes:
-                enc_codes[unit] = work.tile([P, P * unit[3]], U32, name="x_wide", bufs=8, align_bytes=64)
-                enc_scales[unit] = work.tile([P, P * unit[3]], U8, name="enc_scales", bufs=8, align_bytes=64)
+                enc_codes[unit] = work.tile([P, P * unit[3]], U32, name="x_wide", bufs=9, align_bytes=64)
+                enc_scales[unit] = work.tile([P, P * unit[3]], U8, name="enc_scales", bufs=9, align_bytes=64)
             nc.vector.quantize_mx(
                 out=enc_codes[unit][:, P * a : P * b].bitcast(FP8X4),
                 scales=enc_scales[unit][:, P * a : P * b],
@@ -381,42 +408,38 @@ def tile_mae_pa_kernel(tc, x_bytes, x_scale, eps, W11, b11, W31, b31, W32, b32, 
                     stop=(g == GROUPS - 1 and r % 2 == 1),
                 )
 
-        biased, both, z = {}, {}, {}
+        late = {}
+        both = keep.tile([P, 2, ROWS, LATENT], F32, name="mu_sigma")
+        z = keep.tile([P, ROWS, LATENT], F32, name="z")
         out_views = [o.rearrange("(p r) l -> p r l", r=ROWS) for o in (out_0, out_1, out_2)]
 
-        def add_bias(i, a=0, b=2):
-            if i not in biased:
-                biased[i] = work.tile([P, 2, 2 * LATENT], F32, name="biased", bufs=4)
+        def add_bias(a, b):
             nc.vector.tensor_tensor(
-                out=biased[i][:, a:b, :], in0=bias3[:].unsqueeze(1).to_broadcast([P, b - a, 2 * LATENT]),
-                in1=acc[i][:, a:b, :], op=ADD,
+                out=late["biased"][:, a:b, :], in0=bias3[:].unsqueeze(1).to_broadcast([P, b - a, 2 * LATENT]),
+                in1=acc[a // 2][:, a % 2 : a % 2 + b - a, :], op=ADD,
             )
 
-        def mu_sigma(i, a=0, b=2, queue=nc.sync):
-            if i not in both:
-                both[i] = work.tile([P, 2, 2, LATENT], F32, name="mu_sigma", bufs=4)
+        def relus(a, b):
             nc.scalar.activation(
-                out=both[i][:, :, a:b, :], in_=biased[i][:, a:b, :].rearrange("p r (w l) -> p w r l", w=2), func=RELU
-            )
-            if b == 2:
-                for w in range(2):
-                    queue.dma_start(out=out_views[w][:, 2 * i : 2 * i + 2, :], in_=both[i][:, w, :, :])
-
-        def z_noise(i, a=0, b=2):
-            if i not in z:
-                z[i] = work.tile([P, 2, LATENT], F32, name="z", bufs=4)
-            nc.vector.scalar_tensor_tensor(
-                out=z[i][:, a:b, :], in0=biased[i][:, a:b, LATENT:], scalar=0.0,
-                in1=eps_sb[:, 2 * i + a : 2 * i + b, :], op0=MAX, op1=MULT,
+                out=both[:, :, a:b, :], in_=late["biased"][:, a:b, :].rearrange("p r (w l) -> p w r l", w=2), func=RELU
             )
 
-        def z_add_mu(i, a=0, b=2):
+        def store_mu_sigma(a, b, queue=nc.sync):
+            for w in range(2):
+                queue.dma_start(out=out_views[w][:, a:b, :], in_=both[:, w, a:b, :])
+
+        def z_noise(a, b):
             nc.vector.scalar_tensor_tensor(
-                out=z[i][:, a:b, :], in0=biased[i][:, a:b, :LATENT], scalar=0.0,
-                in1=z[i][:, a:b, :], op0=MAX, op1=ADD,
+                out=z[:, a:b, :], in0=late["biased"][:, a:b, LATENT:], scalar=0.0, in1=eps_sb[:, a:b, :], op0=MAX, op1=MULT
             )
-            if b == 2:
-                nc.sync.dma_start(out=out_views[2][:, 2 * i : 2 * i + 2, :], in_=z[i][:])
+
+        def z_add_mu(a, b):
+            nc.vector.scalar_tensor_tensor(
+                out=z[:, a:b, :], in0=late["biased"][:, a:b, :LATENT], scalar=0.0, in1=z[:, a:b, :], op0=MAX, op1=ADD
+            )
+
+        def store_z(a, b):
+            nc.sync.dma_start(out=out_views[2][:, a:b, :], in_=z[:, a:b, :])
 
         unused_bank = sums.tile([P, HALF], F32, name="sum0")
         warm_up(unused_bank, 256)
@@ -429,8 +452,6 @@ def tile_mae_pa_kernel(tc, x_bytes, x_scale, eps, W11, b11, W31, b31, W32, b32, 
             x_widen(r)
             x_turn(r)
             x_product(r)
-        w_target(0, 1, "w_laid1")
-        w_target(1, 0, "w_laid2")
         w_gpsimd(0, 0, 0, PASS)
         w_gpsimd(0, 1, 0, HEAD_CHANNELS)
         x_widen(4)
@@ -450,9 +471,7 @@ def tile_mae_pa_kernel(tc, x_bytes, x_scale, eps, W11, b11, W31, b31, W32, b32, 
         x_quant(0)
         w_quant(0, 1)
 
-        released = keep.tile([P, 2, 4 * PASS], BF16, name="x_laid0", align_bytes=64)
-        w_laid[1, 1] = released[:, 0, :]
-        w3_laid[0] = released[:, 1, : 8 * LATENT]
+        w_laid[1, 1] = keep.tile([P, 4 * PASS], BF16, name="x_laid0", align_bytes=64)[:]
         w_gpsimd(1, 1, 0, PASS)
         for w in range(2):
             w3_gpsimd(0, w)
@@ -460,96 +479,109 @@ def tile_mae_pa_kernel(tc, x_bytes, x_scale, eps, W11, b11, W31, b31, W32, b32, 
         x_turn(7)
         for r in range(4, ROWS):
             x_product(r)
-        for a in (0, BANK_CHANNELS):
-            w_matmuls(2, 0, a)
-            w_empty(2, 0, a)
+        w_matmuls(2, 0, BANK_CHANNELS)
+        w_scalar(2, 0, 0, BANK_CHANNELS)
+        w_empty(2, 0, BANK_CHANNELS)
         w3_matmuls(1, 0, 2)
         w3_empty(1, 0, 2)
-        w3_matmuls(2, 0, 1)
-        w3_empty(2, 0, 1)
+        w3_matmuls(2, 0, 2)
+        w_scalar(3, 0, 0, BANK_CHANNELS)
+        w3_empty(2, 0, 2)
         w_quant(1, 0)
         x_quant(1)
-        w_quant(2, 0)
         w_quant(1, 1)
+        w_quant(2, 0)
         for i in range(4):
             vector_bank((1, 0, 0, 4), i)
 
         g5, g6, g7 = GROUPS - 3, GROUPS - 2, GROUPS - 1
         for j in range(PERIODS):
-            v_unit, s_unit = (1, j, 0, 4), (0, j + 1, 0, 4)
+            v_unit, s_unit, before = (1, j, 0, 4), (0, j + 1, 0, 4), (0, j, 0, 4)
             last = j == PERIODS - 1
+            share = SCALAR_CHANNELS
             if last:
-                for m in range(10, 14):
+                w_scalar(j + 2, 1, 0, share)
+                for m in range(12, 16):
                     w3_copy(nc.scalar.copy, m // 2, m % 2)
             else:
-                w_scalar(j + 3, 0, 0, PASS - VECTOR_CHANNELS)
-            w_scalar(j + 2, 1, GPSIMD_CHANNELS, PASS)
-            w_gpsimd(j + 2, 1, 0, GPSIMD_CHANNELS)
+                w_scalar(j + 3, 0, BANK_CHANNELS if j == 0 else 0, PASS)
+                w_scalar(j + 2, 1, 0, share)
+            if j == 0:
+                enc_laid[before] = keep.tile([P, HALF, 2, 2], BF16, name="x_laid0", align_bytes=64)
+            lay_gpsimd(before, 0, GPSIMD_TOKENS)
             for i in range(4):
                 vector_add(v_unit, i)
-            m = 15 if last else 5 + j
+            m = 6 + j
             w3_matmuls(m // 2, m % 2, m % 2 + 1)
             w3_empty(m // 2, m % 2, m % 2 + 1)
             scalar_unit(s_unit)
             if 0 < j < PERIODS - 1:
                 second_stage((1, j - 1, 0, 4))
-            join((0, j, 0, 4))
-            if last:
-                join_relu(v_unit)
-                w_quant(g7, 1)
-                w3_quant(j)
-            else:
-                w_vector(j + 3, 0, PASS - VECTOR_CHANNELS, PASS)
-                join_relu(v_unit)
-                w3_quant(j)
-                w_quant(j + 2, 1)
-            enc_quant((0, j, 0, 4))
+            w_vector(j + 2, 1, share, PASS)
+            lay(nc.vector.tensor_copy, before, GPSIMD_TOKENS, HALF)
+            join_relu(v_unit)
+            w_quant(j + 2, 1)
+            enc_quant(before)
+            w3_quant(j)
             if not last:
                 for i in range(4):
                     vector_bank((1, j + 1, 0, 4), i)
-                second_stage((0, j, 0, 4))
-                w_quant(j + 3, 0)
+                second_stage(before)
                 enc_quant(v_unit)
+                w_quant(j + 3, 0)
 
         s6, s7 = (0, g6, 0, 4), (0, g7, 0, 4)
         v6 = [(1, g6, 0, 2), (1, g6, 2, 2)]
         s7b = [(1, g7, 0, 2), (1, g7, 2, 2)]
-        w3_copy(nc.vector.tensor_copy, g7, 0)
-        w3_quant(g6)
+        s6_rows = [(0, g6, 0, 2), (0, g6, 2, 2)]
+        late["biased"] = keep.tile([P, ROWS, 2 * LATENT], F32, name="x_laid1", align_bytes=64)
         enc_quant((1, g5, 0, 4))
+        w3_quant(g6)
         vector_bank(v6[0], 0)
         scalar_bank(s7, 0)
-        second_stage((0, g5, 0, 4))
-        scalar_bank(s7, 2)
         vector_bank(v6[0], 1)
+        scalar_bank(s7, 2)
+        second_stage((0, g5, 0, 4))
+        laid_tile(s6_rows[0], 0)
+        lay_gpsimd(s6, 0, TAIL_TOKENS, s6_rows[0])
         vector_add(v6[0], 0)
-        w3_quant(g7)
-        join(s6)
         vector_add(v6[0], 1)
-        enc_quant(s6)
         scalar_bank(s7, 1)
-        scalar_bank(s7, 3)
         vector_bank(v6[1], 0)
-        scalar_pair_bank(s7b[0], 0)
-        second_stage(s6)
-        join_relu(v6[0])
-        vector_add(v6[1], 0)
-        enc_quant(v6[0])
-        scalar_pair_bank(s7b[0], 1)
+        scalar_bank(s7, 3)
         vector_bank(v6[1], 1)
-        join(s7, 0, 2)
-        join(s7, 2, 4)
-        enc_quant(s7, 0, 2)
-        enc_quant(s7, 2, 4)
+        laid_tile(v6[0], 1)
+        w3_quant(g7)
+        join_relu(v6[0])
+        lay(nc.vector.tensor_copy, s6, TAIL_TOKENS, PAIR, s6_rows[0])
+        enc_quant(v6[0])
+        enc_quant(s6_rows[0])
+        laid_tile(s6_rows[1], 1)
+        lay_gpsimd(s6, PAIR, PAIR + TAIL_TOKENS, s6_rows[1])
+        vector_add(v6[1], 0)
         vector_add(v6[1], 1)
-        scalar_pair_bank(s7b[1], 0)
-        second_stage(s7)
-        scalar_pair_bank(s7b[1], 1)
-        join(s7b[0])
+        scalar_pair_bank(s7b[0], 0)
+        second_stage(s6_rows[0])
+        scalar_pair_bank(s7b[0], 1)
+        laid_tile(s7, 0)
+        laid_tile(v6[1], 2)
+        join(s7, 0, 2)
+        lay(nc.vector.tensor_copy, s6, PAIR + TAIL_TOKENS, HALF, s6_rows[1])
+        enc_quant(s7, 0, 2)
+        join(s7, 2, 4)
+        enc_quant(s6_rows[1])
         join_relu(v6[1])
-        enc_quant(s7b[0])
-        add_bias(0)
+        enc_quant(s7, 2, 4)
+        scalar_pair_bank(s7b[1], 0)
+        second_stage(s7, 0, 2)
+        scalar_pair_bank(s7b[1], 1)
+        second_stage(s6_rows[1])
+        second_stage(s7, 2, 4)
+        laid_tile(s7b[0], 1)
+        laid_tile(s7b[1], 0)
+        join(s7b[0])
         enc_quant(v6[1])
+        enc_quant(s7b[0])
         for g in (g5 - 1, g5):
             second_stage((1, g, 0, 4), 0, 2)
         second_stage(v6[0])
@@ -557,22 +589,26 @@ def tile_mae_pa_kernel(tc, x_bytes, x_scale, eps, W11, b11, W31, b31, W32, b32, 
         for g in (g5 - 1, g5):
             second_stage((1, g, 0, 4), 2, 4)
         second_stage(v6[1])
-        add_bias(1)
-        join(s7b[1])
-        z_noise(0)
-        enc_quant(s7b[1])
+        lay_gpsimd(s7b[1], P, PAIR)
+        lay(nc.scalar.copy, s7b[1], 0, P)
+        for a in (0, 2, 4):
+            add_bias(a, a + 2)
+            relus(a, a + 2)
+            store_mu_sigma(a, a + 2)
+        enc_quant(s7b[1], 0, 1)
+        enc_quant(s7b[1], 1, 2)
         second_stage(s7b[1])
-        mu_sigma(0)
-        mu_sigma(1)
-        add_bias(2)
-        z_add_mu(0)
-        z_noise(1)
-        mu_sigma(2)
-        for r in range(2):
-            add_bias(3, r, r + 1)
-        z_add_mu(1)
-        z_noise(2)
-        mu_sigma(3, 0, 2, nc.scalar)
-        z_noise(3)
-        z_add_mu(2)
-        z_add_mu(3)
+        z_noise(0, 4)
+        z_noise(4, 6)
+        add_bias(6, 7)
+        add_bias(7, 8)
+        z_add_mu(0, 4)
+        store_z(0, 4)
+        relus(6, 7)
+        relus(7, 8)
+        store_mu_sigma(6, 8, nc.scalar)
+        z_noise(6, 8)
+        z_add_mu(4, 6)
+        store_z(4, 6)
+        z_add_mu(6, 8)
+        store_z(6, 8)

@@ -32,6 +32,7 @@ PERIODS = 6
 GPSIMD_TOKENS = 424
 SCALAR_CHANNELS = 264
 TAIL_TOKENS = 192
+BIAS_RUN = 16
 PAIRED = [(0, 7, 0, 4), (1, 7, 0, 2)]
 HEAD_CHANNELS = 128
 MATMUL_ROWS = range(0, ROWS, 2)
@@ -81,11 +82,12 @@ def tile_mae_pa_kernel(tc, x_bytes, x_scale, eps, W11, b11, W31, b31, W32, b32, 
                 for g in range(g0, g1):
                     w3_raw[g, w] = tile[:, g - g0, :]
 
-        scale = keep.tile([P, 2, 4], F32, name="scale")
+        scale_cols = keep.tile([P, 2, 4], F32, name="scale_cols")
+        scale = keep.tile([P, 2, P, 4], F32, name="scale")
         bias1 = keep.tile([P, GROUPS, 4], BF16, name="bias1")
         b11_view = b11.rearrange("(g p t) -> p g t", p=P, t=4)
         load_x(0, 1)
-        nc.sync.dma_start(out=scale[:], in_=x_scale.rearrange("o (c p t) -> p (o c) t", p=P, t=4))
+        nc.sync.dma_start(out=scale_cols[:], in_=x_scale.rearrange("o (c p t) -> p (o c) t", p=P, t=4))
         load_x(1, 2)
         load_x(2, 4)
         load_w11(0, 0, 1)
@@ -162,10 +164,7 @@ def tile_mae_pa_kernel(tc, x_bytes, x_scale, eps, W11, b11, W31, b31, W32, b32, 
                 x_laid[h] = keep.tile([P, 2, HALF, 4], BF16, name=f"x_laid{h}", align_bytes=64)
             nc.vector.tensor_tensor(
                 out=x_laid[h][:, c0:c1, P * row : P * (row + 1), :].rearrange("p c n (u e) -> p c n u e", u=2),
-                in0=scale[:, c0:c1, :]
-                .rearrange("p c (u e) -> p c u e", u=2)
-                .unsqueeze(2)
-                .to_broadcast([P, c1 - c0, P, 2, 2]),
+                in0=scale[:, c0:c1, :, :].rearrange("p c n (u e) -> p c n u e", u=2),
                 in1=x_turned[r, c0].rearrange("p u c (n e) -> p c n u e", e=2),
                 op=MULT,
             )
@@ -331,12 +330,23 @@ def tile_mae_pa_kernel(tc, x_bytes, x_scale, eps, W11, b11, W31, b31, W32, b32, 
             for e in range(2):
                 passes(bank[:, e, :], unit, 2 * u + e, slice(n0, n0 + PAIR))
 
+        bias_runs = keep.tile([P, 2 * GROUPS, BIAS_RUN, 2], BF16, name="bias_runs")
+
+        def lay_bias(g0, g1):
+            nc.vector.tensor_copy(
+                out=bias_runs[:, 2 * g0 : 2 * g1, :, :],
+                in_=bias1[:, g0:g1, :].rearrange("p g (u e) -> p (g u) e", e=2).unsqueeze(2)
+                .to_broadcast([P, 2 * (g1 - g0), BIAS_RUN, 2]),
+            )
+
         def vector_add(unit, i):
             q, u = divmod(i, 2)
             nc.vector.tensor_tensor(
-                out=plane_tile(unit, "planes_v")[:, u, PAIR * q : PAIR * (q + 1), :],
-                in0=bias1[:, unit[1], 2 * u : 2 * u + 2].unsqueeze(1).to_broadcast([P, PAIR, 2]),
-                in1=v_banks[unit, i][:].rearrange("p e n -> p n e"),
+                out=plane_tile(unit, "planes_v")[:, u, PAIR * q : PAIR * (q + 1), :].rearrange(
+                    "p (m n) e -> p m n e", n=BIAS_RUN
+                ),
+                in0=bias_runs[:, 2 * unit[1] + u, :, :].unsqueeze(1).to_broadcast([P, PAIR // BIAS_RUN, BIAS_RUN, 2]),
+                in1=v_banks[unit, i][:].rearrange("p e (m n) -> p m n e", n=BIAS_RUN),
                 op=ADD,
             )
 
@@ -444,6 +454,7 @@ def tile_mae_pa_kernel(tc, x_bytes, x_scale, eps, W11, b11, W31, b31, W32, b32, 
         unused_bank = sums.tile([P, HALF], F32, name="sum0")
         warm_up(unused_bank, 256)
         warm_up(unused_bank, 256)
+        nc.vector.tensor_copy(out=scale[:], in_=scale_cols[:].unsqueeze(2).to_broadcast([P, 2, P, 4]))
         for c in range(2):
             x_widen(0, c, c + 1)
             x_turn(0, c, c + 1)
@@ -489,6 +500,7 @@ def tile_mae_pa_kernel(tc, x_bytes, x_scale, eps, W11, b11, W31, b31, W32, b32, 
         w3_empty(2, 0, 2)
         w_quant(1, 0)
         x_quant(1)
+        lay_bias(0, 4)
         w_quant(1, 1)
         w_quant(2, 0)
         for i in range(4):
@@ -520,6 +532,8 @@ def tile_mae_pa_kernel(tc, x_bytes, x_scale, eps, W11, b11, W31, b31, W32, b32, 
             w_vector(j + 2, 1, share, PASS)
             lay(nc.vector.tensor_copy, before, GPSIMD_TOKENS, HALF)
             join_relu(v_unit)
+            if j == 2:
+                lay_bias(4, GROUPS)
             w_quant(j + 2, 1)
             enc_quant(before)
             w3_quant(j)

@@ -29,8 +29,8 @@ PAIR = 2 * P
 BANK_CHANNELS = 256
 PERIODS = 6
 
-GPSIMD_TOKENS = 424
-SCALAR_CHANNELS = 264
+GPSIMD_TOKENS = 448
+SCALAR_CHANNELS = 304
 TAIL_TOKENS = 192
 BIAS_RUN = 16
 PAIRED = [(0, 7, 0, 4), (1, 7, 0, 2)]
@@ -326,7 +326,9 @@ def tile_mae_pa_kernel(tc, x_bytes, x_scale, eps, W11, b11, W31, b31, W32, b32, 
         def vector_bank(unit, i):
             q, u = divmod(i, 2)
             n0 = P * unit[2] + PAIR * q
-            v_banks[unit, i] = bank = psum.tile([P, 2, PAIR], F32, name="bank")
+            if (unit, i) not in v_banks:
+                v_banks[unit, i] = psum.tile([P, 2, PAIR], F32, name="bank")
+            bank = v_banks[unit, i]
             for e in range(2):
                 passes(bank[:, e, :], unit, 2 * u + e, slice(n0, n0 + PAIR))
 
@@ -338,6 +340,12 @@ def tile_mae_pa_kernel(tc, x_bytes, x_scale, eps, W11, b11, W31, b31, W32, b32, 
                 in_=bias1[:, g0:g1, :].rearrange("p g (u e) -> p (g u) e", e=2).unsqueeze(2)
                 .to_broadcast([P, 2 * (g1 - g0), BIAS_RUN, 2]),
             )
+
+        def vector_banks(unit):
+            for i in range(4):
+                v_banks[unit, i] = psum.tile([P, 2, PAIR], F32, name="bank")
+            for i in (1, 0, 3, 2):
+                vector_bank(unit, i)
 
         def vector_add(unit, i):
             q, u = divmod(i, 2)
@@ -530,16 +538,20 @@ def tile_mae_pa_kernel(tc, x_bytes, x_scale, eps, W11, b11, W31, b31, W32, b32, 
             if 0 < j < PERIODS - 1:
                 second_stage((1, j - 1, 0, 4))
             w_vector(j + 2, 1, share, PASS)
-            lay(nc.vector.tensor_copy, before, GPSIMD_TOKENS, HALF)
             join_relu(v_unit)
             if j == 2:
                 lay_bias(4, GROUPS)
-            w_quant(j + 2, 1)
-            enc_quant(before)
+            lay(nc.vector.tensor_copy, before, GPSIMD_TOKENS, HALF)
+            if last:
+                w_quant(j + 2, 1)
             w3_quant(j)
+            if last:
+                enc_quant(before)
+            else:
+                enc_quant(before)
+                w_quant(j + 2, 1)
             if not last:
-                for i in range(4):
-                    vector_bank((1, j + 1, 0, 4), i)
+                vector_banks((1, j + 1, 0, 4))
                 second_stage(before)
                 enc_quant(v_unit)
                 w_quant(j + 3, 0)

@@ -27,14 +27,12 @@ ROWS = TOKENS // P
 HALF = TOKENS // 2
 PAIR = 2 * P
 BANK_CHANNELS = 256
-PERIODS = 6
+PERIODS = GROUPS - 2
 
 GPSIMD_TOKENS = 448
-SCALAR_CHANNELS = 304
-TAIL_TOKENS = 192
+GPSIMD_TAIL_TOKENS = 192
+SCALAR_CHANNELS = 288
 BIAS_RUN = 16
-PAIRED = [(0, 7, 0, 4), (1, 7, 0, 2)]
-HEAD_CHANNELS = 128
 MATMUL_ROWS = range(0, ROWS, 2)
 
 
@@ -61,6 +59,7 @@ def tile_mae_pa_kernel(tc, x_bytes, x_scale, eps, W11, b11, W31, b31, W32, b32, 
         x_view = x_bytes.rearrange("(p r) k -> p (r k)", r=ROWS)
         w11_view = W11.rearrange("(c p j) n -> c p j n", c=2, j=4)
         w3_views = [w.rearrange("(g p j) l -> p g (j l)", p=P, j=4) for w in (W31, W32)]
+        b11_view = b11.rearrange("(g p t) -> p g t", p=P, t=4)
         x_raw, w11_raw, w3_raw = {}, {}, {}
 
         def load_x(r0, r1):
@@ -85,7 +84,6 @@ def tile_mae_pa_kernel(tc, x_bytes, x_scale, eps, W11, b11, W31, b31, W32, b32, 
         scale_cols = keep.tile([P, 2, 4], F32, name="scale_cols")
         scale = keep.tile([P, 2, P, 4], F32, name="scale")
         bias1 = keep.tile([P, GROUPS, 4], BF16, name="bias1")
-        b11_view = b11.rearrange("(g p t) -> p g t", p=P, t=4)
         load_x(0, 1)
         nc.sync.dma_start(out=scale_cols[:], in_=x_scale.rearrange("o (c p t) -> p (o c) t", p=P, t=4))
         load_x(1, 2)
@@ -109,8 +107,8 @@ def tile_mae_pa_kernel(tc, x_bytes, x_scale, eps, W11, b11, W31, b31, W32, b32, 
         load_w11(0, 5, 7)
         load_w11(1, 4, 6)
         load_w3(5, GROUPS)
-        load_w11(0, 7, 8)
-        load_w11(1, 6, 8)
+        load_w11(0, 7, GROUPS)
+        load_w11(1, 6, GROUPS)
         bias3 = keep.tile([P, 2 * LATENT], BF16, name="bias3")
         nc.sync.dma_start(out=bias3[:, :LATENT], in_=b31.partition_broadcast(P))
         nc.sync.dma_start(out=bias3[:, LATENT:], in_=b32.partition_broadcast(P))
@@ -123,13 +121,23 @@ def tile_mae_pa_kernel(tc, x_bytes, x_scale, eps, W11, b11, W31, b31, W32, b32, 
         def warm_up(bank, columns):
             nc.tensor.matmul(out=bank[:, :columns], lhsT=zeros[:, :P], rhs=zeros[:, :columns], start=True, stop=True)
 
-        x_codes = [keep.tile([P, 2, HALF], U32, name=f"x_codes{h}", align_bytes=64) for h in range(2)]
-        x_scales = [keep.tile([P, 2, HALF], U8, name=f"x_scales{h}", align_bytes=64) for h in range(2)]
+        def quantize(codes, scales, laid):
+            nc.vector.quantize_mx(out=codes.bitcast(FP8X4), scales=scales, in_=laid)
+
+        def laid_buffer(name):
+            return keep.tile([P, 2, 4 * HALF], BF16, name=name, align_bytes=64)
+
+        def codes_tiles(name, columns, bufs):
+            codes = work.tile([P, columns], U32, name=f"{name}_codes", bufs=bufs, align_bytes=64)
+            scales = work.tile([P, columns], U8, name=f"{name}_scales", bufs=bufs, align_bytes=64)
+            return codes, scales
+
+        x_quantised = [codes_tiles("x", 2 * HALF, 2) for h in range(2)]
         x_wide, x_turned, x_laid = {}, {}, {}
 
         def x_widen(r, c0=0, c1=2):
             if r not in x_wide:
-                x_wide[r] = work.tile([P, IMAGE], BF16, name="x_wide", bufs=9, align_bytes=64)
+                x_wide[r] = work.tile([P, IMAGE], BF16, name="enc_codes", bufs=4, align_bytes=64)
             nc.scalar.copy(
                 out=x_wide[r][:, PASS * c0 : PASS * c1], in_=x_raw[r][:, PASS * c0 : PASS * c1].bitcast(FP8)
             )
@@ -161,30 +169,32 @@ def tile_mae_pa_kernel(tc, x_bytes, x_scale, eps, W11, b11, W31, b31, W32, b32, 
         def x_product(r, c0=0, c1=2):
             h, row = divmod(r, 4)
             if h not in x_laid:
-                x_laid[h] = keep.tile([P, 2, HALF, 4], BF16, name=f"x_laid{h}", align_bytes=64)
+                x_laid[h] = laid_buffer(f"laid{h}")
             nc.vector.tensor_tensor(
-                out=x_laid[h][:, c0:c1, P * row : P * (row + 1), :].rearrange("p c n (u e) -> p c n u e", u=2),
+                out=x_laid[h][:, c0:c1, PASS * row : PASS * (row + 1)].rearrange("p c (n u e) -> p c n u e", u=2, e=2),
                 in0=scale[:, c0:c1, :, :].rearrange("p c n (u e) -> p c n u e", u=2),
                 in1=x_turned[r, c0].rearrange("p u c (n e) -> p c n u e", e=2),
                 op=MULT,
             )
 
         def x_quant(h):
-            nc.vector.quantize_mx(
-                out=x_codes[h][:].rearrange("p c n -> p (c n)").bitcast(FP8X4),
-                scales=x_scales[h][:].rearrange("p c n -> p (c n)"),
-                in_=x_laid[h][:].rearrange("p c n t -> p (c n t)"),
-            )
+            quantize(x_quantised[h][0][:], x_quantised[h][1][:], x_laid[h][:].rearrange("p c n -> p (c n)"))
 
-        w_laid, w3_laid, w_banks, w_codes, w_scales = {}, {}, {}, {}, {}
+        w_laid, w_quantised, banks = {}, {}, {}
+
+        def w_buffer(name, passes):
+            laid = laid_buffer(name)
+            codes, scales = codes_tiles("w", 2 * PASS, 4)
+            for i, key in enumerate(passes):
+                w_laid[key] = (laid, i)
+                w_quantised[key] = (codes, scales, i)
 
         def w_target(g, c):
-            if (g, c) not in w_laid:
-                w_laid[g, c] = work.tile([P, 4 * PASS], BF16, name="w_laid", bufs=3, align_bytes=64)[:]
-            return w_laid[g, c]
+            laid, i = w_laid[g, c]
+            return laid[:, i, :]
 
-        def w_matmuls(g, c, a, width=BANK_CHANNELS):
-            w_banks[g, c, a] = bank = psum.tile([P, 2 * BANK_CHANNELS], F32, name="bank")
+        def w_matmuls(g, c, a, width):
+            banks[g, c, a] = bank = psum.tile([P, 2 * BANK_CHANNELS], F32, name="bank")
             for n0 in range(0, width, P):
                 nc.tensor.matmul(
                     out=bank[:, 2 * n0 : 2 * (n0 + P)].bitcast(BF16),
@@ -194,12 +204,12 @@ def tile_mae_pa_kernel(tc, x_bytes, x_scale, eps, W11, b11, W31, b31, W32, b32, 
                     stop=True,
                 )
 
-        def w_empty(g, c, a, width=BANK_CHANNELS):
+        def w_empty(g, c, a, width):
             nc.scalar.copy(
                 out=w_target(g, c).bitcast(F32).rearrange("p (t m u) -> p t m u", t=4, u=2)[
                     :, :, a // 4 : (a + width) // 4, :
                 ],
-                in_=w_banks[g, c, a][:, : 2 * width].rearrange("p (m t u) -> p t m u", t=4, u=2),
+                in_=banks[g, c, a][:, : 2 * width].rearrange("p (m t u) -> p t m u", t=4, u=2),
             )
 
         def w_copy(engine_copy, g, c, a, b):
@@ -223,114 +233,107 @@ def tile_mae_pa_kernel(tc, x_bytes, x_scale, eps, W11, b11, W31, b31, W32, b32, 
                 scalar1=1.0, scalar2=0.0, op0=MULT, op1=ADD,
             )
 
-        def w_quant(g, c):
-            if g not in w_codes:
-                w_codes[g] = work.tile([P, 2, PASS], U32, name="w_codes", bufs=4, align_bytes=64)
-                w_scales[g] = work.tile([P, 2, PASS], U8, name="w_scales", bufs=4, align_bytes=64)
-            nc.vector.quantize_mx(
-                out=w_codes[g][:, c, :].bitcast(FP8X4), scales=w_scales[g][:, c, :], in_=w_laid[g, c]
-            )
+        def w_quant(g, c, passes=1):
+            laid, i = w_laid[g, c]
+            codes, scales = w_quantised[g, c][:2]
+            cols = slice(PASS * i, PASS * (i + passes))
+            quantize(codes[:, cols], scales[:, cols], laid[:, i : i + passes, :].rearrange("p c n -> p (c n)"))
 
-        w3_codes = keep.tile([P, GROUPS, 2 * LATENT], U32, name="w3_codes", align_bytes=64)
-        w3_scales = keep.tile([P, GROUPS, 2 * LATENT], U8, name="w3_scales", align_bytes=64)
+        w3_laid = {}
+        w3_codes, w3_scales = codes_tiles("w3", GROUPS * 2 * LATENT, 1)
 
-        def w3_target(g, w):
+        def w3_target(m, count=1):
+            g, w = divmod(m, 2)
             if g not in w3_laid:
-                w3_laid[g] = work.tile([P, 8 * LATENT], BF16, name="w3_laid", bufs=4, align_bytes=64)[:]
-            return w3_laid[g][:, 4 * LATENT * w : 4 * LATENT * (w + 1)]
+                w3_laid[g] = work.tile([P, 8 * LATENT], BF16, name="w3_laid", bufs=4, align_bytes=64)
+            return w3_laid[g][:, 4 * LATENT * w : 4 * LATENT * (w + count)]
 
-        def w3_copy(engine_copy, g, w):
-            engine_copy(
-                out=w3_target(g, w).rearrange("p (m i j) -> p m j i", i=2, j=4),
-                in_=w3_raw[g, w].rearrange("p (j m i) -> p m j i", j=4, i=2),
+        def w3_scalar(m):
+            nc.scalar.copy(
+                out=w3_target(m).rearrange("p (l i j) -> p l j i", i=2, j=4),
+                in_=w3_raw[divmod(m, 2)].rearrange("p (j l i) -> p l j i", j=4, i=2),
             )
 
-        def w3_gpsimd(g, w):
+        def w3_gpsimd(m):
             nc.gpsimd.tensor_scalar(
-                out=w3_target(g, w).rearrange("p (l j) -> p l j", j=4),
-                in0=w3_raw[g, w].rearrange("p (j l) -> p l j", j=4),
+                out=w3_target(m).rearrange("p (l j) -> p l j", j=4),
+                in0=w3_raw[divmod(m, 2)].rearrange("p (j l) -> p l j", j=4),
                 scalar1=1.0, scalar2=0.0, op0=MULT, op1=ADD,
             )
 
-        def w3_matmuls(g, w0, w1):
-            w_banks[g, w0] = bank = psum.tile([P, 4 * LATENT], F32, name="bank")
-            for w in range(w0, w1):
+        def w3_matmuls(m, count):
+            banks[m] = bank = psum.tile([P, 4 * LATENT], F32, name="bank")
+            for i in range(count):
                 nc.tensor.matmul(
-                    out=bank[:, 2 * LATENT * (w - w0) : 2 * LATENT * (w - w0 + 1)].bitcast(BF16),
+                    out=bank[:, 2 * LATENT * i : 2 * LATENT * (i + 1)].bitcast(BF16),
                     lhsT=ident_bf[:],
-                    rhs=w3_raw[g, w].rearrange("p (j l) -> p l j", j=4),
+                    rhs=w3_raw[divmod(m + i, 2)].rearrange("p (j l) -> p l j", j=4),
                     start=True,
                     stop=True,
                 )
 
-        def w3_empty(g, w0, w1):
-            w3_target(g, w0)
-            nc.scalar.copy(
-                out=w3_laid[g][:, 4 * LATENT * w0 : 4 * LATENT * w1].bitcast(F32),
-                in_=w_banks[g, w0][:, : 2 * LATENT * (w1 - w0)],
-            )
+        def w3_empty(m, count):
+            nc.scalar.copy(out=w3_target(m, count).bitcast(F32), in_=banks[m][:, : 2 * LATENT * count])
 
-        def w3_quant(g, w0=0, w1=2):
-            cols = slice(LATENT * w0, LATENT * w1)
-            nc.vector.quantize_mx(
-                out=w3_codes[:, g, cols].bitcast(FP8X4), scales=w3_scales[:, g, cols],
-                in_=w3_laid[g][:, 4 * LATENT * w0 : 4 * LATENT * w1],
-            )
+        def w3_quant(g):
+            cols = slice(2 * LATENT * g, 2 * LATENT * (g + 1))
+            quantize(w3_codes[:, cols], w3_scales[:, cols], w3_laid[g][:])
 
-        planes, v_banks, enc_laid, enc_codes, enc_scales = {}, {}, {}, {}, {}
+        emptied, enc_laid, enc_quantised = {}, {}, {}
 
-        def passes(out, unit, t, cols):
-            h, g = unit[:2]
+        def passes(out, g, t, row0, rows):
+            h, row = divmod(row0, 4)
             for c in range(2):
+                w_codes, w_scales, i = w_quantised[g, c]
+                w_cols = slice(PASS * i + P * t, PASS * i + P * (t + 1))
+                x_cols = slice(HALF * c + P * row, HALF * c + P * (row + rows))
                 nc.tensor.matmul_mx(
                     out=out,
-                    lhsT=w_codes[g][:, c, P * t : P * (t + 1)].bitcast(FP8X4),
-                    lhsT_scale=w_scales[g][:, c, P * t : P * (t + 1)],
-                    rhs=x_codes[h][:, c, cols].bitcast(FP8X4),
-                    rhs_scale=x_scales[h][:, c, cols],
+                    lhsT=w_codes[:, w_cols].bitcast(FP8X4),
+                    lhsT_scale=w_scales[:, w_cols],
+                    rhs=x_quantised[h][0][:, x_cols].bitcast(FP8X4),
+                    rhs_scale=x_quantised[h][1][:, x_cols],
                     start=(c == 0),
                     stop=(c == 1),
                 )
 
-        def plane_tile(unit, tag):
-            if unit not in planes:
-                tag, bufs = (tag, 2 if unit[0] == 0 else 1) if unit[3] == 4 else ("planes_of_pair", 3)
-                planes[unit] = work.tile([P, 2, P * unit[3], 2], BF16, name=tag, bufs=bufs)
-            return planes[unit]
+        def emptied_tile(unit):
+            if unit not in emptied:
+                g, row0, rows = unit
+                tag, bufs = (f"emptied{row0}", 2 - row0 // 4) if rows == 4 else ("emptied_pair", 3)
+                emptied[unit] = work.tile([P, 4 * P * rows], BF16, name=tag, bufs=bufs)
+            return emptied[unit][:]
 
-        def scalar_bank(unit, t):
-            bank = psum.tile([P, HALF], F32, name="bank")
-            passes(bank[:], unit, t, slice(0, HALF))
-            scalar_empty(unit, t, bank[:])
+        def by_slot(unit):
+            return emptied_tile(unit).rearrange("p (t n) -> p t n", t=4)
 
-        def scalar_empty(unit, t, sums_of_t):
-            tile = plane_tile(unit, "planes_s")
+        def by_plane(unit):
+            return emptied_tile(unit).rearrange("p (u n e) -> p u n e", u=2, e=2)
+
+        def scalar_empty(unit, t, sums_of_t, planes):
             nc.scalar.activation(
-                out=tile[:, t // 2, :, t % 2] if unit in PAIRED else tile[:].rearrange("p u n e -> p (u n e)")[
-                    :, P * unit[3] * t : P * unit[3] * (t + 1)
-                ],
-                in_=sums_of_t, func=RELU, bias=bias1[:, unit[1], t : t + 1],
+                out=by_plane(unit)[:, t // 2, :, t % 2] if planes else by_slot(unit)[:, t, :],
+                in_=sums_of_t, func=RELU, bias=bias1[:, unit[0], t : t + 1],
             )
 
-        def scalar_unit(unit):
-            for t in (0, 2, 1, 3):
-                scalar_bank(unit, t)
+        def scalar_bank(unit, t, planes=False):
+            bank = psum.tile([P, HALF], F32, name="bank")
+            passes(bank[:], unit[0], t, unit[1], 4)
+            scalar_empty(unit, t, bank[:], planes)
 
-        def scalar_pair_bank(unit, e):
+        def scalar_pair_bank(unit, e, planes=False):
             bank = psum.tile([P, 2, PAIR], F32, name="bank")
             for u in range(2):
-                passes(bank[:, u, :], unit, 2 * u + e, slice(P * unit[2], P * unit[2] + PAIR))
+                passes(bank[:, u, :], unit[0], 2 * u + e, unit[1], 2)
             for u in range(2):
-                scalar_empty(unit, 2 * u + e, bank[:, u, :])
+                scalar_empty(unit, 2 * u + e, bank[:, u, :], planes)
 
-        def vector_bank(unit, i):
-            q, u = divmod(i, 2)
-            n0 = P * unit[2] + PAIR * q
-            if (unit, i) not in v_banks:
-                v_banks[unit, i] = psum.tile([P, 2, PAIR], F32, name="bank")
-            bank = v_banks[unit, i]
-            for e in range(2):
-                passes(bank[:, e, :], unit, 2 * u + e, slice(n0, n0 + PAIR))
+        def vector_banks(unit, numbers):
+            for i in numbers:
+                banks[unit, i] = psum.tile([P, 2, PAIR], F32, name="bank")
+            for i in reversed(numbers):
+                for e in range(2):
+                    passes(banks[unit, i][:, e, :], unit[0], 2 * (i % 2) + e, unit[1] + 2 * (i // 2), 2)
 
         bias_runs = keep.tile([P, 2 * GROUPS, BIAS_RUN, 2], BF16, name="bias_runs")
 
@@ -341,95 +344,83 @@ def tile_mae_pa_kernel(tc, x_bytes, x_scale, eps, W11, b11, W31, b31, W32, b32, 
                 .to_broadcast([P, 2 * (g1 - g0), BIAS_RUN, 2]),
             )
 
-        def vector_banks(unit):
-            for i in range(4):
-                v_banks[unit, i] = psum.tile([P, 2, PAIR], F32, name="bank")
-            for i in (1, 0, 3, 2):
-                vector_bank(unit, i)
-
         def vector_add(unit, i):
             q, u = divmod(i, 2)
             nc.vector.tensor_tensor(
-                out=plane_tile(unit, "planes_v")[:, u, PAIR * q : PAIR * (q + 1), :].rearrange(
-                    "p (m n) e -> p m n e", n=BIAS_RUN
-                ),
-                in0=bias_runs[:, 2 * unit[1] + u, :, :].unsqueeze(1).to_broadcast([P, PAIR // BIAS_RUN, BIAS_RUN, 2]),
-                in1=v_banks[unit, i][:].rearrange("p e (m n) -> p m n e", n=BIAS_RUN),
+                out=by_plane(unit)[:, u, PAIR * q : PAIR * (q + 1), :].rearrange("p (m n) e -> p m n e", n=BIAS_RUN),
+                in0=bias_runs[:, 2 * unit[0] + u, :, :].unsqueeze(1).to_broadcast([P, PAIR // BIAS_RUN, BIAS_RUN, 2]),
+                in1=banks[unit, i][:].rearrange("p e (m n) -> p m n e", n=BIAS_RUN),
                 op=ADD,
             )
 
-        def laid_tile(unit, slot=None):
-            if unit not in enc_laid:
-                slot = (unit[0] + unit[1]) % 2 if slot is None else slot
-                enc_laid[unit] = keep.tile([P, P * unit[3], 2, 2], BF16, name=f"enc_laid{slot}", align_bytes=64)
-            return enc_laid[unit]
+        def enc_buffer(name, units):
+            laid = laid_buffer(name)[:].rearrange("p c n -> p (c n)")
+            rows = sum(unit[2] for unit in units)
+            codes, scales = codes_tiles("enc", P * rows, 4) if rows > 2 else codes_tiles("pair", PAIR, 6)
+            n0 = 0
+            for g, row0, count in units:
+                for r in range(row0, row0 + count):
+                    enc_laid[g, r] = (laid, n0)
+                    enc_quantised[g, r] = (codes, scales, n0)
+                    n0 = n0 + P
 
-        def join(unit, a=0, b=None, engine_copy=nc.vector.tensor_copy):
-            b = b or unit[3]
+        def laid_tokens(unit, a, b):
+            laid, n0 = enc_laid[unit[0], unit[1] + a // P]
+            n0 = n0 + a % P
+            return laid[:, 4 * n0 : 4 * (n0 + b - a)]
+
+        def lay(engine_copy, unit, a, b):
             engine_copy(
-                out=laid_tile(unit)[:, P * a : P * b, :, :],
-                in_=planes[unit][:, :, P * a : P * b, :].rearrange("p u n e -> p n u e"),
+                out=laid_tokens(unit, a, b).rearrange("p (m i t) -> p m t i", i=2, t=4),
+                in_=by_slot(unit)[:, :, a:b].rearrange("p t (m i) -> p m t i", i=2),
             )
 
-        def four_planes(unit):
-            return planes[unit][:].rearrange("p u n e -> p (u n e)").rearrange("p (t n) -> p t n", t=4)
-
-        def laid_tokens(unit, a, b, into):
-            n0 = P * (into[2] - unit[2])
-            return laid_tile(into)[:, a - n0 : b - n0, :, :]
-
-        def lay(engine_copy, unit, a, b, into=None):
-            engine_copy(
-                out=laid_tokens(unit, a, b, into or unit).rearrange("p (m i) u e -> p m (u e) i", i=2),
-                in_=four_planes(unit)[:, :, a:b].rearrange("p t (m i) -> p m t i", i=2),
-            )
-
-        def lay_gpsimd(unit, a, b, into=None):
+        def lay_gpsimd(unit, a, b):
             nc.gpsimd.tensor_scalar(
-                out=laid_tokens(unit, a, b, into or unit).rearrange("p n u e -> p n (u e)"),
-                in0=four_planes(unit)[:, :, a:b].rearrange("p t n -> p n t"),
+                out=laid_tokens(unit, a, b).rearrange("p (n t) -> p n t", t=4),
+                in0=by_slot(unit)[:, :, a:b].rearrange("p t n -> p n t"),
                 scalar1=1.0, scalar2=0.0, op0=MULT, op1=ADD,
+            )
+
+        def join(engine_copy, unit, a, b):
+            engine_copy(
+                out=laid_tokens(unit, a, b).rearrange("p (n u e) -> p n u e", u=2, e=2),
+                in_=by_plane(unit)[:, :, a:b, :].rearrange("p u n e -> p n u e"),
             )
 
         def join_relu(unit):
             nc.vector.tensor_scalar(
-                out=laid_tile(unit)[:], in0=planes[unit][:].rearrange("p u n e -> p n u e"),
+                out=laid_tokens(unit, 0, P * unit[2]).rearrange("p (n u e) -> p n u e", u=2, e=2),
+                in0=by_plane(unit).rearrange("p u n e -> p n u e"),
                 scalar1=0.0, scalar2=None, op0=MAX,
             )
 
-        def enc_quant(unit, a=0, b=None):
-            b = b or unit[3]
-            if unit not in enc_codes:
-                enc_codes[unit] = work.tile([P, P * unit[3]], U32, name="x_wide", bufs=9, align_bytes=64)
-                enc_scales[unit] = work.tile([P, P * unit[3]], U8, name="enc_scales", bufs=9, align_bytes=64)
-            nc.vector.quantize_mx(
-                out=enc_codes[unit][:, P * a : P * b].bitcast(FP8X4),
-                scales=enc_scales[unit][:, P * a : P * b],
-                in_=enc_laid[unit][:, P * a : P * b, :, :].rearrange("p n u e -> p (n u e)"),
-            )
+        def enc_quant(g, row0, rows):
+            laid, n0 = enc_laid[g, row0]
+            codes, scales = enc_quantised[g, row0][:2]
+            n1 = n0 + P * rows
+            quantize(codes[:, n0:n1], scales[:, n0:n1], laid[:, 4 * n0 : 4 * n1])
 
         acc = {}
 
-        def second_stage(unit, a=0, b=None):
-            h, g, row0, rows = unit
-            for r in range(a, b or rows):
-                i = 2 * h + (row0 + r) // 2
-                if i not in acc:
-                    acc[i] = sums.tile([P, 2, 2 * LATENT], F32, name=f"sum{i}")
+        def second_stage(g, row0, rows):
+            w_cols = slice(2 * LATENT * g, 2 * LATENT * (g + 1))
+            for r in range(row0, row0 + rows):
+                if r // 2 not in acc:
+                    acc[r // 2] = sums.tile([P, 2, 2 * LATENT], F32, name=f"sum{r // 2}")
+                codes, scales, n0 = enc_quantised[g, r]
                 nc.tensor.matmul_mx(
-                    out=acc[i][:, r % 2, :],
-                    lhsT=enc_codes[unit][:, P * r : P * (r + 1)].bitcast(FP8X4),
-                    lhsT_scale=enc_scales[unit][:, P * r : P * (r + 1)],
-                    rhs=w3_codes[:, g, :].bitcast(FP8X4),
-                    rhs_scale=w3_scales[:, g, :],
+                    out=acc[r // 2][:, r % 2, :],
+                    lhsT=codes[:, n0 : n0 + P].bitcast(FP8X4),
+                    lhsT_scale=scales[:, n0 : n0 + P],
+                    rhs=w3_codes[:, w_cols].bitcast(FP8X4),
+                    rhs_scale=w3_scales[:, w_cols],
                     start=(g == 0 and r % 2 == 0),
                     stop=(g == GROUPS - 1 and r % 2 == 1),
                 )
 
-        late = {}
-        both = keep.tile([P, 2, ROWS, LATENT], F32, name="mu_sigma")
-        z = keep.tile([P, ROWS, LATENT], F32, name="z")
         out_views = [o.rearrange("(p r) l -> p r l", r=ROWS) for o in (out_0, out_1, out_2)]
+        late = {}
 
         def add_bias(a, b):
             nc.vector.tensor_tensor(
@@ -439,25 +430,28 @@ def tile_mae_pa_kernel(tc, x_bytes, x_scale, eps, W11, b11, W31, b31, W32, b32, 
 
         def relus(a, b):
             nc.scalar.activation(
-                out=both[:, :, a:b, :], in_=late["biased"][:, a:b, :].rearrange("p r (w l) -> p w r l", w=2), func=RELU
+                out=late["mu_sigma"][:, :, a:b, :],
+                in_=late["biased"][:, a:b, :].rearrange("p r (w l) -> p w r l", w=2), func=RELU,
             )
 
         def store_mu_sigma(a, b, queue=nc.sync):
             for w in range(2):
-                queue.dma_start(out=out_views[w][:, a:b, :], in_=both[:, w, a:b, :])
+                queue.dma_start(out=out_views[w][:, a:b, :], in_=late["mu_sigma"][:, w, a:b, :])
 
         def z_noise(a, b):
             nc.vector.scalar_tensor_tensor(
-                out=z[:, a:b, :], in0=late["biased"][:, a:b, LATENT:], scalar=0.0, in1=eps_sb[:, a:b, :], op0=MAX, op1=MULT
+                out=late["z"][:, a:b, :], in0=late["biased"][:, a:b, LATENT:], scalar=0.0,
+                in1=eps_sb[:, a:b, :], op0=MAX, op1=MULT,
             )
 
         def z_add_mu(a, b):
             nc.vector.scalar_tensor_tensor(
-                out=z[:, a:b, :], in0=late["biased"][:, a:b, :LATENT], scalar=0.0, in1=z[:, a:b, :], op0=MAX, op1=ADD
+                out=late["z"][:, a:b, :], in0=late["biased"][:, a:b, :LATENT], scalar=0.0,
+                in1=late["z"][:, a:b, :], op0=MAX, op1=ADD,
             )
 
         def store_z(a, b):
-            nc.sync.dma_start(out=out_views[2][:, a:b, :], in_=z[:, a:b, :])
+            nc.sync.dma_start(out=out_views[2][:, a:b, :], in_=late["z"][:, a:b, :])
 
         unused_bank = sums.tile([P, HALF], F32, name="sum0")
         warm_up(unused_bank, 256)
@@ -471,17 +465,19 @@ def tile_mae_pa_kernel(tc, x_bytes, x_scale, eps, W11, b11, W31, b31, W32, b32, 
             x_widen(r)
             x_turn(r)
             x_product(r)
+        w_buffer("laid2", [(0, 0), (0, 1)])
+        w_buffer("laid3", [(1, 0)])
         w_gpsimd(0, 0, 0, PASS)
-        w_gpsimd(0, 1, 0, HEAD_CHANNELS)
+        w_gpsimd(0, 1, 0, P)
         x_widen(4)
         x_turn(4)
         x_widen(5)
-        w_matmuls(0, 1, BANK_CHANNELS)
-        w_scalar(0, 1, HEAD_CHANNELS, BANK_CHANNELS)
+        w_matmuls(0, 1, BANK_CHANNELS, BANK_CHANNELS)
+        w_scalar(0, 1, P, BANK_CHANNELS)
         x_turn(5)
         x_widen(6)
         x_widen(7)
-        w_empty(0, 1, BANK_CHANNELS)
+        w_empty(0, 1, BANK_CHANNELS, BANK_CHANNELS)
         x_turn(6)
         w_matmuls(1, 0, 0, P)
         w_scalar(1, 0, P, PASS)
@@ -490,54 +486,54 @@ def tile_mae_pa_kernel(tc, x_bytes, x_scale, eps, W11, b11, W31, b31, W32, b32, 
         x_quant(0)
         w_quant(0, 1)
 
-        w_laid[1, 1] = keep.tile([P, 4 * PASS], BF16, name="x_laid0", align_bytes=64)[:]
+        w_buffer("laid0", [(1, 1), (2, 0)])
         w_gpsimd(1, 1, 0, PASS)
-        for w in range(2):
-            w3_gpsimd(0, w)
-        scalar_unit((0, 0, 0, 4))
+        w3_gpsimd(0)
+        w3_gpsimd(1)
+        for t in range(4):
+            scalar_bank((0, 0, 4), t)
         x_turn(7)
-        for r in range(4, ROWS):
+        for r in (6, 4, 5, 7):
             x_product(r)
-        w_matmuls(2, 0, BANK_CHANNELS)
+        w_matmuls(2, 0, BANK_CHANNELS, BANK_CHANNELS)
         w_scalar(2, 0, 0, BANK_CHANNELS)
-        w_empty(2, 0, BANK_CHANNELS)
-        w3_matmuls(1, 0, 2)
-        w3_empty(1, 0, 2)
-        w3_matmuls(2, 0, 2)
+        w_empty(2, 0, BANK_CHANNELS, BANK_CHANNELS)
+        w3_matmuls(2, 2)
+        w3_empty(2, 2)
+        w3_matmuls(4, 2)
+        w_buffer("laid2", [(2, 1), (3, 0)])
         w_scalar(3, 0, 0, BANK_CHANNELS)
-        w3_empty(2, 0, 2)
+        w3_empty(4, 2)
         w_quant(1, 0)
         x_quant(1)
         lay_bias(0, 4)
-        w_quant(1, 1)
-        w_quant(2, 0)
+        w_quant(1, 1, 2)
         for i in range(4):
-            vector_bank((1, 0, 0, 4), i)
+            vector_banks((0, 4, 4), [i])
 
-        g5, g6, g7 = GROUPS - 3, GROUPS - 2, GROUPS - 1
         for j in range(PERIODS):
-            v_unit, s_unit, before = (1, j, 0, 4), (0, j + 1, 0, 4), (0, j, 0, 4)
             last = j == PERIODS - 1
-            share = SCALAR_CHANNELS
+            v_unit, s_unit, before = (j, 4, 4), (j + 1, 0, 4), (j, 0, 4)
+            if j > 0:
+                w_buffer(f"laid{2 + j % 2}", [(j + 2, 1)] if last else [(j + 2, 1), (j + 3, 0)])
             if last:
-                w_scalar(j + 2, 1, 0, share)
-                for m in range(12, 16):
-                    w3_copy(nc.scalar.copy, m // 2, m % 2)
+                w_scalar(j + 2, 1, 0, SCALAR_CHANNELS)
+                for m in range(2 * PERIODS, 2 * GROUPS):
+                    w3_scalar(m)
             else:
                 w_scalar(j + 3, 0, BANK_CHANNELS if j == 0 else 0, PASS)
-                w_scalar(j + 2, 1, 0, share)
-            if j == 0:
-                enc_laid[before] = keep.tile([P, HALF, 2, 2], BF16, name="x_laid0", align_bytes=64)
+                w_scalar(j + 2, 1, 0, SCALAR_CHANNELS)
+            enc_buffer("laid1", [before, v_unit])
             lay_gpsimd(before, 0, GPSIMD_TOKENS)
             for i in range(4):
                 vector_add(v_unit, i)
-            m = 6 + j
-            w3_matmuls(m // 2, m % 2, m % 2 + 1)
-            w3_empty(m // 2, m % 2, m % 2 + 1)
-            scalar_unit(s_unit)
-            if 0 < j < PERIODS - 1:
-                second_stage((1, j - 1, 0, 4))
-            w_vector(j + 2, 1, share, PASS)
+            w3_matmuls(PERIODS + j, 1)
+            w3_empty(PERIODS + j, 1)
+            for t in range(4):
+                scalar_bank(s_unit, t)
+            if 0 < j and not last:
+                second_stage(j - 1, 4, 4)
+            w_vector(j + 2, 1, SCALAR_CHANNELS, PASS)
             join_relu(v_unit)
             if j == 2:
                 lay_bias(4, GROUPS)
@@ -545,96 +541,89 @@ def tile_mae_pa_kernel(tc, x_bytes, x_scale, eps, W11, b11, W31, b31, W32, b32, 
             if last:
                 w_quant(j + 2, 1)
             w3_quant(j)
-            if last:
-                enc_quant(before)
-            else:
-                enc_quant(before)
-                w_quant(j + 2, 1)
+            enc_quant(j, 0, ROWS)
             if not last:
-                vector_banks((1, j + 1, 0, 4))
-                second_stage(before)
-                enc_quant(v_unit)
-                w_quant(j + 3, 0)
+                vector_banks((j + 1, 4, 4), [0, 1])
+                vector_banks((j + 1, 4, 4), [2, 3])
+                second_stage(j, 0, 4)
+                w_quant(j + 2, 1, 2)
 
-        s6, s7 = (0, g6, 0, 4), (0, g7, 0, 4)
-        v6 = [(1, g6, 0, 2), (1, g6, 2, 2)]
-        s7b = [(1, g7, 0, 2), (1, g7, 2, 2)]
-        s6_rows = [(0, g6, 0, 2), (0, g6, 2, 2)]
-        late["biased"] = keep.tile([P, ROWS, 2 * LATENT], F32, name="x_laid1", align_bytes=64)
-        enc_quant((1, g5, 0, 4))
+        g4, g5, g6, g7 = range(GROUPS - 4, GROUPS)
+        s6, s7 = (g6, 0, 4), (g7, 0, 4)
+        v6 = [(g6, 4, 2), (g6, 6, 2)]
+        s7b = [(g7, 4, 2), (g7, 6, 2)]
+        late["biased"] = keep.tile([P, ROWS, 2 * LATENT], F32, name="laid0", align_bytes=64)
+        late["mu_sigma"] = keep.tile([P, 2, ROWS, LATENT], F32, name="w11_raw0_5")
+        late["z"] = keep.tile([P, ROWS, LATENT], F32, name="w11_raw0_0")
         w3_quant(g6)
-        vector_bank(v6[0], 0)
-        scalar_bank(s7, 0)
-        vector_bank(v6[0], 1)
-        scalar_bank(s7, 2)
-        second_stage((0, g5, 0, 4))
-        laid_tile(s6_rows[0], 0)
-        lay_gpsimd(s6, 0, TAIL_TOKENS, s6_rows[0])
+        vector_banks(v6[0], [0])
+        scalar_bank(s7, 0, planes=True)
+        vector_banks(v6[0], [1])
+        scalar_bank(s7, 2, planes=True)
+        second_stage(g5, 0, 4)
+        enc_buffer("laid1", [(g6, 0, 2)])
+        lay_gpsimd(s6, 0, GPSIMD_TAIL_TOKENS)
         vector_add(v6[0], 0)
         vector_add(v6[0], 1)
-        scalar_bank(s7, 1)
-        vector_bank(v6[1], 0)
-        scalar_bank(s7, 3)
-        vector_bank(v6[1], 1)
-        laid_tile(v6[0], 1)
+        scalar_bank(s7, 1, planes=True)
+        vector_banks(v6[1], [0])
+        scalar_bank(s7, 3, planes=True)
+        vector_banks(v6[1], [1])
+        enc_buffer("laid2", [v6[0]])
         w3_quant(g7)
         join_relu(v6[0])
-        lay(nc.vector.tensor_copy, s6, TAIL_TOKENS, PAIR, s6_rows[0])
-        enc_quant(v6[0])
-        enc_quant(s6_rows[0])
-        laid_tile(s6_rows[1], 1)
-        lay_gpsimd(s6, PAIR, PAIR + TAIL_TOKENS, s6_rows[1])
+        lay(nc.vector.tensor_copy, s6, GPSIMD_TAIL_TOKENS, PAIR)
+        enc_quant(g6, 4, 2)
+        enc_quant(g6, 0, 2)
+        enc_buffer("laid2", [(g6, 2, 2)])
+        lay_gpsimd(s6, PAIR, PAIR + GPSIMD_TAIL_TOKENS)
         vector_add(v6[1], 0)
         vector_add(v6[1], 1)
-        scalar_pair_bank(s7b[0], 0)
-        second_stage(s6_rows[0])
-        scalar_pair_bank(s7b[0], 1)
-        laid_tile(s7, 0)
-        laid_tile(v6[1], 2)
-        join(s7, 0, 2)
-        lay(nc.vector.tensor_copy, s6, PAIR + TAIL_TOKENS, HALF, s6_rows[1])
-        enc_quant(s7, 0, 2)
-        join(s7, 2, 4)
-        enc_quant(s6_rows[1])
+        scalar_pair_bank(s7b[0], 0, planes=True)
+        second_stage(g6, 0, 2)
+        scalar_pair_bank(s7b[0], 1, planes=True)
+        enc_buffer("laid1", [s7])
+        enc_buffer("laid3", [v6[1]])
+        join(nc.vector.tensor_copy, s7, 0, PAIR)
+        lay(nc.vector.tensor_copy, s6, PAIR + GPSIMD_TAIL_TOKENS, HALF)
+        enc_quant(g7, 0, 2)
+        join(nc.vector.tensor_copy, s7, PAIR, HALF)
+        enc_quant(g6, 2, 2)
         join_relu(v6[1])
-        enc_quant(s7, 2, 4)
+        enc_quant(g7, 2, 2)
         scalar_pair_bank(s7b[1], 0)
-        second_stage(s7, 0, 2)
+        second_stage(g7, 0, 2)
         scalar_pair_bank(s7b[1], 1)
-        second_stage(s6_rows[1])
-        second_stage(s7, 2, 4)
-        laid_tile(s7b[0], 1)
-        laid_tile(s7b[1], 0)
-        join(s7b[0])
-        enc_quant(v6[1])
-        enc_quant(s7b[0])
-        for g in (g5 - 1, g5):
-            second_stage((1, g, 0, 4), 0, 2)
-        second_stage(v6[0])
-        second_stage(s7b[0])
-        for g in (g5 - 1, g5):
-            second_stage((1, g, 0, 4), 2, 4)
-        second_stage(v6[1])
+        second_stage(g6, 2, 2)
+        second_stage(g7, 2, 2)
+        enc_buffer("laid2", [s7b[0]])
+        join(nc.vector.tensor_copy, s7b[0], 0, PAIR)
+        enc_quant(g6, 6, 2)
+        enc_quant(g7, 4, 2)
+        for row0 in (4, 6):
+            for g in range(g4, GROUPS if row0 == 4 else g7):
+                second_stage(g, row0, 2)
+        enc_buffer("laid3", [s7b[1]])
         lay_gpsimd(s7b[1], P, PAIR)
         lay(nc.scalar.copy, s7b[1], 0, P)
         for a in (0, 2, 4):
             add_bias(a, a + 2)
             relus(a, a + 2)
             store_mu_sigma(a, a + 2)
-        enc_quant(s7b[1], 0, 1)
-        enc_quant(s7b[1], 1, 2)
-        second_stage(s7b[1])
+        enc_quant(g7, 6, 1)
+        enc_quant(g7, 7, 1)
+        second_stage(g7, 6, 2)
         z_noise(0, 4)
         z_noise(4, 6)
         add_bias(6, 7)
-        add_bias(7, 8)
         z_add_mu(0, 4)
         store_z(0, 4)
+        add_bias(7, 8)
         relus(6, 7)
         relus(7, 8)
         store_mu_sigma(6, 8, nc.scalar)
-        z_noise(6, 8)
         z_add_mu(4, 6)
         store_z(4, 6)
+        z_noise(6, 8)
         z_add_mu(6, 8)
         store_z(6, 8)

@@ -31,7 +31,7 @@ PERIODS = GROUPS - 2
 
 GPSIMD_TOKENS = 448
 GPSIMD_TAIL_TOKENS = 192
-SCALAR_CHANNELS = 288
+SCALAR_CHANNELS = 304
 BIAS_RUN = 16
 MATMUL_ROWS = range(0, ROWS, 2)
 
@@ -281,21 +281,24 @@ def tile_mae_pa_kernel(tc, x_bytes, x_scale, eps, W11, b11, W31, b31, W32, b32, 
 
         emptied, enc_laid, enc_quantised = {}, {}, {}
 
-        def passes(out, g, t, row0, rows):
+        def one_pass(out, g, c, t, row0, rows):
             h, row = divmod(row0, 4)
+            w_codes, w_scales, i = w_quantised[g, c]
+            w_cols = slice(PASS * i + P * t, PASS * i + P * (t + 1))
+            x_cols = slice(HALF * c + P * row, HALF * c + P * (row + rows))
+            nc.tensor.matmul_mx(
+                out=out,
+                lhsT=w_codes[:, w_cols].bitcast(FP8X4),
+                lhsT_scale=w_scales[:, w_cols],
+                rhs=x_quantised[h][0][:, x_cols].bitcast(FP8X4),
+                rhs_scale=x_quantised[h][1][:, x_cols],
+                start=(c == 0),
+                stop=(c == 1),
+            )
+
+        def passes(out, g, t, row0, rows):
             for c in range(2):
-                w_codes, w_scales, i = w_quantised[g, c]
-                w_cols = slice(PASS * i + P * t, PASS * i + P * (t + 1))
-                x_cols = slice(HALF * c + P * row, HALF * c + P * (row + rows))
-                nc.tensor.matmul_mx(
-                    out=out,
-                    lhsT=w_codes[:, w_cols].bitcast(FP8X4),
-                    lhsT_scale=w_scales[:, w_cols],
-                    rhs=x_quantised[h][0][:, x_cols].bitcast(FP8X4),
-                    rhs_scale=x_quantised[h][1][:, x_cols],
-                    start=(c == 0),
-                    stop=(c == 1),
-                )
+                one_pass(out, g, c, t, row0, rows)
 
         def emptied_tile(unit):
             if unit not in emptied:
@@ -331,9 +334,10 @@ def tile_mae_pa_kernel(tc, x_bytes, x_scale, eps, W11, b11, W31, b31, W32, b32, 
         def vector_banks(unit, numbers):
             for i in numbers:
                 banks[unit, i] = psum.tile([P, 2, PAIR], F32, name="bank")
-            for i in reversed(numbers):
-                for e in range(2):
-                    passes(banks[unit, i][:, e, :], unit[0], 2 * (i % 2) + e, unit[1] + 2 * (i // 2), 2)
+            for e in range(2):
+                for c in range(2):
+                    for i in reversed(numbers):
+                        one_pass(banks[unit, i][:, e, :], unit[0], c, 2 * (i % 2) + e, unit[1] + 2 * (i // 2), 2)
 
         bias_runs = keep.tile([P, 2 * GROUPS, BIAS_RUN, 2], BF16, name="bias_runs")
 
@@ -499,16 +503,17 @@ def tile_mae_pa_kernel(tc, x_bytes, x_scale, eps, W11, b11, W31, b31, W32, b32, 
         w_scalar(2, 0, 0, BANK_CHANNELS)
         w_empty(2, 0, BANK_CHANNELS, BANK_CHANNELS)
         w3_matmuls(2, 2)
+        w3_scalar(5)
         w3_empty(2, 2)
-        w3_matmuls(4, 2)
+        w3_matmuls(4, 1)
         w_buffer("laid2", [(2, 1), (3, 0)])
         w_scalar(3, 0, 0, BANK_CHANNELS)
-        w3_empty(4, 2)
+        w3_empty(4, 1)
         w_quant(1, 0)
         x_quant(1)
         lay_bias(0, 4)
         w_quant(1, 1, 2)
-        for i in range(4):
+        for i in (0, 2, 1, 3):
             vector_banks((0, 4, 4), [i])
 
         for j in range(PERIODS):
@@ -525,7 +530,7 @@ def tile_mae_pa_kernel(tc, x_bytes, x_scale, eps, W11, b11, W31, b31, W32, b32, 
                 w_scalar(j + 2, 1, 0, SCALAR_CHANNELS)
             enc_buffer("laid1", [before, v_unit])
             lay_gpsimd(before, 0, GPSIMD_TOKENS)
-            for i in range(4):
+            for i in (0, 2, 1, 3):
                 vector_add(v_unit, i)
             w3_matmuls(PERIODS + j, 1)
             w3_empty(PERIODS + j, 1)
@@ -543,8 +548,8 @@ def tile_mae_pa_kernel(tc, x_bytes, x_scale, eps, W11, b11, W31, b31, W32, b32, 
             w3_quant(j)
             enc_quant(j, 0, ROWS)
             if not last:
-                vector_banks((j + 1, 4, 4), [0, 1])
-                vector_banks((j + 1, 4, 4), [2, 3])
+                vector_banks((j + 1, 4, 4), [0, 2])
+                vector_banks((j + 1, 4, 4), [1, 3])
                 second_stage(j, 0, 4)
                 w_quant(j + 2, 1, 2)
 

@@ -83,9 +83,21 @@ def tile_mae_pa_kernel(tc, x_bytes, x_scale, eps, W11, b11, W31, b31, W32, b32, 
 
         scale_cols = keep.tile([P, 2, 4], F32, name="scale_cols")
         scale = keep.tile([P, 2, P, 4], F32, name="scale")
-        bias1 = keep.tile([P, GROUPS, 4], BF16, name="bias1")
+        bias1 = {}
+
+        def load_bias1(queue, g0, g1):
+            tile = keep.tile([P, g1 - g0, 4], BF16, name=f"bias1_{g0}")
+            queue.dma_start(out=tile[:], in_=b11_view[:, g0:g1, :])
+            for g in range(g0, g1):
+                bias1[g] = (tile, g0)
+
+        def bias1_view(g0, g1):
+            tile, first = bias1[g0]
+            return tile[:, g0 - first : g1 - first, :]
+
         load_x(0, 1)
-        nc.sync.dma_start(out=scale_cols[:], in_=x_scale.rearrange("o (c p t) -> p (o c) t", p=P, t=4))
+        nc.scalar.dma_start(out=scale_cols[:], in_=x_scale.rearrange("o (c p t) -> p (o c) t", p=P, t=4))
+        load_bias1(nc.scalar, 0, 1)
         load_x(1, 2)
         load_x(2, 4)
         load_w11(0, 0, 1)
@@ -94,16 +106,16 @@ def tile_mae_pa_kernel(tc, x_bytes, x_scale, eps, W11, b11, W31, b31, W32, b32, 
         load_x(6, ROWS)
         load_w11(0, 1, 2)
         load_w11(1, 1, 2)
-        nc.sync.dma_start(out=bias1[:, :4, :], in_=b11_view[:, :4, :])
         load_w3(0, 1)
         load_w11(0, 2, 3)
         load_w3(1, 3)
         load_w11(0, 3, 4)
         load_w11(1, 2, 3)
+        load_bias1(nc.sync, 1, 3)
         load_w3(3, 5)
         load_w11(0, 4, 5)
         load_w11(1, 3, 4)
-        nc.sync.dma_start(out=bias1[:, 4:, :], in_=b11_view[:, 4:, :])
+        load_bias1(nc.sync, 3, GROUPS)
         load_w11(0, 5, 7)
         load_w11(1, 4, 6)
         load_w3(5, GROUPS)
@@ -316,7 +328,7 @@ def tile_mae_pa_kernel(tc, x_bytes, x_scale, eps, W11, b11, W31, b31, W32, b32, 
         def scalar_empty(unit, t, sums_of_t, planes):
             nc.scalar.activation(
                 out=by_plane(unit)[:, t // 2, :, t % 2] if planes else by_slot(unit)[:, t, :],
-                in_=sums_of_t, func=RELU, bias=bias1[:, unit[0], t : t + 1],
+                in_=sums_of_t, func=RELU, bias=bias1_view(unit[0], unit[0] + 1)[:, 0, t : t + 1],
             )
 
         def scalar_bank(unit, t, planes=False):
@@ -344,7 +356,7 @@ def tile_mae_pa_kernel(tc, x_bytes, x_scale, eps, W11, b11, W31, b31, W32, b32, 
         def lay_bias(g0, g1):
             nc.vector.tensor_copy(
                 out=bias_runs[:, 2 * g0 : 2 * g1, :, :],
-                in_=bias1[:, g0:g1, :].rearrange("p g (u e) -> p (g u) e", e=2).unsqueeze(2)
+                in_=bias1_view(g0, g1).rearrange("p g (u e) -> p (g u) e", e=2).unsqueeze(2)
                 .to_broadcast([P, 2 * (g1 - g0), BIAS_RUN, 2]),
             )
 
@@ -497,7 +509,7 @@ def tile_mae_pa_kernel(tc, x_bytes, x_scale, eps, W11, b11, W31, b31, W32, b32, 
         for t in range(4):
             scalar_bank((0, 0, 4), t)
         x_turn(7)
-        for r in (6, 4, 5, 7):
+        for r in (5, 4, 6, 7):
             x_product(r)
         w_matmuls(2, 0, BANK_CHANNELS, BANK_CHANNELS)
         w_scalar(2, 0, 0, BANK_CHANNELS)
@@ -511,7 +523,7 @@ def tile_mae_pa_kernel(tc, x_bytes, x_scale, eps, W11, b11, W31, b31, W32, b32, 
         w3_empty(4, 1)
         w_quant(1, 0)
         x_quant(1)
-        lay_bias(0, 4)
+        lay_bias(0, 1)
         w_quant(1, 1, 2)
         for i in (0, 2, 1, 3):
             vector_banks((0, 4, 4), [i])
@@ -540,8 +552,8 @@ def tile_mae_pa_kernel(tc, x_bytes, x_scale, eps, W11, b11, W31, b31, W32, b32, 
                 second_stage(j - 1, 4, 4)
             w_vector(j + 2, 1, SCALAR_CHANNELS, PASS)
             join_relu(v_unit)
-            if j == 2:
-                lay_bias(4, GROUPS)
+            if j in (0, 2):
+                lay_bias(*((1, 3) if j == 0 else (3, GROUPS - 1)))
             lay(nc.vector.tensor_copy, before, GPSIMD_TOKENS, HALF)
             if last:
                 w_quant(j + 2, 1)
@@ -575,9 +587,9 @@ def tile_mae_pa_kernel(tc, x_bytes, x_scale, eps, W11, b11, W31, b31, W32, b32, 
         scalar_bank(s7, 3, planes=True)
         vector_banks(v6[1], [1])
         enc_buffer("laid2", [v6[0]])
-        w3_quant(g7)
-        join_relu(v6[0])
         lay(nc.vector.tensor_copy, s6, GPSIMD_TAIL_TOKENS, PAIR)
+        join_relu(v6[0])
+        w3_quant(g7)
         enc_quant(g6, 4, 2)
         enc_quant(g6, 0, 2)
         enc_buffer("laid2", [(g6, 2, 2)])
@@ -589,16 +601,16 @@ def tile_mae_pa_kernel(tc, x_bytes, x_scale, eps, W11, b11, W31, b31, W32, b32, 
         scalar_pair_bank(s7b[0], 1, planes=True)
         enc_buffer("laid1", [s7])
         enc_buffer("laid3", [v6[1]])
-        join(nc.vector.tensor_copy, s7, 0, PAIR)
         lay(nc.vector.tensor_copy, s6, PAIR + GPSIMD_TAIL_TOKENS, HALF)
+        join(nc.vector.tensor_copy, s7, 0, PAIR)
+        enc_quant(g6, 2, 2)
         enc_quant(g7, 0, 2)
         join(nc.vector.tensor_copy, s7, PAIR, HALF)
-        enc_quant(g6, 2, 2)
         join_relu(v6[1])
         enc_quant(g7, 2, 2)
         scalar_pair_bank(s7b[1], 0)
-        second_stage(g7, 0, 2)
         scalar_pair_bank(s7b[1], 1)
+        second_stage(g7, 0, 2)
         second_stage(g6, 2, 2)
         second_stage(g7, 2, 2)
         enc_buffer("laid2", [s7b[0]])

@@ -83,21 +83,9 @@ def tile_mae_pa_kernel(tc, x_bytes, x_scale, eps, W11, b11, W31, b31, W32, b32, 
 
         scale_cols = keep.tile([P, 2, 4], F32, name="scale_cols")
         scale = keep.tile([P, 2, P, 4], F32, name="scale")
-        bias1 = {}
-
-        def load_bias1(queue, g0, g1):
-            tile = keep.tile([P, g1 - g0, 4], BF16, name=f"bias1_{g0}")
-            queue.dma_start(out=tile[:], in_=b11_view[:, g0:g1, :])
-            for g in range(g0, g1):
-                bias1[g] = (tile, g0)
-
-        def bias1_view(g0, g1):
-            tile, first = bias1[g0]
-            return tile[:, g0 - first : g1 - first, :]
-
+        bias1 = keep.tile([P, GROUPS, 4], BF16, name="bias1")
         load_x(0, 1)
-        nc.scalar.dma_start(out=scale_cols[:], in_=x_scale.rearrange("o (c p t) -> p (o c) t", p=P, t=4))
-        load_bias1(nc.scalar, 0, 1)
+        nc.sync.dma_start(out=scale_cols[:], in_=x_scale.rearrange("o (c p t) -> p (o c) t", p=P, t=4))
         load_x(1, 2)
         load_x(2, 4)
         load_w11(0, 0, 1)
@@ -106,16 +94,16 @@ def tile_mae_pa_kernel(tc, x_bytes, x_scale, eps, W11, b11, W31, b31, W32, b32, 
         load_x(6, ROWS)
         load_w11(0, 1, 2)
         load_w11(1, 1, 2)
+        nc.sync.dma_start(out=bias1[:, :4, :], in_=b11_view[:, :4, :])
         load_w3(0, 1)
         load_w11(0, 2, 3)
         load_w3(1, 3)
         load_w11(0, 3, 4)
         load_w11(1, 2, 3)
-        load_bias1(nc.sync, 1, 3)
         load_w3(3, 5)
         load_w11(0, 4, 5)
         load_w11(1, 3, 4)
-        load_bias1(nc.sync, 3, GROUPS)
+        nc.sync.dma_start(out=bias1[:, 4:, :], in_=b11_view[:, 4:, :])
         load_w11(0, 5, 7)
         load_w11(1, 4, 6)
         load_w3(5, GROUPS)
@@ -328,7 +316,7 @@ def tile_mae_pa_kernel(tc, x_bytes, x_scale, eps, W11, b11, W31, b31, W32, b32, 
         def scalar_empty(unit, t, sums_of_t, planes):
             nc.scalar.activation(
                 out=by_plane(unit)[:, t // 2, :, t % 2] if planes else by_slot(unit)[:, t, :],
-                in_=sums_of_t, func=RELU, bias=bias1_view(unit[0], unit[0] + 1)[:, 0, t : t + 1],
+                in_=sums_of_t, func=RELU, bias=bias1[:, unit[0], t : t + 1],
             )
 
         def scalar_bank(unit, t, planes=False):
@@ -351,12 +339,12 @@ def tile_mae_pa_kernel(tc, x_bytes, x_scale, eps, W11, b11, W31, b31, W32, b32, 
                     for i in reversed(numbers):
                         one_pass(banks[unit, i][:, e, :], unit[0], c, 2 * (i % 2) + e, unit[1] + 2 * (i // 2), 2)
 
-        bias_runs = keep.tile([P, 2 * GROUPS, BIAS_RUN, 2], BF16, name="bias_runs")
+        bias_runs = keep.tile([P, 2 * (GROUPS - 1), BIAS_RUN, 2], BF16, name="bias_runs")
 
         def lay_bias(g0, g1):
             nc.vector.tensor_copy(
                 out=bias_runs[:, 2 * g0 : 2 * g1, :, :],
-                in_=bias1_view(g0, g1).rearrange("p g (u e) -> p (g u) e", e=2).unsqueeze(2)
+                in_=bias1[:, g0:g1, :].rearrange("p g (u e) -> p (g u) e", e=2).unsqueeze(2)
                 .to_broadcast([P, 2 * (g1 - g0), BIAS_RUN, 2]),
             )
 
@@ -523,7 +511,7 @@ def tile_mae_pa_kernel(tc, x_bytes, x_scale, eps, W11, b11, W31, b31, W32, b32, 
         w3_empty(4, 1)
         w_quant(1, 0)
         x_quant(1)
-        lay_bias(0, 1)
+        lay_bias(0, 4)
         w_quant(1, 1, 2)
         for i in (0, 2, 1, 3):
             vector_banks((0, 4, 4), [i])
@@ -552,8 +540,8 @@ def tile_mae_pa_kernel(tc, x_bytes, x_scale, eps, W11, b11, W31, b31, W32, b32, 
                 second_stage(j - 1, 4, 4)
             w_vector(j + 2, 1, SCALAR_CHANNELS, PASS)
             join_relu(v_unit)
-            if j in (0, 2):
-                lay_bias(*((1, 3) if j == 0 else (3, GROUPS - 1)))
+            if j == 2:
+                lay_bias(4, GROUPS - 1)
             lay(nc.vector.tensor_copy, before, GPSIMD_TOKENS, HALF)
             if last:
                 w_quant(j + 2, 1)

@@ -34,6 +34,7 @@ GPSIMD_TAIL_TOKENS = 192
 SCALAR_CHANNELS = 304
 BIAS_RUN = 16
 MATMUL_ROWS = range(0, ROWS, 2)
+GPSIMD_LATE_TOKENS = 400
 
 
 def tile_mae_pa_kernel(tc, x_bytes, x_scale, eps, W11, b11, W31, b31, W32, b32, out_0, out_1, out_2):
@@ -303,7 +304,7 @@ def tile_mae_pa_kernel(tc, x_bytes, x_scale, eps, W11, b11, W31, b31, W32, b32, 
         def emptied_tile(unit):
             if unit not in emptied:
                 g, row0, rows = unit
-                tag, bufs = (f"emptied{row0}", 2 - row0 // 4) if rows == 4 else ("emptied_pair", 3)
+                tag, bufs = ("emptied", 4) if rows == 4 else ("emptied_pair", 2)
                 emptied[unit] = work.tile([P, 4 * P * rows], BF16, name=tag, bufs=bufs)
             return emptied[unit][:]
 
@@ -313,23 +314,24 @@ def tile_mae_pa_kernel(tc, x_bytes, x_scale, eps, W11, b11, W31, b31, W32, b32, 
         def by_plane(unit):
             return emptied_tile(unit).rearrange("p (u n e) -> p u n e", u=2, e=2)
 
-        def scalar_empty(unit, t, sums_of_t, planes):
+        def scalar_empty(unit, t):
             nc.scalar.activation(
-                out=by_plane(unit)[:, t // 2, :, t % 2] if planes else by_slot(unit)[:, t, :],
-                in_=sums_of_t, func=RELU, bias=bias1[:, unit[0], t : t + 1],
+                out=by_slot(unit)[:, t, :], in_=banks[unit, t], func=RELU, bias=bias1[:, unit[0], t : t + 1]
             )
 
-        def scalar_bank(unit, t, planes=False):
+        def scalar_bank(unit, t):
             bank = psum.tile([P, HALF], F32, name="bank")
+            banks[unit, t] = bank[:]
             passes(bank[:], unit[0], t, unit[1], 4)
-            scalar_empty(unit, t, bank[:], planes)
+            scalar_empty(unit, t)
 
-        def scalar_pair_bank(unit, e, planes=False):
+        def scalar_pair_bank(unit, e):
             bank = psum.tile([P, 2, PAIR], F32, name="bank")
             for u in range(2):
+                banks[unit, 2 * u + e] = bank[:, u, :]
                 passes(bank[:, u, :], unit[0], 2 * u + e, unit[1], 2)
             for u in range(2):
-                scalar_empty(unit, 2 * u + e, bank[:, u, :], planes)
+                scalar_empty(unit, 2 * u + e)
 
         def vector_banks(unit, numbers):
             for i in numbers:
@@ -339,7 +341,7 @@ def tile_mae_pa_kernel(tc, x_bytes, x_scale, eps, W11, b11, W31, b31, W32, b32, 
                     for i in reversed(numbers):
                         one_pass(banks[unit, i][:, e, :], unit[0], c, 2 * (i % 2) + e, unit[1] + 2 * (i // 2), 2)
 
-        bias_runs = keep.tile([P, 2 * (GROUPS - 1), BIAS_RUN, 2], BF16, name="bias_runs")
+        bias_runs = keep.tile([P, 2 * GROUPS, BIAS_RUN, 2], BF16, name="bias_runs")
 
         def lay_bias(g0, g1):
             nc.vector.tensor_copy(
@@ -384,12 +386,6 @@ def tile_mae_pa_kernel(tc, x_bytes, x_scale, eps, W11, b11, W31, b31, W32, b32, 
                 out=laid_tokens(unit, a, b).rearrange("p (n t) -> p n t", t=4),
                 in0=by_slot(unit)[:, :, a:b].rearrange("p t n -> p n t"),
                 scalar1=1.0, scalar2=0.0, op0=MULT, op1=ADD,
-            )
-
-        def join(engine_copy, unit, a, b):
-            engine_copy(
-                out=laid_tokens(unit, a, b).rearrange("p (n u e) -> p n u e", u=2, e=2),
-                in_=by_plane(unit)[:, :, a:b, :].rearrange("p u n e -> p n u e"),
             )
 
         def join_relu(unit):
@@ -522,9 +518,8 @@ def tile_mae_pa_kernel(tc, x_bytes, x_scale, eps, W11, b11, W31, b31, W32, b32, 
             if j > 0:
                 w_buffer(f"laid{2 + j % 2}", [(j + 2, 1)] if last else [(j + 2, 1), (j + 3, 0)])
             if last:
-                w_scalar(j + 2, 1, 0, SCALAR_CHANNELS)
-                for m in range(2 * PERIODS, 2 * GROUPS):
-                    w3_scalar(m)
+                w_scalar(j + 2, 1, 0, PASS)
+                w3_scalar(PERIODS + j)
             else:
                 w_scalar(j + 3, 0, BANK_CHANNELS if j == 0 else 0, PASS)
                 w_scalar(j + 2, 1, 0, SCALAR_CHANNELS)
@@ -532,19 +527,21 @@ def tile_mae_pa_kernel(tc, x_bytes, x_scale, eps, W11, b11, W31, b31, W32, b32, 
             lay_gpsimd(before, 0, GPSIMD_TOKENS)
             for i in (0, 2, 1, 3):
                 vector_add(v_unit, i)
-            w3_matmuls(PERIODS + j, 1)
-            w3_empty(PERIODS + j, 1)
+            if not last:
+                w3_matmuls(PERIODS + j, 1)
+                w3_empty(PERIODS + j, 1)
             for t in range(4):
                 scalar_bank(s_unit, t)
             if 0 < j and not last:
                 second_stage(j - 1, 4, 4)
-            w_vector(j + 2, 1, SCALAR_CHANNELS, PASS)
-            join_relu(v_unit)
-            if j == 2:
-                lay_bias(4, GROUPS - 1)
-            lay(nc.vector.tensor_copy, before, GPSIMD_TOKENS, HALF)
             if last:
                 w_quant(j + 2, 1)
+            else:
+                w_vector(j + 2, 1, SCALAR_CHANNELS, PASS)
+            join_relu(v_unit)
+            if j == 2:
+                lay_bias(4, GROUPS)
+            lay(nc.vector.tensor_copy, before, GPSIMD_TOKENS, HALF)
             w3_quant(j)
             enc_quant(j, 0, ROWS)
             if not last:
@@ -554,81 +551,72 @@ def tile_mae_pa_kernel(tc, x_bytes, x_scale, eps, W11, b11, W31, b31, W32, b32, 
                 w_quant(j + 2, 1, 2)
 
         g4, g5, g6, g7 = range(GROUPS - 4, GROUPS)
-        s6, s7 = (g6, 0, 4), (g7, 0, 4)
-        v6 = [(g6, 4, 2), (g6, 6, 2)]
+        s6, v7, s6b = (g6, 0, 4), (g7, 0, 4), (g6, 4, 4)
         s7b = [(g7, 4, 2), (g7, 6, 2)]
         late["biased"] = keep.tile([P, ROWS, 2 * LATENT], F32, name="laid0", align_bytes=64)
         late["mu_sigma"] = keep.tile([P, 2, ROWS, LATENT], F32, name="w11_raw0_5")
         late["z"] = keep.tile([P, ROWS, LATENT], F32, name="w11_raw0_0")
+        w3_scalar(2 * g6)
+        w3_scalar(2 * g6 + 1)
+        for i in (0, 2, 1):
+            vector_banks(v7, [i])
+        scalar_bank(s6b, 0)
+        w3_scalar(2 * g7)
+        w3_scalar(2 * g7 + 1)
+        second_stage(g4, 4, 4)
+        enc_buffer("laid1", [s6, v7])
+        lay_gpsimd(s6, 0, GPSIMD_LATE_TOKENS)
+        vector_add(v7, 0)
+        vector_banks(v7, [3])
+        for i in (2, 1, 3):
+            vector_add(v7, i)
+        for t in (1, 2, 3):
+            scalar_bank(s6b, t)
+        lay(nc.vector.tensor_copy, s6, GPSIMD_LATE_TOKENS, HALF)
         w3_quant(g6)
-        vector_banks(v6[0], [0])
-        scalar_bank(s7, 0, planes=True)
-        vector_banks(v6[0], [1])
-        scalar_bank(s7, 2, planes=True)
-        second_stage(g5, 0, 4)
-        enc_buffer("laid1", [(g6, 0, 2)])
-        lay_gpsimd(s6, 0, GPSIMD_TAIL_TOKENS)
-        vector_add(v6[0], 0)
-        vector_add(v6[0], 1)
-        scalar_bank(s7, 1, planes=True)
-        vector_banks(v6[1], [0])
-        scalar_bank(s7, 3, planes=True)
-        vector_banks(v6[1], [1])
-        enc_buffer("laid2", [v6[0]])
-        lay(nc.vector.tensor_copy, s6, GPSIMD_TAIL_TOKENS, PAIR)
-        join_relu(v6[0])
+        join_relu(v7)
         w3_quant(g7)
+        enc_quant(g6, 0, ROWS)
+        for unit in s7b:
+            scalar_pair_bank(unit, 0)
+            scalar_pair_bank(unit, 1)
+        second_stage(g5, 0, 4)
+        for row0 in (0, 2):
+            second_stage(g6, row0, 2)
+            second_stage(g7, row0, 2)
+        second_stage(g5, 4, 4)
+        enc_buffer("laid2", [(g6, 4, 2)])
+        enc_buffer("laid3", [(g6, 6, 2)])
+        lay(nc.vector.tensor_copy, s6b, 0, PAIR)
+        lay(nc.vector.tensor_copy, s6b, PAIR, HALF)
         enc_quant(g6, 4, 2)
-        enc_quant(g6, 0, 2)
-        enc_buffer("laid2", [(g6, 2, 2)])
-        lay_gpsimd(s6, PAIR, PAIR + GPSIMD_TAIL_TOKENS)
-        vector_add(v6[1], 0)
-        vector_add(v6[1], 1)
-        scalar_pair_bank(s7b[0], 0, planes=True)
-        second_stage(g6, 0, 2)
-        scalar_pair_bank(s7b[0], 1, planes=True)
-        enc_buffer("laid1", [s7])
-        enc_buffer("laid3", [v6[1]])
-        lay(nc.vector.tensor_copy, s6, PAIR + GPSIMD_TAIL_TOKENS, HALF)
-        join(nc.vector.tensor_copy, s7, 0, PAIR)
-        enc_quant(g6, 2, 2)
-        enc_quant(g7, 0, 2)
-        join(nc.vector.tensor_copy, s7, PAIR, HALF)
-        join_relu(v6[1])
-        enc_quant(g7, 2, 2)
-        scalar_pair_bank(s7b[1], 0)
-        scalar_pair_bank(s7b[1], 1)
-        second_stage(g7, 0, 2)
-        second_stage(g6, 2, 2)
-        second_stage(g7, 2, 2)
-        enc_buffer("laid2", [s7b[0]])
-        join(nc.vector.tensor_copy, s7b[0], 0, PAIR)
         enc_quant(g6, 6, 2)
-        enc_quant(g7, 4, 2)
-        for row0 in (4, 6):
-            for g in range(g4, GROUPS if row0 == 4 else g7):
-                second_stage(g, row0, 2)
-        enc_buffer("laid3", [s7b[1]])
-        lay_gpsimd(s7b[1], P, PAIR)
-        lay(nc.scalar.copy, s7b[1], 0, P)
-        for a in (0, 2, 4):
+        second_stage(g6, 4, 4)
+        enc_buffer("laid2", [s7b[1]])
+        lay_gpsimd(s7b[1], 0, GPSIMD_TAIL_TOKENS)
+        enc_buffer("laid1", [s7b[0]])
+        lay(nc.scalar.copy, s7b[0], 0, PAIR)
+        for a in (0, 2):
             add_bias(a, a + 2)
             relus(a, a + 2)
             store_mu_sigma(a, a + 2)
-        enc_quant(g7, 6, 1)
-        enc_quant(g7, 7, 1)
-        second_stage(g7, 6, 2)
+        enc_quant(g7, 4, 2)
+        second_stage(g7, 4, 2)
+        lay(nc.vector.tensor_copy, s7b[1], GPSIMD_TAIL_TOKENS, PAIR)
         z_noise(0, 4)
-        z_noise(4, 6)
-        add_bias(6, 7)
+        enc_quant(g7, 6, 2)
+        second_stage(g7, 6, 2)
+        add_bias(4, 6)
+        relus(4, 6)
         z_add_mu(0, 4)
         store_z(0, 4)
-        add_bias(7, 8)
-        relus(6, 7)
-        relus(7, 8)
+        store_mu_sigma(4, 6)
+        add_bias(6, 8)
+        relus(6, 8)
         store_mu_sigma(6, 8, nc.scalar)
+        z_noise(4, 6)
+        z_noise(6, 8)
         z_add_mu(4, 6)
         store_z(4, 6)
-        z_noise(6, 8)
         z_add_mu(6, 8)
         store_z(6, 8)

@@ -35,6 +35,7 @@ SCALAR_CHANNELS = 304
 BIAS_RUN = 16
 MATMUL_ROWS = range(0, ROWS, 2)
 GPSIMD_LATE_TOKENS = 400
+TURNED = (2,)
 
 
 def tile_mae_pa_kernel(tc, x_bytes, x_scale, eps, W11, b11, W31, b31, W32, b32, out_0, out_1, out_2):
@@ -113,6 +114,10 @@ def tile_mae_pa_kernel(tc, x_bytes, x_scale, eps, W11, b11, W31, b31, W32, b32, 
         bias3 = keep.tile([P, 2 * LATENT], BF16, name="bias3")
         nc.sync.dma_start(out=bias3[:, :LATENT], in_=b31.partition_broadcast(P))
         nc.sync.dma_start(out=bias3[:, LATENT:], in_=b32.partition_broadcast(P))
+        bias3_cols = []
+        for w, b in enumerate((b31, b32)):
+            bias3_cols.append(keep.tile([P, 1], BF16, name=f"bias3_col{w}"))
+            nc.sync.dma_start(out=bias3_cols[w][:], in_=b.rearrange("(p o) -> p o", o=1))
         eps_sb = keep.tile([P, ROWS, LATENT], BF16, name="eps_sb")
         nc.sync.dma_start(out=eps_sb[:], in_=eps.rearrange("(p r) l -> p r l", r=ROWS))
 
@@ -404,23 +409,52 @@ def tile_mae_pa_kernel(tc, x_bytes, x_scale, eps, W11, b11, W31, b31, W32, b32, 
         acc = {}
 
         def second_stage(g, row0, rows):
-            w_cols = slice(2 * LATENT * g, 2 * LATENT * (g + 1))
             for r in range(row0, row0 + rows):
-                if r // 2 not in acc:
-                    acc[r // 2] = sums.tile([P, 2, 2 * LATENT], F32, name=f"sum{r // 2}")
-                codes, scales, n0 = enc_quantised[g, r]
+                pair, place = divmod(r, 2)
+                if pair not in acc:
+                    acc[pair] = sums.tile([P, 2, 2 * LATENT], F32, name=f"sum{pair}")
+                if pair in TURNED:
+                    codes, scales, n0 = enc_quantised[g, 2 * pair]
+                    w_cols = slice(LATENT * (2 * g + place), LATENT * (2 * g + place + 1))
+                    still, moving = (w3_codes[:, w_cols], w3_scales[:, w_cols]), (codes[:, n0 : n0 + PAIR], scales[:, n0 : n0 + PAIR])
+                else:
+                    codes, scales, n0 = enc_quantised[g, r]
+                    w_cols = slice(2 * LATENT * g, 2 * LATENT * (g + 1))
+                    still, moving = (codes[:, n0 : n0 + P], scales[:, n0 : n0 + P]), (w3_codes[:, w_cols], w3_scales[:, w_cols])
                 nc.tensor.matmul_mx(
-                    out=acc[r // 2][:, r % 2, :],
-                    lhsT=codes[:, n0 : n0 + P].bitcast(FP8X4),
-                    lhsT_scale=scales[:, n0 : n0 + P],
-                    rhs=w3_codes[:, w_cols].bitcast(FP8X4),
-                    rhs_scale=w3_scales[:, w_cols],
-                    start=(g == 0 and r % 2 == 0),
-                    stop=(g == GROUPS - 1 and r % 2 == 1),
+                    out=acc[pair][:, place, :],
+                    lhsT=still[0].bitcast(FP8X4),
+                    lhsT_scale=still[1],
+                    rhs=moving[0].bitcast(FP8X4),
+                    rhs_scale=moving[1],
+                    start=(g == 0 and place == 0),
+                    stop=(g == GROUPS - 1 and place == 1),
                 )
 
         out_views = [o.rearrange("(p r) l -> p r l", r=ROWS) for o in (out_0, out_1, out_2)]
         late = {}
+
+        def latent_relu(w, pair):
+            nc.scalar.activation(
+                out=late["latent"][:, pair, w, :], in_=acc[pair][:, w, :], func=RELU, bias=bias3_cols[w][:]
+            )
+
+        def turn_back(w, pair):
+            banks["back", w, pair] = bank = psum.tile([P, 2, LATENT], F32, name="bank")
+            for r in range(2):
+                nc.tensor.transpose(bank[:, r, :], late["latent"][:, pair, w, P * r : P * (r + 1)], ident[:])
+
+        def copy_back(w, pair):
+            a, b = 2 * pair, 2 * pair + 2
+            nc.scalar.copy(out=late["mu_sigma"][:, w, a:b, :], in_=banks["back", w, pair][:])
+            nc.sync.dma_start(out=out_views[w][:, a:b, :], in_=late["mu_sigma"][:, w, a:b, :])
+
+        def z_step(w, pair):
+            a, b = 2 * pair, 2 * pair + 2
+            nc.vector.tensor_tensor(
+                out=late["z"][:, a:b, :], in0=eps_sb[:, a:b, :] if w else late["z"][:, a:b, :],
+                in1=banks["back", w, pair][:], op=MULT if w else ADD,
+            )
 
         def add_bias(a, b):
             nc.vector.tensor_tensor(
@@ -556,6 +590,7 @@ def tile_mae_pa_kernel(tc, x_bytes, x_scale, eps, W11, b11, W31, b31, W32, b32, 
         late["biased"] = keep.tile([P, ROWS, 2 * LATENT], F32, name="laid0", align_bytes=64)
         late["mu_sigma"] = keep.tile([P, 2, ROWS, LATENT], F32, name="w11_raw0_5")
         late["z"] = keep.tile([P, ROWS, LATENT], F32, name="w11_raw0_0")
+        late["latent"] = keep.tile([P, 4, 2, PAIR], F32, name="w11_raw1_4")
         w3_scalar(2 * g6)
         w3_scalar(2 * g6 + 1)
         for i in (0, 2, 1):
@@ -596,27 +631,33 @@ def tile_mae_pa_kernel(tc, x_bytes, x_scale, eps, W11, b11, W31, b31, W32, b32, 
         lay_gpsimd(s7b[1], 0, GPSIMD_TAIL_TOKENS)
         enc_buffer("laid1", [s7b[0]])
         lay(nc.scalar.copy, s7b[0], 0, PAIR)
+        lay(nc.scalar.copy, s7b[1], GPSIMD_TAIL_TOKENS, PAIR)
         for a in (0, 2):
             add_bias(a, a + 2)
             relus(a, a + 2)
             store_mu_sigma(a, a + 2)
         enc_quant(g7, 4, 2)
         second_stage(g7, 4, 2)
-        lay(nc.vector.tensor_copy, s7b[1], GPSIMD_TAIL_TOKENS, PAIR)
-        z_noise(0, 4)
+        latent_relu(1, 2)
+        latent_relu(0, 2)
         enc_quant(g7, 6, 2)
         second_stage(g7, 6, 2)
-        add_bias(4, 6)
-        relus(4, 6)
-        z_add_mu(0, 4)
-        store_z(0, 4)
-        store_mu_sigma(4, 6)
+        turn_back(1, 2)
+        turn_back(0, 2)
+        z_noise(0, 2)
+        z_noise(2, 4)
+        z_add_mu(0, 2)
+        store_z(0, 2)
+        z_add_mu(2, 4)
+        store_z(2, 4)
         add_bias(6, 8)
+        copy_back(1, 2)
+        copy_back(0, 2)
         relus(6, 8)
         store_mu_sigma(6, 8, nc.scalar)
-        z_noise(4, 6)
         z_noise(6, 8)
-        z_add_mu(4, 6)
-        store_z(4, 6)
+        z_step(1, 2)
         z_add_mu(6, 8)
         store_z(6, 8)
+        z_step(0, 2)
+        store_z(4, 6)

@@ -203,9 +203,9 @@ def tile_mae_pa_kernel(tc, x_bytes, x_scale, eps, W11, b11, W31, b31, W32, b32, 
             banks[g, c, a] = bank = psum.tile([P, 2 * BANK_CHANNELS], F32, name="bank")
             for n0 in range(0, width, P):
                 nc.tensor.matmul(
-                    out=bank[:, 2 * n0 : 2 * (n0 + P)].bitcast(BF16),
+                    out=bank[:, 2 * n0 : 2 * (n0 + P)].bitcast(BF16).rearrange("p (n j) -> p j n", j=4),
                     lhsT=ident_bf[:],
-                    rhs=w11_raw[g, c][:, :, a + n0 : a + n0 + P].rearrange("p j n -> p n j"),
+                    rhs=w11_raw[g, c][:, :, a + n0 : a + n0 + P],
                     start=True,
                     stop=True,
                 )
@@ -271,9 +271,9 @@ def tile_mae_pa_kernel(tc, x_bytes, x_scale, eps, W11, b11, W31, b31, W32, b32, 
             banks[m] = bank = psum.tile([P, 4 * LATENT], F32, name="bank")
             for i in range(count):
                 nc.tensor.matmul(
-                    out=bank[:, 2 * LATENT * i : 2 * LATENT * (i + 1)].bitcast(BF16),
+                    out=bank[:, 2 * LATENT * i : 2 * LATENT * (i + 1)].bitcast(BF16).rearrange("p (l j) -> p j l", j=4),
                     lhsT=ident_bf[:],
-                    rhs=w3_raw[divmod(m + i, 2)].rearrange("p (j l) -> p l j", j=4),
+                    rhs=w3_raw[divmod(m + i, 2)].rearrange("p (j l) -> p j l", j=4),
                     start=True,
                     stop=True,
                 )

@@ -29,12 +29,12 @@ PAIR = 2 * P
 BANK_CHANNELS = 256
 PERIODS = GROUPS - 2
 
-GPSIMD_TOKENS = 448
-GPSIMD_TAIL_TOKENS = 192
-SCALAR_CHANNELS = 304
+GPSIMD_TOKENS = 480
+GPSIMD_TAIL_TOKENS = 208
+SCALAR_CHANNELS = 296
 BIAS_RUN = 16
 MATMUL_ROWS = range(0, ROWS, 2)
-GPSIMD_LATE_TOKENS = 400
+GPSIMD_LATE_TOKENS = 424
 TURNED = (2,)
 
 
@@ -388,8 +388,8 @@ def tile_mae_pa_kernel(tc, x_bytes, x_scale, eps, W11, b11, W31, b31, W32, b32, 
 
         def lay_gpsimd(unit, a, b):
             nc.gpsimd.tensor_scalar(
-                out=laid_tokens(unit, a, b).rearrange("p (n t) -> p n t", t=4),
-                in0=by_slot(unit)[:, :, a:b].rearrange("p t n -> p n t"),
+                out=laid_tokens(unit, a, b).rearrange("p (m i t) -> p m t i", i=2, t=4),
+                in0=by_slot(unit)[:, :, a:b].rearrange("p t (m i) -> p m t i", i=2),
                 scalar1=1.0, scalar2=0.0, op0=MULT, op1=ADD,
             )
 

from contextlib import ExitStack

import concourse.mybir as mybir
from concourse.masks import make_identity

TOKENS, IMAGE, HIDDEN, LATENT = 1024, 1024, 4096, 128

F32 = mybir.dt.float32
BF16 = mybir.dt.bfloat16
U32 = mybir.dt.uint32
U8 = mybir.dt.uint8
FP8 = mybir.dt.float8_e4m3fn
FP8X4 = mybir.dt.float8_e4m3fn_x4

ADD = mybir.AluOpType.add
MULT = mybir.AluOpType.mult
MAX = mybir.AluOpType.max
RELU = mybir.ActivationFunctionType.Relu
COPY = mybir.ActivationFunctionType.Copy

FLOPS = 2 * TOKENS * IMAGE * HIDDEN + 2 * TOKENS * HIDDEN * 2 * LATENT

P = 128
PASS = 4 * P
GROUPS = HIDDEN // PASS
ROWS = TOKENS // P
HALF = TOKENS // 2
PAIR = 2 * P
BANK_CHANNELS = 256
PERIODS = GROUPS - 2

GPSIMD_TOKENS = 480
GPSIMD_TAIL_TOKENS = 208
SCALAR_CHANNELS = 296
BIAS_RUN = 16
MATMUL_ROWS = range(0, ROWS, 2)
GPSIMD_LATE_TOKENS = 424
TURNED = (2,)


def tile_mae_pa_kernel(tc, x_bytes, x_scale, eps, W11, b11, W31, b31, W32, b32, out_0, out_1, out_2):
    nc = tc.nc
    with ExitStack() as ctx:
        keep = ctx.enter_context(tc.tile_pool(name="keep", bufs=1))
        work = ctx.enter_context(tc.tile_pool(name="work", bufs=2))
        psum = ctx.enter_context(tc.psum_pool(name="psum", bufs=4))
        sums = ctx.enter_context(tc.psum_pool(name="sums", bufs=1))

        ident = keep.tile([P, P], F32, name="ident")
        make_identity(nc, ident[:])
        ctx.enter_context(tc.manual_schedule())
        ctx.enter_context(nc.allow_non_contiguous_dma(reason="runs of four scales and of four biases"))

        zeros = keep.tile([P, 256], F32, name="zeros")
        nc.vector.memset(zeros[:], 0.0)
        wide_ident = keep.tile([P, 2, 2 * P], BF16, name="wide_ident")
        nc.vector.memset(wide_ident[:], 0.0)
        for e in range(2):
            nc.vector.tensor_copy(out=wide_ident[:, e, e : 2 * P : 2], in_=ident[:])

        x_view = x_bytes.rearrange("(p r) k -> p (r k)", r=ROWS)
        w11_view = W11.rearrange("(c p j) n -> c p j n", c=2, j=4)
        w3_views = [w.rearrange("(g p j) l -> p g (j l)", p=P, j=4) for w in (W31, W32)]
        b11_view = b11.rearrange("(g p t) -> p g t", p=P, t=4)
        x_raw, w11_raw, w3_raw = {}, {}, {}

        def load_x(r0, r1):
            tile = keep.tile([P, (r1 - r0) * IMAGE], U8, name=f"x_raw{r0}")
            nc.sync.dma_start(out=tile[:], in_=x_view[:, r0 * IMAGE : r1 * IMAGE])
            for r in range(r0, r1):
                x_raw[r] = tile[:, (r - r0) * IMAGE : (r - r0 + 1) * IMAGE]

        def load_w11(c, g0, g1):
            tile = keep.tile([P, 4, (g1 - g0) * PASS], BF16, name=f"w11_raw{c}_{g0}")
            nc.sync.dma_start(out=tile[:], in_=w11_view[c, :, :, g0 * PASS : g1 * PASS])
            for g in range(g0, g1):
                w11_raw[g, c] = tile[:, :, (g - g0) * PASS : (g - g0 + 1) * PASS]

        def load_w3(g0, g1):
            for w in range(2):
                tile = keep.tile([P, g1 - g0, 4 * LATENT], BF16, name=f"w3_raw{w}_{g0}")
                nc.sync.dma_start(out=tile[:], in_=w3_views[w][:, g0:g1, :])
                for g in range(g0, g1):
                    w3_raw[g, w] = tile[:, g - g0, :]

        scale_cols = keep.tile([P, 2, 4], F32, name="scale_cols")
        scale = keep.tile([P, 2, P, 4], F32, name="scale")
        bias1 = keep.tile([P, GROUPS, 4], BF16, name="bias1")
        load_x(0, 1)
        nc.sync.dma_start(out=scale_cols[:], in_=x_scale.rearrange("o (c p t) -> p (o c) t", p=P, t=4))
        load_x(1, 2)
        load_x(2, 4)
        load_w11(0, 0, 1)
        load_x(4, 6)
        load_w11(1, 0, 1)
        load_x(6, ROWS)
        load_w11(0, 1, 2)
        load_w11(1, 1, 2)
        nc.sync.dma_start(out=bias1[:, :4, :], in_=b11_view[:, :4, :])
        load_w3(0, 1)
        load_w11(0, 2, 3)
        load_w3(1, 3)
        load_w11(0, 3, 4)
        load_w11(1, 2, 3)
        load_w3(3, 5)
        load_w11(0, 4, 5)
        load_w11(1, 3, 4)
        nc.sync.dma_start(out=bias1[:, 4:, :], in_=b11_view[:, 4:, :])
        load_w11(0, 5, 7)
        load_w11(1, 4, 6)
        load_w3(5, GROUPS)
        load_w11(0, 7, GROUPS)
        load_w11(1, 6, GROUPS)
        bias3 = keep.tile([P, 2 * LATENT], BF16, name="bias3")
        nc.sync.dma_start(out=bias3[:, :LATENT], in_=b31.partition_broadcast(P))
        nc.sync.dma_start(out=bias3[:, LATENT:], in_=b32.partition_broadcast(P))
        bias3_cols = []
        for w, b in enumerate((b31, b32)):
            bias3_cols.append(keep.tile([P, 1], BF16, name=f"bias3_col{w}"))
            nc.sync.dma_start(out=bias3_cols[w][:], in_=b.rearrange("(p o) -> p o", o=1))
        eps_sb = keep.tile([P, ROWS, LATENT], BF16, name="eps_sb")
        nc.sync.dma_start(out=eps_sb[:], in_=eps.rearrange("(p r) l -> p r l", r=ROWS))

        ident_bf = keep.tile([P, P], BF16, name="ident_bf")
        nc.scalar.activation(out=ident_bf[:], in_=ident[:], func=COPY)

        def warm_up(bank, columns):
            nc.tensor.matmul(out=bank[:, :columns], lhsT=zeros[:, :P], rhs=zeros[:, :columns], start=True, stop=True)

        def quantize(codes, scales, laid):
            nc.vector.quantize_mx(out=codes.bitcast(FP8X4), scales=scales, in_=laid)

        def laid_buffer(name):
            return keep.tile([P, 2, 4 * HALF], BF16, name=name, align_bytes=64)

        def codes_tiles(name, columns, bufs):
            codes = work.tile([P, columns], U32, name=f"{name}_codes", bufs=bufs, align_bytes=64)
            scales = work.tile([P, columns], U8, name=f"{name}_scales", bufs=bufs, align_bytes=64)
            return codes, scales

        x_quantised = [codes_tiles("x", 2 * HALF, 2) for h in range(2)]
        x_wide, x_turned, x_laid = {}, {}, {}

        def x_widen(r, c0=0, c1=2):
            if r not in x_wide:
                x_wide[r] = work.tile([P, IMAGE], BF16, name="enc_codes", bufs=4, align_bytes=64)
            nc.scalar.copy(
                out=x_wide[r][:, PASS * c0 : PASS * c1], in_=x_raw[r][:, PASS * c0 : PASS * c1].bitcast(FP8)
            )

        def x_turn(r, c0=0, c1=2):
            pool, tag = (psum, "bank") if c1 - c0 == 1 else (sums, f"sum{r % 4}")
            if r in MATMUL_ROWS:
                turned = pool.tile([P, 2, c1 - c0, 2 * P], BF16, name=tag)
                for c in range(c0, c1):
                    for t in range(4):
                        nc.tensor.matmul(
                            out=turned[:, t // 2, c - c0, :],
                            lhsT=x_wide[r][:, PASS * c + t : PASS * (c + 1) : 4],
                            rhs=wide_ident[:, t % 2, :],
                            start=(t % 2 == 0),
                            stop=(t % 2 == 1),
                        )
                x_turned[r, c0] = turned[:]
            else:
                bank = pool.tile([P, 2, c1 - c0, P], F32, name=tag)
                words = x_wide[r][:].bitcast(F32)
                for c in range(c0, c1):
                    for u in range(2):
                        nc.tensor.transpose(
                            bank[:, u, c - c0, :], words[:, 2 * P * c + u : 2 * P * (c + 1) : 2], ident[:]
                        )
                x_turned[r, c0] = bank[:].bitcast(BF16)

        def x_product(r, c0=0, c1=2):
            h, row = divmod(r, 4)
            if h not in x_laid:
                x_laid[h] = laid_buffer(f"laid{h}")
            nc.vector.tensor_tensor(
                out=x_laid[h][:, c0:c1, PASS * row : PASS * (row + 1)].rearrange("p c (n u e) -> p c n u e", u=2, e=2),
                in0=scale[:, c0:c1, :, :].rearrange("p c n (u e) -> p c n u e", u=2),
                in1=x_turned[r, c0].rearrange("p u c (n e) -> p c n u e", e=2),
                op=MULT,
            )

        def x_quant(h):
            quantize(x_quantised[h][0][:], x_quantised[h][1][:], x_laid[h][:].rearrange("p c n -> p (c n)"))

        w_laid, w_quantised, banks = {}, {}, {}

        def w_buffer(name, passes):
            laid = laid_buffer(name)
            codes, scales = codes_tiles("w", 2 * PASS, 4)
            for i, key in enumerate(passes):
                w_laid[key] = (laid, i)
                w_quantised[key] = (codes, scales, i)

        def w_target(g, c):
            laid, i = w_laid[g, c]
            return laid[:, i, :]

        def w_matmuls(g, c, a, width):
            banks[g, c, a] = bank = psum.tile([P, 2 * BANK_CHANNELS], F32, name="bank")
            for n0 in range(0, width, P):
                nc.tensor.matmul(
                    out=bank[:, 2 * n0 : 2 * (n0 + P)].bitcast(BF16).rearrange("p (n j) -> p j n", j=4),
                    lhsT=ident_bf[:],
                    rhs=w11_raw[g, c][:, :, a + n0 : a + n0 + P],
                    start=True,
                    stop=True,
                )

        def w_empty(g, c, a, width):
            nc.scalar.copy(
                out=w_target(g, c).bitcast(F32).rearrange("p (t m u) -> p t m u", t=4, u=2)[
                    :, :, a // 4 : (a + width) // 4, :
                ],
                in_=banks[g, c, a][:, : 2 * width].rearrange("p (m t u) -> p t m u", t=4, u=2),
            )

        def w_copy(engine_copy, g, c, a, b):
            target = w_target(g, c).rearrange("p (t m i j) -> p m t j i", t=4, i=2, j=4)
            engine_copy(
                out=target[:, a // 8 : b // 8, :, :, :],
                in_=w11_raw[g, c][:, :, a:b].rearrange("p j (m i t) -> p m t j i", t=4, i=2),
            )

        def w_vector(g, c, a, b):
            w_copy(nc.vector.tensor_copy, g, c, a, b)

        def w_scalar(g, c, a, b):
            w_copy(nc.scalar.copy, g, c, a, b)

        def w_gpsimd(g, c, a, b):
            target = w_target(g, c).rearrange("p (t m j) -> p m t j", t=4, j=4)
            nc.gpsimd.tensor_scalar(
                out=target[:, a // 4 : b // 4, :, :],
                in0=w11_raw[g, c][:, :, a:b].rearrange("p j (m t) -> p m t j", t=4),
                scalar1=1.0, scalar2=0.0, op0=MULT, op1=ADD,
            )

        def w_quant(g, c, passes=1):
            laid, i = w_laid[g, c]
            codes, scales = w_quantised[g, c][:2]
            cols = slice(PASS * i, PASS * (i + passes))
            quantize(codes[:, cols], scales[:, cols], laid[:, i : i + passes, :].rearrange("p c n -> p (c n)"))

        w3_laid = {}
        w3_codes, w3_scales = codes_tiles("w3", GROUPS * 2 * LATENT, 1)

        def w3_target(m, count=1):
            g, w = divmod(m, 2)
            if g not in w3_laid:
                w3_laid[g] = work.tile([P, 8 * LATENT], BF16, name="w3_laid", bufs=4, align_bytes=64)
            return w3_laid[g][:, 4 * LATENT * w : 4 * LATENT * (w + count)]

        def w3_scalar(m):
            nc.scalar.copy(
                out=w3_target(m).rearrange("p (l i j) -> p l j i", i=2, j=4),
                in_=w3_raw[divmod(m, 2)].rearrange("p (j l i) -> p l j i", j=4, i=2),
            )

        def w3_gpsimd(m):
            nc.gpsimd.tensor_scalar(
                out=w3_target(m).rearrange("p (l j) -> p l j", j=4),
                in0=w3_raw[divmod(m, 2)].rearrange("p (j l) -> p l j", j=4),
                scalar1=1.0, scalar2=0.0, op0=MULT, op1=ADD,
            )

        def w3_matmuls(m, count):
            banks[m] = bank = psum.tile([P, 4 * LATENT], F32, name="bank")
            for i in range(count):
                nc.tensor.matmul(
                    out=bank[:, 2 * LATENT * i : 2 * LATENT * (i + 1)].bitcast(BF16).rearrange("p (l j) -> p j l", j=4),
                    lhsT=ident_bf[:],
                    rhs=w3_raw[divmod(m + i, 2)].rearrange("p (j l) -> p j l", j=4),
                    start=True,
                    stop=True,
                )

        def w3_empty(m, count):
            nc.scalar.copy(out=w3_target(m, count).bitcast(F32), in_=banks[m][:, : 2 * LATENT * count])

        def w3_quant(g):
            cols = slice(2 * LATENT * g, 2 * LATENT * (g + 1))
            quantize(w3_codes[:, cols], w3_scales[:, cols], w3_laid[g][:])

        emptied, enc_laid, enc_quantised = {}, {}, {}

        def one_pass(out, g, c, t, row0, rows):
            h, row = divmod(row0, 4)
            w_codes, w_scales, i = w_quantised[g, c]
            w_cols = slice(PASS * i + P * t, PASS * i + P * (t + 1))
            x_cols = slice(HALF * c + P * row, HALF * c + P * (row + rows))
            nc.tensor.matmul_mx(
                out=out,
                lhsT=w_codes[:, w_cols].bitcast(FP8X4),
                lhsT_scale=w_scales[:, w_cols],
                rhs=x_quantised[h][0][:, x_cols].bitcast(FP8X4),
                rhs_scale=x_quantised[h][1][:, x_cols],
                start=(c == 0),
                stop=(c == 1),
            )

        def passes(out, g, t, row0, rows):
            for c in range(2):
                one_pass(out, g, c, t, row0, rows)

        def emptied_tile(unit):
            if unit not in emptied:
                g, row0, rows = unit
                tag, bufs = ("emptied", 4) if rows == 4 else ("emptied_pair", 2)
                emptied[unit] = work.tile([P, 4 * P * rows], BF16, name=tag, bufs=bufs)
            return emptied[unit][:]

        def by_slot(unit):
            return emptied_tile(unit).rearrange("p (t n) -> p t n", t=4)

        def by_plane(unit):
            return emptied_tile(unit).rearrange("p (u n e) -> p u n e", u=2, e=2)

        def scalar_empty(unit, t):
            nc.scalar.activation(
                out=by_slot(unit)[:, t, :], in_=banks[unit, t], func=RELU, bias=bias1[:, unit[0], t : t + 1]
            )

        def scalar_bank(unit, t):
            bank = psum.tile([P, HALF], F32, name="bank")
            banks[unit, t] = bank[:]
            passes(bank[:], unit[0], t, unit[1], 4)
            scalar_empty(unit, t)

        def scalar_pair_bank(unit, e):
            bank = psum.tile([P, 2, PAIR], F32, name="bank")
            for u in range(2):
                banks[unit, 2 * u + e] = bank[:, u, :]
                passes(bank[:, u, :], unit[0], 2 * u + e, unit[1], 2)
            for u in range(2):
                scalar_empty(unit, 2 * u + e)

        def vector_banks(unit, numbers):
            for i in numbers:
                banks[unit, i] = psum.tile([P, 2, PAIR], F32, name="bank")
            for e in range(2):
                for c in range(2):
                    for i in reversed(numbers):
                        one_pass(banks[unit, i][:, e, :], unit[0], c, 2 * (i % 2) + e, unit[1] + 2 * (i // 2), 2)

        bias_runs = keep.tile([P, 2 * GROUPS, BIAS_RUN, 2], BF16, name="bias_runs")

        def lay_bias(g0, g1):
            nc.vector.tensor_copy(
                out=bias_runs[:, 2 * g0 : 2 * g1, :, :],
                in_=bias1[:, g0:g1, :].rearrange("p g (u e) -> p (g u) e", e=2).unsqueeze(2)
                .to_broadcast([P, 2 * (g1 - g0), BIAS_RUN, 2]),
            )

        def vector_add(unit, i):
            q, u = divmod(i, 2)
            nc.vector.tensor_tensor(
                out=by_plane(unit)[:, u, PAIR * q : PAIR * (q + 1), :].rearrange("p (m n) e -> p m n e", n=BIAS_RUN),
                in0=bias_runs[:, 2 * unit[0] + u, :, :].unsqueeze(1).to_broadcast([P, PAIR // BIAS_RUN, BIAS_RUN, 2]),
                in1=banks[unit, i][:].rearrange("p e (m n) -> p m n e", n=BIAS_RUN),
                op=ADD,
            )

        def enc_buffer(name, units):
            laid = laid_buffer(name)[:].rearrange("p c n -> p (c n)")
            rows = sum(unit[2] for unit in units)
            codes, scales = codes_tiles("enc", P * rows, 4) if rows > 2 else codes_tiles("pair", PAIR, 6)
            n0 = 0
            for g, row0, count in units:
                for r in range(row0, row0 + count):
                    enc_laid[g, r] = (laid, n0)
                    enc_quantised[g, r] = (codes, scales, n0)
                    n0 = n0 + P

        def laid_tokens(unit, a, b):
            laid, n0 = enc_laid[unit[0], unit[1] + a // P]
            n0 = n0 + a % P
            return laid[:, 4 * n0 : 4 * (n0 + b - a)]

        def lay(engine_copy, unit, a, b):
            engine_copy(
                out=laid_tokens(unit, a, b).rearrange("p (m i t) -> p m t i", i=2, t=4),
                in_=by_slot(unit)[:, :, a:b].rearrange("p t (m i) -> p m t i", i=2),
            )

        def lay_gpsimd(unit, a, b):
            nc.gpsimd.tensor_scalar(
                out=laid_tokens(unit, a, b).rearrange("p (m i t) -> p m t i", i=2, t=4),
                in0=by_slot(unit)[:, :, a:b].rearrange("p t (m i) -> p m t i", i=2),
                scalar1=1.0, scalar2=0.0, op0=MULT, op1=ADD,
            )

        def join_relu(unit):
            nc.vector.tensor_scalar(
                out=laid_tokens(unit, 0, P * unit[2]).rearrange("p (n u e) -> p n u e", u=2, e=2),
                in0=by_plane(unit).rearrange("p u n e -> p n u e"),
                scalar1=0.0, scalar2=None, op0=MAX,
            )

        def enc_quant(g, row0, rows):
            laid, n0 = enc_laid[g, row0]
            codes, scales = enc_quantised[g, row0][:2]
            n1 = n0 + P * rows
            quantize(codes[:, n0:n1], scales[:, n0:n1], laid[:, 4 * n0 : 4 * n1])

        acc = {}

        def second_stage(g, row0, rows):
            for r in range(row0, row0 + rows):
                pair, place = divmod(r, 2)
                if pair not in acc:
                    acc[pair] = sums.tile([P, 2, 2 * LATENT], F32, name=f"sum{pair}")
                if pair in TURNED:
                    codes, scales, n0 = enc_quantised[g, 2 * pair]
                    w_cols = slice(LATENT * (2 * g + place), LATENT * (2 * g + place + 1))
                    still, moving = (w3_codes[:, w_cols], w3_scales[:, w_cols]), (codes[:, n0 : n0 + PAIR], scales[:, n0 : n0 + PAIR])
                else:
                    codes, scales, n0 = enc_quantised[g, r]
                    w_cols = slice(2 * LATENT * g, 2 * LATENT * (g + 1))
                    still, moving = (codes[:, n0 : n0 + P], scales[:, n0 : n0 + P]), (w3_codes[:, w_cols], w3_scales[:, w_cols])
                nc.tensor.matmul_mx(
                    out=acc[pair][:, place, :],
                    lhsT=still[0].bitcast(FP8X4),
                    lhsT_scale=still[1],
                    rhs=moving[0].bitcast(FP8X4),
                    rhs_scale=moving[1],
                    start=(g == 0 and place == 0),
                    stop=(g == GROUPS - 1 and place == 1),
                )

        out_views = [o.rearrange("(p r) l -> p r l", r=ROWS) for o in (out_0, out_1, out_2)]
        late = {}

        def latent_relu(w, pair):
            nc.scalar.activation(
                out=late["latent"][:, pair, w, :], in_=acc[pair][:, w, :], func=RELU, bias=bias3_cols[w][:]
            )

        def turn_back(w, pair):
            banks["back", w, pair] = bank = psum.tile([P, 2, LATENT], F32, name="bank")
            for r in range(2):
                nc.tensor.transpose(bank[:, r, :], late["latent"][:, pair, w, P * r : P * (r + 1)], ident[:])

        def copy_back(w, pair):
            a, b = 2 * pair, 2 * pair + 2
            nc.scalar.copy(out=late["mu_sigma"][:, w, a:b, :], in_=banks["back", w, pair][:])
            nc.sync.dma_start(out=out_views[w][:, a:b, :], in_=late["mu_sigma"][:, w, a:b, :])

        def z_step(w, pair):
            a, b = 2 * pair, 2 * pair + 2
            nc.vector.tensor_tensor(
                out=late["z"][:, a:b, :], in0=eps_sb[:, a:b, :] if w else late["z"][:, a:b, :],
                in1=banks["back", w, pair][:], op=MULT if w else ADD,
            )

        def add_bias(a, b):
            nc.vector.tensor_tensor(
                out=late["biased"][:, a:b, :], in0=bias3[:].unsqueeze(1).to_broadcast([P, b - a, 2 * LATENT]),
                in1=acc[a // 2][:, a % 2 : a % 2 + b - a, :], op=ADD,
            )

        def relus(a, b):
            nc.scalar.activation(
                out=late["mu_sigma"][:, :, a:b, :],
                in_=late["biased"][:, a:b, :].rearrange("p r (w l) -> p w r l", w=2), func=RELU,
            )

        def store_mu_sigma(a, b, queue=nc.sync):
            for w in range(2):
                queue.dma_start(out=out_views[w][:, a:b, :], in_=late["mu_sigma"][:, w, a:b, :])

        def z_noise(a, b):
            nc.vector.scalar_tensor_tensor(
                out=late["z"][:, a:b, :], in0=late["biased"][:, a:b, LATENT:], scalar=0.0,
                in1=eps_sb[:, a:b, :], op0=MAX, op1=MULT,
            )

        def z_add_mu(a, b):
            nc.vector.scalar_tensor_tensor(
                out=late["z"][:, a:b, :], in0=late["biased"][:, a:b, :LATENT], scalar=0.0,
                in1=late["z"][:, a:b, :], op0=MAX, op1=ADD,
            )

        def store_z(a, b):
            nc.sync.dma_start(out=out_views[2][:, a:b, :], in_=late["z"][:, a:b, :])

        unused_bank = sums.tile([P, HALF], F32, name="sum0")
        warm_up(unused_bank, 256)
        warm_up(unused_bank, 256)
        nc.vector.tensor_copy(out=scale[:], in_=scale_cols[:].unsqueeze(2).to_broadcast([P, 2, P, 4]))
        for c in range(2):
            x_widen(0, c, c + 1)
            x_turn(0, c, c + 1)
            x_product(0, c, c + 1)
        for r in range(1, 4):
            x_widen(r)
            x_turn(r)
            x_product(r)
        w_buffer("laid2", [(0, 0), (0, 1)])
        w_buffer("laid3", [(1, 0)])
        w_gpsimd(0, 0, 0, PASS)
        w_gpsimd(0, 1, 0, P)
        x_widen(4)
        x_turn(4)
        x_widen(5)
        w_matmuls(0, 1, BANK_CHANNELS, BANK_CHANNELS)
        w_scalar(0, 1, P, BANK_CHANNELS)
        x_turn(5)
        x_widen(6)
        x_widen(7)
        w_empty(0, 1, BANK_CHANNELS, BANK_CHANNELS)
        x_turn(6)
        w_matmuls(1, 0, 0, P)
        w_scalar(1, 0, P, PASS)
        w_empty(1, 0, 0, P)
        w_quant(0, 0)
        x_quant(0)
        w_quant(0, 1)

        w_buffer("laid0", [(1, 1), (2, 0)])
        w_gpsimd(1, 1, 0, PASS)
        w3_gpsimd(0)
        w3_gpsimd(1)
        for t in range(4):
            scalar_bank((0, 0, 4), t)
        x_turn(7)
        for r in (5, 4, 6, 7):
            x_product(r)
        w_matmuls(2, 0, BANK_CHANNELS, BANK_CHANNELS)
        w_scalar(2, 0, 0, BANK_CHANNELS)
        w_empty(2, 0, BANK_CHANNELS, BANK_CHANNELS)
        w3_matmuls(2, 2)
        w3_scalar(5)
        w3_empty(2, 2)
        w3_matmuls(4, 1)
        w_buffer("laid2", [(2, 1), (3, 0)])
        w_scalar(3, 0, 0, BANK_CHANNELS)
        w3_empty(4, 1)
        w_quant(1, 0)
        x_quant(1)
        lay_bias(0, 4)
        w_quant(1, 1, 2)
        for i in (0, 2, 1, 3):
            vector_banks((0, 4, 4), [i])

        for j in range(PERIODS):
            last = j == PERIODS - 1
            v_unit, s_unit, before = (j, 4, 4), (j + 1, 0, 4), (j, 0, 4)
            if j > 0:
                w_buffer(f"laid{2 + j % 2}", [(j + 2, 1)] if last else [(j + 2, 1), (j + 3, 0)])
            if last:
                w_scalar(j + 2, 1, 0, PASS)
                w3_scalar(PERIODS + j)
            else:
                w_scalar(j + 3, 0, BANK_CHANNELS if j == 0 else 0, PASS)
                w_scalar(j + 2, 1, 0, SCALAR_CHANNELS)
            enc_buffer("laid1", [before, v_unit])
            lay_gpsimd(before, 0, GPSIMD_TOKENS)
            for i in (0, 2, 1, 3):
                vector_add(v_unit, i)
            if not last:
                w3_matmuls(PERIODS + j, 1)
                w3_empty(PERIODS + j, 1)
            for t in range(4):
                scalar_bank(s_unit, t)
            if 0 < j and not last:
                second_stage(j - 1, 4, 4)
            if last:
                w_quant(j + 2, 1)
            else:
                w_vector(j + 2, 1, SCALAR_CHANNELS, PASS)
            join_relu(v_unit)
            if j == 2:
                lay_bias(4, GROUPS)
            lay(nc.vector.tensor_copy, before, GPSIMD_TOKENS, HALF)
            w3_quant(j)
            enc_quant(j, 0, ROWS)
            if not last:
                vector_banks((j + 1, 4, 4), [0, 2])
                vector_banks((j + 1, 4, 4), [1, 3])
                second_stage(j, 0, 4)
                w_quant(j + 2, 1, 2)

        g4, g5, g6, g7 = range(GROUPS - 4, GROUPS)
        s6, v7, s6b = (g6, 0, 4), (g7, 0, 4), (g6, 4, 4)
        s7b = [(g7, 4, 2), (g7, 6, 2)]
        late["biased"] = keep.tile([P, ROWS, 2 * LATENT], F32, name="laid0", align_bytes=64)
        late["mu_sigma"] = keep.tile([P, 2, ROWS, LATENT], F32, name="w11_raw0_5")
        late["z"] = keep.tile([P, ROWS, LATENT], F32, name="w11_raw0_0")
        late["latent"] = keep.tile([P, 4, 2, PAIR], F32, name="w11_raw1_4")
        w3_scalar(2 * g6)
        w3_scalar(2 * g6 + 1)
        for i in (0, 2, 1):
            vector_banks(v7, [i])
        scalar_bank(s6b, 0)
        w3_scalar(2 * g7)
        w3_scalar(2 * g7 + 1)
        second_stage(g4, 4, 4)
        enc_buffer("laid1", [s6, v7])
        lay_gpsimd(s6, 0, GPSIMD_LATE_TOKENS)
        vector_add(v7, 0)
        vector_banks(v7, [3])
        for i in (2, 1, 3):
            vector_add(v7, i)
        for t in (1, 2, 3):
            scalar_bank(s6b, t)
        lay(nc.vector.tensor_copy, s6, GPSIMD_LATE_TOKENS, HALF)
        w3_quant(g6)
        join_relu(v7)
        w3_quant(g7)
        enc_quant(g6, 0, ROWS)
        for unit in s7b:
            scalar_pair_bank(unit, 0)
            scalar_pair_bank(unit, 1)
        second_stage(g5, 0, 4)
        for row0 in (0, 2):
            second_stage(g6, row0, 2)
            second_stage(g7, row0, 2)
        second_stage(g5, 4, 4)
        enc_buffer("laid2", [(g6, 4, 2)])
        enc_buffer("laid3", [(g6, 6, 2)])
        lay(nc.vector.tensor_copy, s6b, 0, PAIR)
        lay(nc.vector.tensor_copy, s6b, PAIR, HALF)
        enc_quant(g6, 4, 2)
        enc_quant(g6, 6, 2)
        second_stage(g6, 4, 4)
        enc_buffer("laid2", [s7b[1]])
        lay_gpsimd(s7b[1], 0, GPSIMD_TAIL_TOKENS)
        enc_buffer("laid1", [s7b[0]])
        lay(nc.scalar.copy, s7b[0], 0, PAIR)
        lay(nc.scalar.copy, s7b[1], GPSIMD_TAIL_TOKENS, PAIR)
        for a in (0, 2):
            add_bias(a, a + 2)
            relus(a, a + 2)
            store_mu_sigma(a, a + 2)
        enc_quant(g7, 4, 2)
        second_stage(g7, 4, 2)
        latent_relu(1, 2)
        latent_relu(0, 2)
        enc_quant(g7, 6, 2)
        second_stage(g7, 6, 2)
        turn_back(1, 2)
        turn_back(0, 2)
        z_noise(0, 2)
        z_noise(2, 4)
        z_add_mu(0, 2)
        store_z(0, 2)
        z_add_mu(2, 4)
        store_z(2, 4)
        add_bias(6, 8)
        copy_back(1, 2)
        copy_back(0, 2)
        relus(6, 8)
        store_mu_sigma(6, 8, nc.scalar)
        z_noise(6, 8)
        z_step(1, 2)
        z_add_mu(6, 8)
        store_z(6, 8)
        z_step(0, 2)
        store_z(4, 6)
